import numpy as np
import ml_dtypes


def mxq(x, axis, fmt="e4m3"):
    dtype, down = {"e4m3": (ml_dtypes.float8_e4m3fn, 7), "e5m2": (ml_dtypes.float8_e5m2, 14)}[fmt]
    v = np.moveaxis(np.asarray(x, np.float32).astype(ml_dtypes.bfloat16).astype(np.float64), axis, -1)
    blocks = v.reshape(v.shape[:-1] + (-1, 32))
    amax = np.abs(blocks).max(-1, keepdims=True)
    byte = np.maximum(np.where(amax > 0, np.frexp(amax)[1] - 1 + 127, 0) - down, 1)
    scale = np.exp2(byte - 127.0)
    codes = (blocks / scale).astype(np.float32).astype(dtype).astype(np.float64)
    return np.moveaxis((codes * scale).reshape(v.shape), -1, axis)


WIDE = False


def mx_kscale(k):
    if not WIDE:
        return np.ones(k)
    levels = np.array([10, -10, 5, -5, 0])
    if k % 512:
        return np.exp2(np.random.permutation(np.resize(levels, k // 32))).repeat(32)
    a = np.empty((k // 512, 16))
    for p in range(k // 512):
        a[p, :8] = np.random.permutation(np.resize(levels, 8))
        for g in range(8):
            far = levels[np.abs(levels - a[p, g]) >= 10]
            a[p, g + 8] = far[np.random.randint(len(far))]
    return np.exp2(a.ravel()).repeat(32)


BF16 = ml_dtypes.bfloat16


def bf(x):
    return np.asarray(x, np.float32).astype(BF16)


def f64(x):
    return np.asarray(x).astype(np.float64)


B, N, D, F1, F2, F3, G1, G2 = 4, 32, 512, 512, 1024, 512, 512, 512
ALPHA = 0.2


def lrelu(v):
    return np.maximum(v, ALPHA * v)


def draw0():
    s, t = mx_kscale(D), mx_kscale(F1)
    ss = np.concatenate([s, s])
    return {"x": bf(np.random.standard_normal((B, N, D)) * s),
            "fe_w0": bf(np.random.standard_normal((D + D, F1)) / np.sqrt(D + D) / ss[:, None] * t),
            "fe_b0": bf(np.random.standard_normal(F1) * 0.3 * t),
            "fe_w1": bf(np.random.standard_normal((F1, F2)) * 1.4 / np.sqrt(F1) / t[:, None]),
            "fe_b1": bf(np.random.standard_normal(F2) * 0.3)}


def core(x, fe_w0, fe_b0, fe_w1, fe_b1):
    xq = mxq(f64(x), 2, "e4m3")
    w0 = f64(fe_w0)
    u = xq @ mxq(w0[:D], 0, "e4m3")
    v = xq @ mxq(w0[D:], 0, "e4m3")
    e1 = lrelu(u[:, :, None, :] + v[:, None, :, :] + f64(fe_b0))
    return lrelu((mxq(e1, 3, "e4m3") @ mxq(f64(fe_w1), 0, "e4m3")) + f64(fe_b1))


def e4m3fn_bytes(y):
    return np.clip(np.asarray(y, np.float64), -448.0, 448.0).astype(np.float32).astype(ml_dtypes.float8_e4m3fn).view(np.uint8)


def e4m3fn_values(b):
    return np.asarray(b, np.uint8).view(ml_dtypes.float8_e4m3fn).astype(np.float64)


def setup_inputs():
    d = draw0()
    x0 = np.asarray(d['fe_w1']).astype(np.float64)
    s = (np.max(np.abs(x0), axis=(1,), keepdims=True) / 448.0).astype(np.float32)
    out = {}
    for k, v in d.items():
        if k == 'fe_w1':
            out['fe_w1_bytes'] = e4m3fn_bytes(x0 / s.astype(np.float64))
            out['fe_w1_scale'] = s
        else:
            out[k] = v
    return out


def reference(x, fe_w0, fe_b0, fe_w1_bytes, fe_w1_scale, fe_b1):
    return core(x, fe_w0, fe_b0, e4m3fn_values(fe_w1_bytes) * fe_w1_scale.astype(np.float64), fe_b1)

@@ -1,0 +1,301 @@
+from contextlib import ExitStack
+
+import concourse.mybir as mybir
+from concourse.masks import make_identity
+
+F32 = mybir.dt.float32
+BF16 = mybir.dt.bfloat16
+U32 = mybir.dt.uint32
+U8 = mybir.dt.uint8
+FP8 = mybir.dt.float8_e4m3fn
+FP8X4 = mybir.dt.float8_e4m3fn_x4
+ALU = mybir.AluOpType
+ACT = mybir.ActivationFunctionType
+
+P = 128
+FLOPS = 2 * 128 * 512 * 512 * 2 + 2 * 4096 * 512 * 1024
+ALPHA = 0.2
+CHUNKS = 8
+TOK = 512
+
+
+def tile_graph_gan_pa_kernel(tc, x, fe_w0, fe_b0, fe_w1_bytes, fe_w1_scale, fe_b1, out):
+    nc = tc.nc
+    rows = out.rearrange("b i j c -> (b i j) c")
+
+    with ExitStack() as ctx:
+        keep = ctx.enter_context(tc.tile_pool(name="keep", bufs=1))
+        work = ctx.enter_context(tc.tile_pool(name="work", bufs=2))
+        psum = ctx.enter_context(tc.psum_pool(name="psum", bufs=4))
+        ctx.enter_context(tc.manual_schedule())
+
+        x_sb = keep.tile([P, 512], BF16, name="x_sb", align_bytes=64)
+        w0_raw = [keep.tile([P, 4, 512], BF16, name="w0_raw%d" % h, align_bytes=64) for h in range(2)]
+        w1_bytes = keep.tile([P, 4096], U8, name="w1_bytes", align_bytes=64)
+        w1_scale = keep.tile([P, 4], F32, name="w1_scale")
+        b0_sb = keep.tile([P, 4], BF16, name="b0_sb")
+        b1_rows = keep.tile([P, P], BF16, name="b1_rows")
+        b1_bc = keep.tile([P, P], BF16, name="b1_bc")
+        nc.sync.dma_start(out=x_sb[:], in_=x.rearrange("b n d -> (b n) d"))
+        for h in range(2):
+            nc.sync.dma_start(out=w0_raw[h][:], in_=fe_w0[512 * h : 512 * h + 512, :].rearrange("(p j) w -> p j w", j=4))
+        nc.sync.dma_start(out=w1_bytes[:], in_=fe_w1_bytes.rearrange("(p t) n -> p (t n)", t=4))
+        nc.scalar.dma_start(out=w1_scale[:], in_=fe_w1_scale.rearrange("(p t) o -> p (t o)", t=4))
+        nc.scalar.dma_start(out=b0_sb[:], in_=fe_b0.rearrange("(p t) -> p t", t=4))
+
+        ident = keep.tile([P, P], F32, name="ident")
+        identb = keep.tile([P, P], BF16, name="identb")
+        warm = keep.tile([P, 8], F32, name="warm")
+        nc.gpsimd.memset(warm[:], 0.0)
+        nc.gpsimd.memset(b1_rows[:], 0.0)
+        make_identity(nc, ident[:])
+        make_identity(nc, identb[:])
+        nc.sync.dma_start(out=b1_rows[0:8, :], in_=fe_b1.rearrange("(c m) -> c m", m=P))
+        nc.sync.dma_start(out=b1_bc[:], in_=fe_b1[896:1024].partition_broadcast(P))
+        nc.scalar.activation(out=warm[:], in_=warm[:], func=ACT.Identity, bias=0.0, scale=1.0)
+
+        xw = x_sb[:].bitcast(F32)
+        xt = psum.tile([P, 2, P], F32, name="xt", tag="mm")
+        for u in range(2):
+            nc.tensor.transpose(xt[:, u, :], xw[:, u:256:2], ident[:])
+        xg = keep.tile([P, P, 4], BF16, name="xg", align_bytes=64)
+        nc.vector.tensor_copy(out=xg[:].rearrange("p n t -> p (n t)").bitcast(F32).rearrange("p (n u) -> p n u", u=2), in_=xt[:].rearrange("p u n -> p n u"))
+
+        w0_g = [keep.tile([P, 2048], BF16, name="w0_g%d" % h, align_bytes=64) for h in range(2)]
+        w0_c = [keep.tile([P, 512], U32, name="w0_c%d" % h, align_bytes=64) for h in range(2)]
+        w0_s = [keep.tile([P, 512], U8, name="w0_s%d" % h, align_bytes=64) for h in range(2)]
+
+        def lay_w0(copy, h, t0, t1):
+            copy(
+                out=w0_g[h][:].rearrange("p (t m j) -> p t m j", t=4, j=4)[:, t0:t1],
+                in_=w0_raw[h][:].rearrange("p j (m t) -> p t m j", t=4)[:, t0:t1],
+            )
+
+        x_c = keep.tile([P, P], U32, name="x_c", align_bytes=64)
+        x_s = keep.tile([P, P], U8, name="x_s", align_bytes=64)
+        lay_w0(nc.vector.tensor_copy, 0, 0, 2)
+        lay_w0(nc.scalar.copy, 0, 2, 4)
+        nc.vector.quantize_mx(out=x_c[:].bitcast(FP8X4), scales=x_s[:], in_=xg[:].rearrange("p n t -> p (n t)"))
+        lay_w0(nc.vector.tensor_copy, 1, 0, 2)
+        nc.vector.quantize_mx(out=w0_c[0][:].bitcast(FP8X4), scales=w0_s[0][:], in_=w0_g[0][:])
+        lay_w0(nc.scalar.copy, 1, 2, 4)
+        nc.vector.quantize_mx(out=w0_c[1][:].bitcast(FP8X4), scales=w0_s[1][:], in_=w0_g[1][:])
+
+        w1_p = keep.tile([P, 4, 1024], BF16, name="w1_p", align_bytes=64)
+        w1_g = keep.tile([P, 1024, 4], BF16, name="w1_g", align_bytes=64)
+        w1_c = keep.tile([P, 1024], U32, name="w1_c", align_bytes=64)
+        w1_s = keep.tile([P, 1024], U8, name="w1_s", align_bytes=64)
+
+        def w1_widen(q, t):
+            n0 = 512 * q
+            nc.scalar.activation(
+                out=w1_p[:, t, n0 : n0 + 512],
+                in_=w1_bytes[:, 1024 * t + n0 : 1024 * t + n0 + 512].bitcast(FP8),
+                func=ACT.Copy,
+                scale=w1_scale[:, t : t + 1],
+            )
+
+        def w1_lay(copy, n0, n1):
+            copy(out=w1_g[:, n0:n1, :], in_=w1_p[:, :, n0:n1].rearrange("p t n -> p n t"))
+
+        def w1_quant(q):
+            n0 = 512 * q
+            nc.vector.quantize_mx(
+                out=w1_c[:, n0 : n0 + 512].bitcast(FP8X4),
+                scales=w1_s[:, n0 : n0 + 512],
+                in_=w1_g[:, n0 : n0 + 512, :].rearrange("p n t -> p (n t)"),
+            )
+
+        w1_widen(0, 0)
+        w1_widen(0, 1)
+        uv = []
+        for h in range(2):
+            acc = psum.tile([P, 4, P], F32, name="uv%d" % h, tag="mm")
+            for t in range(4):
+                nc.tensor.matmul_mx(
+                    out=acc[:, t, :],
+                    lhsT=w0_c[h][:, 128 * t : 128 * t + 128].bitcast(FP8X4),
+                    lhsT_scale=w0_s[h][:, 128 * t : 128 * t + 128],
+                    rhs=x_c[:].bitcast(FP8X4),
+                    rhs_scale=x_s[:],
+                    start=True,
+                    stop=True,
+                )
+            uv.append(acc)
+        u_sb = keep.tile([P, P, 4], F32, name="u_sb")
+        v_sb = keep.tile([P, P, 4], F32, name="v_sb")
+        nc.scalar.copy(out=u_sb[:], in_=uv[0][:].rearrange("p t n -> p n t"))
+        nc.vector.tensor_tensor(out=v_sb[:], in0=uv[1][:].rearrange("p t n -> p n t"), in1=b0_sb[:].unsqueeze(1).to_broadcast([P, P, 4]), op=ALU.add)
+        w1_widen(0, 2)
+        w1_widen(0, 3)
+        w1_lay(nc.scalar.copy, 0, 512)
+        for t in range(4):
+            w1_widen(1, t)
+        b1_t = psum.tile([P, P], BF16, name="b1_t", tag="tp")
+        nc.tensor.transpose(b1_t[:], b1_rows[:], identb[:])
+        b1_a = keep.tile([P, 8], F32, name="b1_a")
+        nc.scalar.activation(out=b1_a[:], in_=b1_t[:, 0:8], func=ACT.Copy, scale=ALPHA)
+
+        zpre = {}
+        e1 = {}
+        codes = {}
+
+        def e1_add(k, g):
+            b, i0 = k // 2, 16 * (k % 2) + 8 * g
+            z = work.tile([P, 8, 32, 4], F32, name="zpre", tag="zpre", bufs=3)
+            nc.vector.tensor_tensor(
+                out=z[:],
+                in0=u_sb[:, 32 * b + i0 : 32 * b + i0 + 8, :].unsqueeze(2).to_broadcast([P, 8, 32, 4]),
+                in1=v_sb[:, 32 * b : 32 * b + 32, :].unsqueeze(1).to_broadcast([P, 8, 32, 4]),
+                op=ALU.add,
+            )
+            zpre[k, g] = z
+
+        def e1_lrelu(k, g):
+            if g == 0:
+                e1[k] = work.tile([P, 2048], BF16, name="e1", tag="e1", align_bytes=64)
+            z = zpre[k, g][:].rearrange("p i j t -> p (i j t)")
+            nc.vector.scalar_tensor_tensor(out=e1[k][:, 1024 * g : 1024 * g + 1024], in0=z, scalar=ALPHA, in1=z, op0=ALU.mult, op1=ALU.max)
+
+        def e1_quant(k):
+            c = work.tile([P, TOK], U32, name="e1_c", tag="e1_c", bufs=3, align_bytes=64)
+            s = work.tile([P, TOK], U8, name="e1_s", tag="e1_s", bufs=3, align_bytes=64)
+            nc.vector.quantize_mx(out=c[:].bitcast(FP8X4), scales=s[:], in_=e1[k][:])
+            codes[k] = (c, s)
+
+        rounds = [(k, h) for k in range(CHUNKS) for h in range(2)]
+
+        def ctiles(r):
+            return [0, 1, 2, 3] if rounds[r][1] == 0 else [4, 5, 6]
+
+        pt = {}
+        at = {}
+        rt = {}
+        o_sb = {}
+        p1 = {}
+        zp = {}
+
+        def mx(r, i):
+            k = rounds[r][0]
+            c = ctiles(r)[i]
+            acc = psum.tile([P, TOK], F32, name="pt", tag="mm")
+            nc.tensor.matmul_mx(
+                out=acc[:],
+                lhsT=w1_c[:, 128 * c : 128 * c + 128].bitcast(FP8X4),
+                lhsT_scale=w1_s[:, 128 * c : 128 * c + 128],
+                rhs=codes[k][0][:].bitcast(FP8X4),
+                rhs_scale=codes[k][1][:],
+                start=True,
+                stop=True,
+            )
+            pt[r, i] = acc
+
+        def mx_tok(k):
+            acc = psum.tile([P, 4, P], F32, name="p1", tag="mm")
+            for s in range(4):
+                nc.tensor.matmul_mx(
+                    out=acc[:, s, :],
+                    lhsT=codes[k][0][:, 128 * s : 128 * s + 128].bitcast(FP8X4),
+                    lhsT_scale=codes[k][1][:, 128 * s : 128 * s + 128],
+                    rhs=w1_c[:, 896:1024].bitcast(FP8X4),
+                    rhs_scale=w1_s[:, 896:1024],
+                    start=True,
+                    stop=True,
+                )
+            p1[k] = acc
+
+        def p1_add(k):
+            z = work.tile([P, 4, P], F32, name="zp", tag="zp")
+            nc.vector.tensor_tensor(out=z[:], in0=p1[k][:], in1=b1_bc[:].unsqueeze(1).to_broadcast([P, 4, P]), op=ALU.add)
+            zp[k] = z
+
+        def p1_lrelu(k):
+            nc.vector.scalar_tensor_tensor(out=o_sb[k, 1][:, :, 384:512], in0=zp[k][:], scalar=ALPHA, in1=zp[k][:], op0=ALU.mult, op1=ALU.max)
+
+        def lin(r, i):
+            if i == 0:
+                at[r] = work.tile([P, 4, TOK], F32, name="at", tag="at", bufs=4)
+                rt[r] = work.tile([P, 4, TOK], F32, name="rt", tag="rt", bufs=4)
+                o_sb[rounds[r]] = work.tile([P, 4, TOK], F32, name="o_sb%d" % rounds[r][1], tag="o_sb%d" % rounds[r][1])
+            c = ctiles(r)[i]
+            nc.scalar.activation(out=at[r][:, i, :], in_=pt[r, i][:], func=ACT.Identity, bias=b1_a[:, c : c + 1], scale=ALPHA)
+
+        def relu(r, i0, i1):
+            nc.vector.tensor_scalar(out=rt[r][:, i0:i1, :], in0=at[r][:, i0:i1, :], scalar1=4.0, scalar2=0.0, op0=ALU.mult, op1=ALU.max)
+
+        tp = {}
+
+        def turn(r, s):
+            acc = psum.tile([P, TOK], F32, name="tp", tag="tp")
+            for i in range(len(ctiles(r))):
+                for n, src in enumerate((at[r], rt[r])):
+                    nc.tensor.matmul(
+                        acc[:, 128 * i : 128 * i + 128],
+                        lhsT=src[:, i, 128 * s : 128 * s + 128],
+                        rhs=ident[:],
+                        is_transpose=True,
+                        start=(n == 0),
+                        stop=(n == 1),
+                    )
+            tp[r, s] = acc
+
+        def leave(r, s):
+            k, h = rounds[r]
+            w = 128 * len(ctiles(r))
+            if r >= 14 and s % 2 == 1:
+                nc.vector.tensor_copy(out=o_sb[k, h][:, s, 0:w], in_=tp[r, s][:, 0:w])
+            else:
+                nc.scalar.copy(out=o_sb[k, h][:, s, 0:w], in_=tp[r, s][:, 0:w])
+            r0 = TOK * k + 128 * s
+            nc.sync.dma_start(out=rows[r0 : r0 + 128, 512 * h : 512 * h + 512], in_=o_sb[k, h][:, s, :])
+
+        e1_add(0, 0)
+        e1_add(0, 1)
+        e1_lrelu(0, 0)
+        w1_quant(0)
+        e1_lrelu(0, 1)
+        w1_lay(nc.vector.tensor_copy, 512, 1024)
+        e1_quant(0)
+        w1_quant(1)
+        for i in range(4):
+            mx(0, i)
+
+        pieces = []
+        for k in range(1, CHUNKS):
+            pieces += [(e1_add, k, 0), (e1_add, k, 1), (e1_lrelu, k, 0), (e1_lrelu, k, 1), (e1_quant, k)]
+
+        def due(g):
+            if g < 4:
+                return g + 2
+            if g < 10:
+                return 5 + (5 * (g - 3)) // 6
+            return 10 + (5 * (g - 9)) // 8
+
+        nr = len(rounds)
+        done = 0
+        for r in range(nr + 2):
+            k, h = rounds[r] if r < nr else (CHUNKS, 0)
+            for i in range(4):
+                if r < nr and i < len(ctiles(r)):
+                    lin(r, i)
+                while done < min(due(4 * r + i), len(pieces)):
+                    pieces[done][0](*pieces[done][1:])
+                    done += 1
+                if r < nr and h == 1 and i == 2:
+                    p1_add(k)
+                if r < nr and i % 2 == 1:
+                    relu(r, i - 1, min(i + 1, len(ctiles(r))))
+                if r < nr and h == 1 and i == 3:
+                    p1_lrelu(k)
+                if r > 1:
+                    leave(r - 2, i)
+                if i % 2 == 1:
+                    if 0 < r <= nr:
+                        turn(r - 1, i - 1)
+                        turn(r - 1, i)
+                    if r + 1 < nr:
+                        for m in (i - 1, i):
+                            if m < len(ctiles(r + 1)):
+                                mx(r + 1, m)
+                            else:
+                                mx_tok(k)

@@ -16,6 +16,14 @@ P = 128
 FLOPS = 2 * 128 * 512 * 512 * 2 + 2 * 4096 * 512 * 1024
 ALPHA = 0.2
 CHUNKS = 8
+W0_V = 2
+W0B_V = 2
+ORDER = 0
+FINE = 6
+VLEAVE = 1
+D_FIRST = 1
+D_PEN = 2
+VWIDEN = 1
 TOK = 512
 
 
@@ -31,15 +39,22 @@ def tile_graph_gan_pa_kernel(tc, x, fe_w0, fe_b0, fe_w1_bytes, fe_w1_scale, fe_b
 
         x_sb = keep.tile([P, 512], BF16, name="x_sb", align_bytes=64)
         w0_raw = [keep.tile([P, 4, 512], BF16, name="w0_raw%d" % h, align_bytes=64) for h in range(2)]
-        w1_bytes = keep.tile([P, 4096], U8, name="w1_bytes", align_bytes=64)
+        w1_bytes = [keep.tile([P, 2048], U8, name="w1_bytes%d" % g, align_bytes=64) for g in range(2)]
         w1_scale = keep.tile([P, 4], F32, name="w1_scale")
         b0_sb = keep.tile([P, 4], BF16, name="b0_sb")
         b1_rows = keep.tile([P, P], BF16, name="b1_rows")
-        b1_bc = keep.tile([P, P], BF16, name="b1_bc")
-        nc.sync.dma_start(out=x_sb[:], in_=x.rearrange("b n d -> (b n) d"))
-        for h in range(2):
+        b1_bc = keep.tile([P, 512], BF16, name="b1_bc")
+        w1_rows = fe_w1_bytes.rearrange("(p t) n -> p (t n)", t=4)
+
+        def load_w0(h):
             nc.sync.dma_start(out=w0_raw[h][:], in_=fe_w0[512 * h : 512 * h + 512, :].rearrange("(p j) w -> p j w", j=4))
-        nc.sync.dma_start(out=w1_bytes[:], in_=fe_w1_bytes.rearrange("(p t) n -> p (t n)", t=4))
+
+        def load_w1(g):
+            nc.sync.dma_start(out=w1_bytes[g][:], in_=w1_rows[:, 2048 * g : 2048 * g + 2048])
+
+        nc.sync.dma_start(out=x_sb[:], in_=x.rearrange("b n d -> (b n) d"))
+        for f, a in [[(load_w0, 0), (load_w0, 1), (load_w1, 0), (load_w1, 1)], [(load_w1, 0), (load_w0, 0), (load_w0, 1), (load_w1, 1)], [(load_w0, 0), (load_w1, 0), (load_w0, 1), (load_w1, 1)]][ORDER]:
+            f(a)
         nc.scalar.dma_start(out=w1_scale[:], in_=fe_w1_scale.rearrange("(p t) o -> p (t o)", t=4))
         nc.scalar.dma_start(out=b0_sb[:], in_=fe_b0.rearrange("(p t) -> p t", t=4))
 
@@ -51,7 +66,7 @@ def tile_graph_gan_pa_kernel(tc, x, fe_w0, fe_b0, fe_w1_bytes, fe_w1_scale, fe_b
         make_identity(nc, ident[:])
         make_identity(nc, identb[:])
         nc.sync.dma_start(out=b1_rows[0:8, :], in_=fe_b1.rearrange("(c m) -> c m", m=P))
-        nc.sync.dma_start(out=b1_bc[:], in_=fe_b1[896:1024].partition_broadcast(P))
+        nc.sync.dma_start(out=b1_bc[:], in_=fe_b1[512:1024].partition_broadcast(P))
         nc.scalar.activation(out=warm[:], in_=warm[:], func=ACT.Identity, bias=0.0, scale=1.0)
 
         xw = x_sb[:].bitcast(F32)
@@ -66,48 +81,52 @@ def tile_graph_gan_pa_kernel(tc, x, fe_w0, fe_b0, fe_w1_bytes, fe_w1_scale, fe_b
         w0_s = [keep.tile([P, 512], U8, name="w0_s%d" % h, align_bytes=64) for h in range(2)]
 
         def lay_w0(copy, h, t0, t1):
-            copy(
-                out=w0_g[h][:].rearrange("p (t m j) -> p t m j", t=4, j=4)[:, t0:t1],
-                in_=w0_raw[h][:].rearrange("p j (m t) -> p t m j", t=4)[:, t0:t1],
-            )
+            if t1 > t0:
+                copy(
+                    out=w0_g[h][:].rearrange("p (t m j) -> p t m j", t=4, j=4)[:, t0:t1],
+                    in_=w0_raw[h][:].rearrange("p j (m t) -> p t m j", t=4)[:, t0:t1],
+                )
+
+        w1_p = keep.tile([P, 4, 1024], BF16, name="w1_p", align_bytes=64)
+        w1_g = [keep.tile([P, 512, 4], BF16, name="w1_g%d" % q, align_bytes=64) for q in range(2)]
+        w1_c = [keep.tile([P, 512], U32, name="w1_c%d" % q, align_bytes=64) for q in range(2)]
+        w1_s = [keep.tile([P, 512], U8, name="w1_s%d" % q, align_bytes=64) for q in range(2)]
+
+        def w1_widen(t):
+            n0 = 1024 * (t % 2)
+            src = w1_bytes[t // 2][:, n0 : n0 + 1024].bitcast(FP8)
+            if t >= 4 - VWIDEN:
+                nc.vector.tensor_scalar(out=w1_p[:, t, :], in0=src, scalar1=w1_scale[:, t : t + 1], scalar2=None, op0=ALU.mult)
+            else:
+                nc.scalar.activation(out=w1_p[:, t, :], in_=src, func=ACT.Copy, scale=w1_scale[:, t : t + 1])
+
+        def w1_lay(q):
+            nc.scalar.copy(out=w1_g[q][:].rearrange("p (c i) t -> p c t i", i=4), in_=w1_p[:, :, 512 * q : 512 * q + 512].rearrange("p t (c i) -> p c t i", i=4))
+
+        def w1_quant(q):
+            nc.vector.quantize_mx(out=w1_c[q][:].bitcast(FP8X4), scales=w1_s[q][:], in_=w1_g[q][:].rearrange("p n t -> p (n t)"))
 
         x_c = keep.tile([P, P], U32, name="x_c", align_bytes=64)
         x_s = keep.tile([P, P], U8, name="x_s", align_bytes=64)
-        lay_w0(nc.vector.tensor_copy, 0, 0, 2)
-        lay_w0(nc.scalar.copy, 0, 2, 4)
+        if ORDER == 1:
+            w1_widen(0)
+            w1_widen(1)
+        lay_w0(nc.vector.tensor_copy, 0, 0, W0_V)
+        lay_w0(nc.scalar.copy, 0, W0_V, 4)
         nc.vector.quantize_mx(out=x_c[:].bitcast(FP8X4), scales=x_s[:], in_=xg[:].rearrange("p n t -> p (n t)"))
-        lay_w0(nc.vector.tensor_copy, 1, 0, 2)
+        lay_w0(nc.vector.tensor_copy, 1, 0, W0B_V)
         nc.vector.quantize_mx(out=w0_c[0][:].bitcast(FP8X4), scales=w0_s[0][:], in_=w0_g[0][:])
-        lay_w0(nc.scalar.copy, 1, 2, 4)
+        if ORDER == 2:
+            w1_widen(0)
+            w1_widen(1)
+        lay_w0(nc.scalar.copy, 1, W0B_V, 4)
         nc.vector.quantize_mx(out=w0_c[1][:].bitcast(FP8X4), scales=w0_s[1][:], in_=w0_g[1][:])
 
-        w1_p = keep.tile([P, 4, 1024], BF16, name="w1_p", align_bytes=64)
-        w1_g = keep.tile([P, 1024, 4], BF16, name="w1_g", align_bytes=64)
-        w1_c = keep.tile([P, 1024], U32, name="w1_c", align_bytes=64)
-        w1_s = keep.tile([P, 1024], U8, name="w1_s", align_bytes=64)
-
-        def w1_widen(q, t):
-            n0 = 512 * q
-            nc.scalar.activation(
-                out=w1_p[:, t, n0 : n0 + 512],
-                in_=w1_bytes[:, 1024 * t + n0 : 1024 * t + n0 + 512].bitcast(FP8),
-                func=ACT.Copy,
-                scale=w1_scale[:, t : t + 1],
-            )
-
-        def w1_lay(copy, n0, n1):
-            copy(out=w1_g[:, n0:n1, :], in_=w1_p[:, :, n0:n1].rearrange("p t n -> p n t"))
-
-        def w1_quant(q):
-            n0 = 512 * q
-            nc.vector.quantize_mx(
-                out=w1_c[:, n0 : n0 + 512].bitcast(FP8X4),
-                scales=w1_s[:, n0 : n0 + 512],
-                in_=w1_g[:, n0 : n0 + 512, :].rearrange("p n t -> p (n t)"),
-            )
-
-        w1_widen(0, 0)
-        w1_widen(0, 1)
+        if ORDER == 0:
+            w1_widen(0)
+        else:
+            w1_widen(2)
+        w1_widen(3)
         uv = []
         for h in range(2):
             acc = psum.tile([P, 4, P], F32, name="uv%d" % h, tag="mm")
@@ -126,15 +145,15 @@ def tile_graph_gan_pa_kernel(tc, x, fe_w0, fe_b0, fe_w1_bytes, fe_w1_scale, fe_b
         v_sb = keep.tile([P, P, 4], F32, name="v_sb")
         nc.scalar.copy(out=u_sb[:], in_=uv[0][:].rearrange("p t n -> p n t"))
         nc.vector.tensor_tensor(out=v_sb[:], in0=uv[1][:].rearrange("p t n -> p n t"), in1=b0_sb[:].unsqueeze(1).to_broadcast([P, P, 4]), op=ALU.add)
-        w1_widen(0, 2)
-        w1_widen(0, 3)
-        w1_lay(nc.scalar.copy, 0, 512)
-        for t in range(4):
-            w1_widen(1, t)
+        if ORDER == 0:
+            w1_widen(1)
+            w1_widen(2)
+        w1_lay(0)
         b1_t = psum.tile([P, P], BF16, name="b1_t", tag="tp")
         nc.tensor.transpose(b1_t[:], b1_rows[:], identb[:])
         b1_a = keep.tile([P, 8], F32, name="b1_a")
         nc.scalar.activation(out=b1_a[:], in_=b1_t[:, 0:8], func=ACT.Copy, scale=ALPHA)
+        w1_lay(1)
 
         zpre = {}
         e1 = {}
@@ -163,139 +182,159 @@ def tile_graph_gan_pa_kernel(tc, x, fe_w0, fe_b0, fe_w1_bytes, fe_w1_scale, fe_b
             nc.vector.quantize_mx(out=c[:].bitcast(FP8X4), scales=s[:], in_=e1[k][:])
             codes[k] = (c, s)
 
-        rounds = [(k, h) for k in range(CHUNKS) for h in range(2)]
+        last = CHUNKS - 1
 
-        def ctiles(r):
-            return [0, 1, 2, 3] if rounds[r][1] == 0 else [4, 5, 6]
+        def direct_tiles(k):
+            return 4 if k == last else D_PEN if k == last - 1 else D_FIRST if k == 0 else 1
 
+        rounds = []
+        for k in range(CHUNKS):
+            nd = direct_tiles(k)
+            parts = [(k, s * (4 // nd), (s + 1) * (4 // nd), 512 - 128 * nd) for s in range(nd)]
+            if k < last:
+                rounds.append(([(k, c) for c in range(4)], []))
+                rounds.append(([(k, c) for c in range(4, 8 - nd)], parts))
+            else:
+                rounds.append(([(k, 0), (k, 1)], parts[0:2]))
+                rounds.append(([(k, 2), (k, 3)], parts[2:4]))
+        nr = len(rounds)
         pt = {}
         at = {}
         rt = {}
+        tp = {}
         o_sb = {}
         p1 = {}
         zp = {}
 
-        def mx(r, i):
-            k = rounds[r][0]
-            c = ctiles(r)[i]
-            acc = psum.tile([P, TOK], F32, name="pt", tag="mm")
-            nc.tensor.matmul_mx(
-                out=acc[:],
-                lhsT=w1_c[:, 128 * c : 128 * c + 128].bitcast(FP8X4),
-                lhsT_scale=w1_s[:, 128 * c : 128 * c + 128],
-                rhs=codes[k][0][:].bitcast(FP8X4),
-                rhs_scale=codes[k][1][:],
-                start=True,
-                stop=True,
-            )
-            pt[r, i] = acc
+        def out_tile(k, h):
+            if (k, h) not in o_sb:
+                o_sb[k, h] = work.tile([P, 4, 512], F32, name="o_sb", tag="o_sb", bufs=4)
+            return o_sb[k, h]
 
-        def mx_tok(k):
-            acc = psum.tile([P, 4, P], F32, name="p1", tag="mm")
-            for s in range(4):
+        def store(k, h, c0, c1):
+            dst = rows[TOK * k : TOK * k + TOK, 512 * h + c0 : 512 * h + c1].rearrange("(s p) c -> p s c", p=P)
+            nc.sync.dma_start(out=dst, in_=o_sb[k, h][:, :, c0:c1])
+
+        def products(r):
+            for k, c in rounds[r][0]:
+                m0 = 128 * (c % 4)
+                acc = psum.tile([P, TOK], F32, name="pt", tag="mm")
                 nc.tensor.matmul_mx(
-                    out=acc[:, s, :],
-                    lhsT=codes[k][0][:, 128 * s : 128 * s + 128].bitcast(FP8X4),
-                    lhsT_scale=codes[k][1][:, 128 * s : 128 * s + 128],
-                    rhs=w1_c[:, 896:1024].bitcast(FP8X4),
-                    rhs_scale=w1_s[:, 896:1024],
+                    out=acc[:],
+                    lhsT=w1_c[c // 4][:, m0 : m0 + 128].bitcast(FP8X4),
+                    lhsT_scale=w1_s[c // 4][:, m0 : m0 + 128],
+                    rhs=codes[k][0][:].bitcast(FP8X4),
+                    rhs_scale=codes[k][1][:],
                     start=True,
                     stop=True,
                 )
-            p1[k] = acc
-
-        def p1_add(k):
-            z = work.tile([P, 4, P], F32, name="zp", tag="zp")
-            nc.vector.tensor_tensor(out=z[:], in0=p1[k][:], in1=b1_bc[:].unsqueeze(1).to_broadcast([P, 4, P]), op=ALU.add)
-            zp[k] = z
-
-        def p1_lrelu(k):
-            nc.vector.scalar_tensor_tensor(out=o_sb[k, 1][:, :, 384:512], in0=zp[k][:], scalar=ALPHA, in1=zp[k][:], op0=ALU.mult, op1=ALU.max)
+                pt[k, c] = acc
+            for k, s0, s1, n0 in rounds[r][1]:
+                acc = psum.tile([P, s1 - s0, 512 - n0], F32, name="p1", tag="mm")
+                for s in range(s0, s1):
+                    nc.tensor.matmul_mx(
+                        out=acc[:, s - s0, :],
+                        lhsT=codes[k][0][:, 128 * s : 128 * s + 128].bitcast(FP8X4),
+                        lhsT_scale=codes[k][1][:, 128 * s : 128 * s + 128],
+                        rhs=w1_c[1][:, n0:512].bitcast(FP8X4),
+                        rhs_scale=w1_s[1][:, n0:512],
+                        start=True,
+                        stop=True,
+                    )
+                p1[k, s0] = acc
 
         def lin(r, i):
             if i == 0:
-                at[r] = work.tile([P, 4, TOK], F32, name="at", tag="at", bufs=4)
-                rt[r] = work.tile([P, 4, TOK], F32, name="rt", tag="rt", bufs=4)
-                o_sb[rounds[r]] = work.tile([P, 4, TOK], F32, name="o_sb%d" % rounds[r][1], tag="o_sb%d" % rounds[r][1])
-            c = ctiles(r)[i]
-            nc.scalar.activation(out=at[r][:, i, :], in_=pt[r, i][:], func=ACT.Identity, bias=b1_a[:, c : c + 1], scale=ALPHA)
+                at[r] = work.tile([P, 4, TOK], F32, name="at", tag="at", bufs=3)
+                rt[r] = work.tile([P, 4, TOK], F32, name="rt", tag="rt", bufs=3)
+            k, c = rounds[r][0][i]
+            nc.scalar.activation(out=at[r][:, i, :], in_=pt[k, c][:], func=ACT.Identity, bias=b1_a[:, c : c + 1], scale=ALPHA)
 
         def relu(r, i0, i1):
             nc.vector.tensor_scalar(out=rt[r][:, i0:i1, :], in0=at[r][:, i0:i1, :], scalar1=4.0, scalar2=0.0, op0=ALU.mult, op1=ALU.max)
 
-        tp = {}
-
-        def turn(r, s):
-            acc = psum.tile([P, TOK], F32, name="tp", tag="tp")
-            for i in range(len(ctiles(r))):
+        def turn(r, i):
+            acc = psum.tile([P, 4, P], F32, name="tp", tag="tp")
+            for s in range(4):
                 for n, src in enumerate((at[r], rt[r])):
-                    nc.tensor.matmul(
-                        acc[:, 128 * i : 128 * i + 128],
-                        lhsT=src[:, i, 128 * s : 128 * s + 128],
-                        rhs=ident[:],
-                        is_transpose=True,
-                        start=(n == 0),
-                        stop=(n == 1),
-                    )
-            tp[r, s] = acc
+                    nc.tensor.matmul(acc[:, s, :], lhsT=src[:, i, 128 * s : 128 * s + 128], rhs=ident[:], is_transpose=True, start=(n == 0), stop=(n == 1))
+            tp[r, i] = acc
 
-        def leave(r, s):
-            k, h = rounds[r]
-            w = 128 * len(ctiles(r))
-            if r >= 14 and s % 2 == 1:
-                nc.vector.tensor_copy(out=o_sb[k, h][:, s, 0:w], in_=tp[r, s][:, 0:w])
-            else:
-                nc.scalar.copy(out=o_sb[k, h][:, s, 0:w], in_=tp[r, s][:, 0:w])
-            r0 = TOK * k + 128 * s
-            nc.sync.dma_start(out=rows[r0 : r0 + 128, 512 * h : 512 * h + 512], in_=o_sb[k, h][:, s, :])
+        def leave(r, i):
+            k, c = rounds[r][0][i]
+            m0 = 128 * (c % 4)
+            copy = nc.vector.tensor_copy if r == nr - 1 and i < VLEAVE else nc.scalar.copy
+            copy(out=out_tile(k, c // 4)[:, :, m0 : m0 + 128], in_=tp[r, i][:])
+            if k == last and c >= 2:
+                store(k, 0, m0, m0 + 128)
+            elif k >= FINE:
+                if c % 2 == 1:
+                    store(k, c // 4, m0 - 128, m0 + 128)
+                elif c == 6:
+                    store(k, 1, 256, 512)
+            elif c == 3 or c == 7 - direct_tiles(k):
+                store(k, c // 4, 0, 512)
+
+        def direct_add(k, s0, s1, n0):
+            z = work.tile([P, s1 - s0, 512 - n0], F32, name="zp", tag="zp")
+            nc.vector.tensor_tensor(out=z[:], in0=p1[k, s0][:], in1=b1_bc[:, n0:512].unsqueeze(1).to_broadcast([P, s1 - s0, 512 - n0]), op=ALU.add)
+            zp[k, s0] = z
+
+        def direct_lrelu(k, s0, s1, n0):
+            z = zp[k, s0][:]
+            nc.vector.scalar_tensor_tensor(out=out_tile(k, 1)[:, s0:s1, n0:512], in0=z, scalar=ALPHA, in1=z, op0=ALU.mult, op1=ALU.max)
+
+        def direct_store(k, s0, s1, n0):
+            if k == last:
+                r0 = TOK * k + 128 * s0
+                nc.sync.dma_start(out=rows[r0 : r0 + 128, 512:1024], in_=o_sb[k, 1][:, s0, :])
+            elif n0 == 256 and s1 == 4 and k >= FINE:
+                store(k, 1, 256, 512)
 
         e1_add(0, 0)
         e1_add(0, 1)
         e1_lrelu(0, 0)
-        w1_quant(0)
         e1_lrelu(0, 1)
-        w1_lay(nc.vector.tensor_copy, 512, 1024)
+        e1_add(1, 0)
         e1_quant(0)
-        w1_quant(1)
-        for i in range(4):
-            mx(0, i)
+        w1_quant(0)
+        e1_add(1, 1)
+        products(0)
 
-        pieces = []
-        for k in range(1, CHUNKS):
-            pieces += [(e1_add, k, 0), (e1_add, k, 1), (e1_lrelu, k, 0), (e1_lrelu, k, 1), (e1_quant, k)]
-
-        def due(g):
-            if g < 4:
-                return g + 2
-            if g < 10:
-                return 5 + (5 * (g - 3)) // 6
-            return 10 + (5 * (g - 9)) // 8
-
-        nr = len(rounds)
-        done = 0
-        for r in range(nr + 2):
-            k, h = rounds[r] if r < nr else (CHUNKS, 0)
-            for i in range(4):
-                if r < nr and i < len(ctiles(r)):
-                    lin(r, i)
-                while done < min(due(4 * r + i), len(pieces)):
-                    pieces[done][0](*pieces[done][1:])
-                    done += 1
-                if r < nr and h == 1 and i == 2:
-                    p1_add(k)
-                if r < nr and i % 2 == 1:
-                    relu(r, i - 1, min(i + 1, len(ctiles(r))))
-                if r < nr and h == 1 and i == 3:
-                    p1_lrelu(k)
-                if r > 1:
-                    leave(r - 2, i)
-                if i % 2 == 1:
-                    if 0 < r <= nr:
-                        turn(r - 1, i - 1)
-                        turn(r - 1, i)
-                    if r + 1 < nr:
-                        for m in (i - 1, i):
-                            if m < len(ctiles(r + 1)):
-                                mx(r + 1, m)
-                            else:
-                                mx_tok(k)
+        for r in range(nr + 1):
+            k, h = divmod(r, 2)
+            tiles, parts = rounds[r] if r < nr else ([], [])
+            n = len(tiles)
+            if r > 0:
+                for i in range(len(rounds[r - 1][0])):
+                    turn(r - 1, i)
+            for i in range(n):
+                lin(r, i)
+            if r < nr and h == 0 and k < last:
+                e1_lrelu(k + 1, 0)
+                relu(r, 0, 2)
+                if r == 0:
+                    w1_quant(1)
+                e1_lrelu(k + 1, 1)
+                relu(r, 2, 4)
+                e1_quant(k + 1)
+            elif r < nr:
+                for part in parts:
+                    direct_add(*part)
+                if k + 2 <= last:
+                    e1_add(k + 2, 0)
+                if k == last:
+                    relu(r, 0, n)
+                for part in parts:
+                    direct_lrelu(*part)
+                if k < last:
+                    relu(r, 0, n)
+                if k + 2 <= last:
+                    e1_add(k + 2, 1)
+            if r + 1 < nr:
+                products(r + 1)
+            if r > 0:
+                for i in range(len(rounds[r - 1][0])):
+                    leave(r - 1, i)
+            for part in parts:
+                direct_store(*part)

@@ -18,12 +18,16 @@ ALPHA = 0.2
 CHUNKS = 8
 W0_V = 2
 W0B_V = 2
-ORDER = 0
-FINE = 6
-VLEAVE = 1
-D_FIRST = 1
+XAT = 1
+WIDE = 0
+NPS = 2
+FINE = 5
+VLEAVE = 0
+N_ZERO = 1
+Q1_PRE = 1
+TAIL = 1
 D_PEN = 2
-VWIDEN = 1
+VWIDEN = 0
 TOK = 512
 
 
@@ -52,9 +56,14 @@ def tile_graph_gan_pa_kernel(tc, x, fe_w0, fe_b0, fe_w1_bytes, fe_w1_scale, fe_b
         def load_w1(g):
             nc.sync.dma_start(out=w1_bytes[g][:], in_=w1_rows[:, 2048 * g : 2048 * g + 2048])
 
-        nc.sync.dma_start(out=x_sb[:], in_=x.rearrange("b n d -> (b n) d"))
-        for f, a in [[(load_w0, 0), (load_w0, 1), (load_w1, 0), (load_w1, 1)], [(load_w1, 0), (load_w0, 0), (load_w0, 1), (load_w1, 1)], [(load_w0, 0), (load_w1, 0), (load_w0, 1), (load_w1, 1)]][ORDER]:
-            f(a)
+        load_w0(0)
+        if XAT == 1:
+            nc.sync.dma_start(out=x_sb[:], in_=x.rearrange("b n d -> (b n) d"))
+        load_w0(1)
+        if XAT == 2:
+            nc.sync.dma_start(out=x_sb[:], in_=x.rearrange("b n d -> (b n) d"))
+        load_w1(0)
+        load_w1(1)
         nc.scalar.dma_start(out=w1_scale[:], in_=fe_w1_scale.rearrange("(p t) o -> p (t o)", t=4))
         nc.scalar.dma_start(out=b0_sb[:], in_=fe_b0.rearrange("(p t) -> p t", t=4))
 
@@ -69,13 +78,6 @@ def tile_graph_gan_pa_kernel(tc, x, fe_w0, fe_b0, fe_w1_bytes, fe_w1_scale, fe_b
         nc.sync.dma_start(out=b1_bc[:], in_=fe_b1[512:1024].partition_broadcast(P))
         nc.scalar.activation(out=warm[:], in_=warm[:], func=ACT.Identity, bias=0.0, scale=1.0)
 
-        xw = x_sb[:].bitcast(F32)
-        xt = psum.tile([P, 2, P], F32, name="xt", tag="mm")
-        for u in range(2):
-            nc.tensor.transpose(xt[:, u, :], xw[:, u:256:2], ident[:])
-        xg = keep.tile([P, P, 4], BF16, name="xg", align_bytes=64)
-        nc.vector.tensor_copy(out=xg[:].rearrange("p n t -> p (n t)").bitcast(F32).rearrange("p (n u) -> p n u", u=2), in_=xt[:].rearrange("p u n -> p n u"))
-
         w0_g = [keep.tile([P, 2048], BF16, name="w0_g%d" % h, align_bytes=64) for h in range(2)]
         w0_c = [keep.tile([P, 512], U32, name="w0_c%d" % h, align_bytes=64) for h in range(2)]
         w0_s = [keep.tile([P, 512], U8, name="w0_s%d" % h, align_bytes=64) for h in range(2)]
@@ -87,48 +89,44 @@ def tile_graph_gan_pa_kernel(tc, x, fe_w0, fe_b0, fe_w1_bytes, fe_w1_scale, fe_b
                     in_=w0_raw[h][:].rearrange("p j (m t) -> p t m j", t=4)[:, t0:t1],
                 )
 
-        w1_p = keep.tile([P, 4, 1024], BF16, name="w1_p", align_bytes=64)
+        w1_p = [keep.tile([P, 4, 512], BF16, name="w1_p%d" % q, align_bytes=64) for q in range(2)]
         w1_g = [keep.tile([P, 512, 4], BF16, name="w1_g%d" % q, align_bytes=64) for q in range(2)]
         w1_c = [keep.tile([P, 512], U32, name="w1_c%d" % q, align_bytes=64) for q in range(2)]
         w1_s = [keep.tile([P, 512], U8, name="w1_s%d" % q, align_bytes=64) for q in range(2)]
 
-        def w1_widen(t):
-            n0 = 1024 * (t % 2)
-            src = w1_bytes[t // 2][:, n0 : n0 + 1024].bitcast(FP8)
-            if t >= 4 - VWIDEN:
-                nc.vector.tensor_scalar(out=w1_p[:, t, :], in0=src, scalar1=w1_scale[:, t : t + 1], scalar2=None, op0=ALU.mult)
+        def w1_widen(q, t):
+            n0 = 1024 * (t % 2) + 512 * q
+            src = w1_bytes[t // 2][:, n0 : n0 + 512].bitcast(FP8)
+            dst = w1_p[q][:, t, :]
+            if 4 * q + t >= 8 - VWIDEN:
+                nc.vector.tensor_scalar(out=dst, in0=src, scalar1=w1_scale[:, t : t + 1], scalar2=None, op0=ALU.mult)
             else:
-                nc.scalar.activation(out=w1_p[:, t, :], in_=src, func=ACT.Copy, scale=w1_scale[:, t : t + 1])
+                nc.scalar.activation(out=dst, in_=src, func=ACT.Copy, scale=w1_scale[:, t : t + 1])
 
-        def w1_lay(q):
-            nc.scalar.copy(out=w1_g[q][:].rearrange("p (c i) t -> p c t i", i=4), in_=w1_p[:, :, 512 * q : 512 * q + 512].rearrange("p t (c i) -> p c t i", i=4))
+        w1_ps = {}
+
+        def w1_weave(q, g):
+            acc = psum.tile([P, 2, 128, 4], BF16, name="w1_ps", tag="tp")
+            for m in range(2):
+                n0 = 256 * g + 128 * m
+                nc.tensor.matmul(acc[:, m], lhsT=identb[:], rhs=w1_p[q][:, :, n0 : n0 + 128].rearrange("p t n -> p n t"), start=True, stop=True)
+            w1_ps[q, g] = acc
+
+        def w1_leave(q, g):
+            nc.scalar.copy(out=w1_g[q][:, 256 * g : 256 * g + 256, :].rearrange("p n t -> p (n t)"), in_=w1_ps[q, g][:].rearrange("p m n t -> p (m n t)"))
 
         def w1_quant(q):
             nc.vector.quantize_mx(out=w1_c[q][:].bitcast(FP8X4), scales=w1_s[q][:], in_=w1_g[q][:].rearrange("p n t -> p (n t)"))
 
         x_c = keep.tile([P, P], U32, name="x_c", align_bytes=64)
         x_s = keep.tile([P, P], U8, name="x_s", align_bytes=64)
-        if ORDER == 1:
-            w1_widen(0)
-            w1_widen(1)
-        lay_w0(nc.vector.tensor_copy, 0, 0, W0_V)
-        lay_w0(nc.scalar.copy, 0, W0_V, 4)
-        nc.vector.quantize_mx(out=x_c[:].bitcast(FP8X4), scales=x_s[:], in_=xg[:].rearrange("p n t -> p (n t)"))
-        lay_w0(nc.vector.tensor_copy, 1, 0, W0B_V)
-        nc.vector.quantize_mx(out=w0_c[0][:].bitcast(FP8X4), scales=w0_s[0][:], in_=w0_g[0][:])
-        if ORDER == 2:
-            w1_widen(0)
-            w1_widen(1)
-        lay_w0(nc.scalar.copy, 1, W0B_V, 4)
-        nc.vector.quantize_mx(out=w0_c[1][:].bitcast(FP8X4), scales=w0_s[1][:], in_=w0_g[1][:])
+        xg = keep.tile([P, P, 4], BF16, name="xg", align_bytes=64)
+        xw = x_sb[:].bitcast(F32)
+        xt = psum.tile([P, 2, P], F32, name="xt", tag="mm")
+        for u in range(2):
+            nc.tensor.transpose(xt[:, u, :], xw[:, u:256:2], ident[:])
 
-        if ORDER == 0:
-            w1_widen(0)
-        else:
-            w1_widen(2)
-        w1_widen(3)
-        uv = []
-        for h in range(2):
+        def first_layer(h):
             acc = psum.tile([P, 4, P], F32, name="uv%d" % h, tag="mm")
             for t in range(4):
                 nc.tensor.matmul_mx(
@@ -140,41 +138,45 @@ def tile_graph_gan_pa_kernel(tc, x, fe_w0, fe_b0, fe_w1_bytes, fe_w1_scale, fe_b
                     start=True,
                     stop=True,
                 )
-            uv.append(acc)
+            return acc[:].rearrange("p t n -> p n t")
+
+        lay_w0(nc.vector.tensor_copy, 0, 0, W0_V)
+        lay_w0(nc.scalar.copy, 0, W0_V, 4)
+        nc.vector.tensor_copy(out=xg[:].rearrange("p n t -> p (n t)").bitcast(F32).rearrange("p (n u) -> p n u", u=2), in_=xt[:].rearrange("p u n -> p n u"))
+        nc.vector.quantize_mx(out=w0_c[0][:].bitcast(FP8X4), scales=w0_s[0][:], in_=w0_g[0][:])
+        nc.vector.quantize_mx(out=x_c[:].bitcast(FP8X4), scales=x_s[:], in_=xg[:].rearrange("p n t -> p (n t)"))
+        lay_w0(nc.vector.tensor_copy, 1, 0, W0B_V)
+        lay_w0(nc.scalar.copy, 1, W0B_V, 4)
+        u_ps = first_layer(0)
+        nc.vector.quantize_mx(out=w0_c[1][:].bitcast(FP8X4), scales=w0_s[1][:], in_=w0_g[1][:])
+        v_ps = first_layer(1)
         u_sb = keep.tile([P, P, 4], F32, name="u_sb")
         v_sb = keep.tile([P, P, 4], F32, name="v_sb")
-        nc.scalar.copy(out=u_sb[:], in_=uv[0][:].rearrange("p t n -> p n t"))
-        nc.vector.tensor_tensor(out=v_sb[:], in0=uv[1][:].rearrange("p t n -> p n t"), in1=b0_sb[:].unsqueeze(1).to_broadcast([P, P, 4]), op=ALU.add)
-        if ORDER == 0:
-            w1_widen(1)
-            w1_widen(2)
-        w1_lay(0)
+        nc.vector.tensor_tensor(out=u_sb[:], in0=u_ps, in1=b0_sb[:].unsqueeze(1).to_broadcast([P, P, 4]), op=ALU.add)
         b1_t = psum.tile([P, P], BF16, name="b1_t", tag="tp")
         nc.tensor.transpose(b1_t[:], b1_rows[:], identb[:])
         b1_a = keep.tile([P, 8], F32, name="b1_a")
-        nc.scalar.activation(out=b1_a[:], in_=b1_t[:, 0:8], func=ACT.Copy, scale=ALPHA)
-        w1_lay(1)
 
         zpre = {}
         e1 = {}
         codes = {}
 
-        def e1_add(k, g):
-            b, i0 = k // 2, 16 * (k % 2) + 8 * g
-            z = work.tile([P, 8, 32, 4], F32, name="zpre", tag="zpre", bufs=3)
+        def e1_add(k, g0, g1, v):
+            b, i0, ni = k // 2, 16 * (k % 2) + 8 * g0, 8 * (g1 - g0)
+            if g0 == 0:
+                zpre[k] = work.tile([P, 16, 32, 4], F32, name="zpre", tag="zpre")
             nc.vector.tensor_tensor(
-                out=z[:],
-                in0=u_sb[:, 32 * b + i0 : 32 * b + i0 + 8, :].unsqueeze(2).to_broadcast([P, 8, 32, 4]),
-                in1=v_sb[:, 32 * b : 32 * b + 32, :].unsqueeze(1).to_broadcast([P, 8, 32, 4]),
+                out=zpre[k][:, 8 * g0 : 8 * g1],
+                in0=u_sb[:, 32 * b + i0 : 32 * b + i0 + ni, :].unsqueeze(2).to_broadcast([P, ni, 32, 4]),
+                in1=v[:, 32 * b : 32 * b + 32, :].unsqueeze(1).to_broadcast([P, ni, 32, 4]),
                 op=ALU.add,
             )
-            zpre[k, g] = z
 
-        def e1_lrelu(k, g):
-            if g == 0:
+        def e1_lrelu(k, g0, g1):
+            if g0 == 0:
                 e1[k] = work.tile([P, 2048], BF16, name="e1", tag="e1", align_bytes=64)
-            z = zpre[k, g][:].rearrange("p i j t -> p (i j t)")
-            nc.vector.scalar_tensor_tensor(out=e1[k][:, 1024 * g : 1024 * g + 1024], in0=z, scalar=ALPHA, in1=z, op0=ALU.mult, op1=ALU.max)
+            z = zpre[k][:, 8 * g0 : 8 * g1].rearrange("p i j t -> p (i j t)")
+            nc.vector.scalar_tensor_tensor(out=e1[k][:, 1024 * g0 : 1024 * g1], in0=z, scalar=ALPHA, in1=z, op0=ALU.mult, op1=ALU.max)
 
         def e1_quant(k):
             c = work.tile([P, TOK], U32, name="e1_c", tag="e1_c", bufs=3, align_bytes=64)
@@ -185,7 +187,7 @@ def tile_graph_gan_pa_kernel(tc, x, fe_w0, fe_b0, fe_w1_bytes, fe_w1_scale, fe_b
         last = CHUNKS - 1
 
         def direct_tiles(k):
-            return 4 if k == last else D_PEN if k == last - 1 else D_FIRST if k == 0 else 1
+            return 4 if k == last else D_PEN if k == last - 1 else 0 if k < N_ZERO else 1
 
         rounds = []
         for k in range(CHUNKS):
@@ -215,8 +217,8 @@ def tile_graph_gan_pa_kernel(tc, x, fe_w0, fe_b0, fe_w1_bytes, fe_w1_scale, fe_b
             dst = rows[TOK * k : TOK * k + TOK, 512 * h + c0 : 512 * h + c1].rearrange("(s p) c -> p s c", p=P)
             nc.sync.dma_start(out=dst, in_=o_sb[k, h][:, :, c0:c1])
 
-        def products(r):
-            for k, c in rounds[r][0]:
+        def products(tiles):
+            for k, c in tiles:
                 m0 = 128 * (c % 4)
                 acc = psum.tile([P, TOK], F32, name="pt", tag="mm")
                 nc.tensor.matmul_mx(
@@ -229,8 +231,10 @@ def tile_graph_gan_pa_kernel(tc, x, fe_w0, fe_b0, fe_w1_bytes, fe_w1_scale, fe_b
                     stop=True,
                 )
                 pt[k, c] = acc
-            for k, s0, s1, n0 in rounds[r][1]:
-                acc = psum.tile([P, s1 - s0, 512 - n0], F32, name="p1", tag="mm")
+
+        def direct_products(parts, tag):
+            for k, s0, s1, n0 in parts:
+                acc = psum.tile([P, s1 - s0, 512 - n0], F32, name="p1", tag=tag)
                 for s in range(s0, s1):
                     nc.tensor.matmul_mx(
                         out=acc[:, s - s0, :],
@@ -291,50 +295,89 @@ def tile_graph_gan_pa_kernel(tc, x, fe_w0, fe_b0, fe_w1_bytes, fe_w1_scale, fe_b
             elif n0 == 256 and s1 == 4 and k >= FINE:
                 store(k, 1, 256, 512)
 
-        e1_add(0, 0)
-        e1_add(0, 1)
-        e1_lrelu(0, 0)
-        e1_lrelu(0, 1)
-        e1_add(1, 0)
-        e1_quant(0)
+        for t in range(4):
+            w1_widen(0, t)
+        w1_weave(0, 0)
+        w1_weave(0, 1)
+        e1_add(0, 0, 1, v_ps)
+        for t in range(4):
+            w1_widen(1, t)
+        nc.scalar.activation(out=b1_a[:], in_=b1_t[:, 0:8], func=ACT.Copy, scale=ALPHA)
+        w1_weave(1, 0)
+        w1_weave(1, 1)
+        e1_add(0, 1, 2, v_ps)
+        w1_leave(0, 0)
+        w1_leave(0, 1)
+        nc.scalar.copy(out=v_sb[:], in_=v_ps)
+        w1_leave(1, 0)
+        w1_leave(1, 1)
+        e1_lrelu(0, 0, 1)
+        e1_lrelu(0, 1, 2)
         w1_quant(0)
-        e1_add(1, 1)
-        products(0)
+        e1_quant(0)
+        e1_add(1, 0, 1, v_sb)
+        e1_add(1, 1, 2, v_sb)
+        if Q1_PRE:
+            w1_quant(1)
+        products(rounds[0][0])
 
         for r in range(nr + 1):
             k, h = divmod(r, 2)
             tiles, parts = rounds[r] if r < nr else ([], [])
             n = len(tiles)
-            if r > 0:
-                for i in range(len(rounds[r - 1][0])):
-                    turn(r - 1, i)
+            before = len(rounds[r - 1][0]) if r > 0 else 0
+            for i in range(before):
+                turn(r - 1, i)
             for i in range(n):
                 lin(r, i)
-            if r < nr and h == 0 and k < last:
-                e1_lrelu(k + 1, 0)
+            if r == nr:
+                pass
+            elif k == last:
+                if TAIL == 0:
+                    for part in parts:
+                        direct_add(*part)
+                    relu(r, 0, n)
+                    for part in parts:
+                        direct_lrelu(*part)
+                else:
+                    direct_add(*parts[0])
+                    direct_add(*parts[1])
+                    direct_lrelu(*parts[0])
+                    direct_store(*parts[0])
+                    relu(r, 0, n)
+                    direct_lrelu(*parts[1])
+            elif h == 0 and (r == 0 or not WIDE):
+                e1_lrelu(k + 1, 0, 1)
                 relu(r, 0, 2)
-                if r == 0:
+                if r == 0 and not Q1_PRE:
                     w1_quant(1)
-                e1_lrelu(k + 1, 1)
+                e1_lrelu(k + 1, 1, 2)
                 relu(r, 2, 4)
                 e1_quant(k + 1)
-            elif r < nr:
+            elif h == 0:
+                e1_lrelu(k + 1, 0, 2)
+                relu(r, 0, 4)
+                e1_quant(k + 1)
+            else:
                 for part in parts:
                     direct_add(*part)
                 if k + 2 <= last:
-                    e1_add(k + 2, 0)
-                if k == last:
+                    e1_add(k + 2, 0, 2 if WIDE else 1, v_sb)
+                if WIDE:
                     relu(r, 0, n)
                 for part in parts:
                     direct_lrelu(*part)
-                if k < last:
+                if not WIDE:
                     relu(r, 0, n)
-                if k + 2 <= last:
-                    e1_add(k + 2, 1)
+                    if k + 2 <= last:
+                        e1_add(k + 2, 1, 2, v_sb)
             if r + 1 < nr:
-                products(r + 1)
-            if r > 0:
-                for i in range(len(rounds[r - 1][0])):
-                    leave(r - 1, i)
-            for part in parts:
+                if TAIL and r + 1 >= nr - 2:
+                    direct_products(rounds[r + 1][1], "mm")
+                products(rounds[r + 1][0])
+                if not (TAIL and r + 1 >= nr - 2):
+                    direct_products(rounds[r + 1][1], "mm")
+            for i in range(before):
+                leave(r - 1, i)
+            for part in parts[1 if TAIL and k == last else 0:]:
                 direct_store(*part)

@@ -16,24 +16,27 @@ P = 128
 FLOPS = 2 * 128 * 512 * 512 * 2 + 2 * 4096 * 512 * 1024
 ALPHA = 0.2
 CHUNKS = 8
-W0_V = 2
-W0B_V = 2
-XAT = 1
-WIDE = 0
-NPS = 2
-FINE = 5
-VLEAVE = 0
-N_ZERO = 1
-Q1_PRE = 1
-TAIL = 1
-D_PEN = 2
-VWIDEN = 0
-TOK = 512
+PAIRS = 512
+W0_ON_VECTOR = 88
+I_SPLIT = 8
+TURN_BANKS = 4
+FINE_STORES_FROM = 5
+
+
+def direct_tiles(k):
+    if k == 0:
+        return 0
+    if k == CHUNKS - 1:
+        return 4
+    if k == CHUNKS - 2:
+        return 2
+    return 1
 
 
 def tile_graph_gan_pa_kernel(tc, x, fe_w0, fe_b0, fe_w1_bytes, fe_w1_scale, fe_b1, out):
     nc = tc.nc
     rows = out.rearrange("b i j c -> (b i j) c")
+    last = CHUNKS - 1
 
     with ExitStack() as ctx:
         keep = ctx.enter_context(tc.tile_pool(name="keep", bufs=1))
@@ -47,337 +50,291 @@ def tile_graph_gan_pa_kernel(tc, x, fe_w0, fe_b0, fe_w1_bytes, fe_w1_scale, fe_b
         w1_scale = keep.tile([P, 4], F32, name="w1_scale")
         b0_sb = keep.tile([P, 4], BF16, name="b0_sb")
         b1_rows = keep.tile([P, P], BF16, name="b1_rows")
-        b1_bc = keep.tile([P, 512], BF16, name="b1_bc")
+        b1_spread = keep.tile([P, 512], BF16, name="b1_spread")
+        w0_rows = fe_w0.rearrange("(h p t) w -> h p t w", h=2, t=4)
         w1_rows = fe_w1_bytes.rearrange("(p t) n -> p (t n)", t=4)
-
-        def load_w0(h):
-            nc.sync.dma_start(out=w0_raw[h][:], in_=fe_w0[512 * h : 512 * h + 512, :].rearrange("(p j) w -> p j w", j=4))
-
-        def load_w1(g):
+        nc.sync.dma_start(out=w0_raw[0][:], in_=w0_rows[0])
+        nc.sync.dma_start(out=x_sb[:], in_=x.rearrange("b n d -> (b n) d"))
+        nc.sync.dma_start(out=w0_raw[1][:], in_=w0_rows[1])
+        for g in range(2):
             nc.sync.dma_start(out=w1_bytes[g][:], in_=w1_rows[:, 2048 * g : 2048 * g + 2048])
-
-        load_w0(0)
-        if XAT == 1:
-            nc.sync.dma_start(out=x_sb[:], in_=x.rearrange("b n d -> (b n) d"))
-        load_w0(1)
-        if XAT == 2:
-            nc.sync.dma_start(out=x_sb[:], in_=x.rearrange("b n d -> (b n) d"))
-        load_w1(0)
-        load_w1(1)
         nc.scalar.dma_start(out=w1_scale[:], in_=fe_w1_scale.rearrange("(p t) o -> p (t o)", t=4))
         nc.scalar.dma_start(out=b0_sb[:], in_=fe_b0.rearrange("(p t) -> p t", t=4))
 
         ident = keep.tile([P, P], F32, name="ident")
-        identb = keep.tile([P, P], BF16, name="identb")
-        warm = keep.tile([P, 8], F32, name="warm")
-        nc.gpsimd.memset(warm[:], 0.0)
-        nc.gpsimd.memset(b1_rows[:], 0.0)
+        ident_bf = keep.tile([P, P], BF16, name="ident_bf")
         make_identity(nc, ident[:])
-        make_identity(nc, identb[:])
+        nc.vector.memset(b1_rows[:], 0.0)
         nc.sync.dma_start(out=b1_rows[0:8, :], in_=fe_b1.rearrange("(c m) -> c m", m=P))
-        nc.sync.dma_start(out=b1_bc[:], in_=fe_b1[512:1024].partition_broadcast(P))
-        nc.scalar.activation(out=warm[:], in_=warm[:], func=ACT.Identity, bias=0.0, scale=1.0)
+        nc.sync.dma_start(out=b1_spread[:], in_=fe_b1[512:1024].partition_broadcast(P))
+        nc.scalar.activation(out=ident_bf[:], in_=ident[:], func=ACT.Copy)
 
-        w0_g = [keep.tile([P, 2048], BF16, name="w0_g%d" % h, align_bytes=64) for h in range(2)]
-        w0_c = [keep.tile([P, 512], U32, name="w0_c%d" % h, align_bytes=64) for h in range(2)]
-        w0_s = [keep.tile([P, 512], U8, name="w0_s%d" % h, align_bytes=64) for h in range(2)]
+        def quantise(codes, scales, values):
+            nc.vector.quantize_mx(out=codes.bitcast(FP8X4), scales=scales, in_=values)
 
-        def lay_w0(copy, h, t0, t1):
-            if t1 > t0:
-                copy(
-                    out=w0_g[h][:].rearrange("p (t m j) -> p t m j", t=4, j=4)[:, t0:t1],
-                    in_=w0_raw[h][:].rearrange("p j (m t) -> p t m j", t=4)[:, t0:t1],
-                )
-
-        w1_p = [keep.tile([P, 4, 512], BF16, name="w1_p%d" % q, align_bytes=64) for q in range(2)]
-        w1_g = [keep.tile([P, 512, 4], BF16, name="w1_g%d" % q, align_bytes=64) for q in range(2)]
-        w1_c = [keep.tile([P, 512], U32, name="w1_c%d" % q, align_bytes=64) for q in range(2)]
-        w1_s = [keep.tile([P, 512], U8, name="w1_s%d" % q, align_bytes=64) for q in range(2)]
-
-        def w1_widen(q, t):
-            n0 = 1024 * (t % 2) + 512 * q
-            src = w1_bytes[t // 2][:, n0 : n0 + 512].bitcast(FP8)
-            dst = w1_p[q][:, t, :]
-            if 4 * q + t >= 8 - VWIDEN:
-                nc.vector.tensor_scalar(out=dst, in0=src, scalar1=w1_scale[:, t : t + 1], scalar2=None, op0=ALU.mult)
-            else:
-                nc.scalar.activation(out=dst, in_=src, func=ACT.Copy, scale=w1_scale[:, t : t + 1])
-
-        w1_ps = {}
-
-        def w1_weave(q, g):
-            acc = psum.tile([P, 2, 128, 4], BF16, name="w1_ps", tag="tp")
-            for m in range(2):
-                n0 = 256 * g + 128 * m
-                nc.tensor.matmul(acc[:, m], lhsT=identb[:], rhs=w1_p[q][:, :, n0 : n0 + 128].rearrange("p t n -> p n t"), start=True, stop=True)
-            w1_ps[q, g] = acc
-
-        def w1_leave(q, g):
-            nc.scalar.copy(out=w1_g[q][:, 256 * g : 256 * g + 256, :].rearrange("p n t -> p (n t)"), in_=w1_ps[q, g][:].rearrange("p m n t -> p (m n t)"))
-
-        def w1_quant(q):
-            nc.vector.quantize_mx(out=w1_c[q][:].bitcast(FP8X4), scales=w1_s[q][:], in_=w1_g[q][:].rearrange("p n t -> p (n t)"))
-
-        x_c = keep.tile([P, P], U32, name="x_c", align_bytes=64)
-        x_s = keep.tile([P, P], U8, name="x_s", align_bytes=64)
-        xg = keep.tile([P, P, 4], BF16, name="xg", align_bytes=64)
-        xw = x_sb[:].bitcast(F32)
-        xt = psum.tile([P, 2, P], F32, name="xt", tag="mm")
-        for u in range(2):
-            nc.tensor.transpose(xt[:, u, :], xw[:, u:256:2], ident[:])
-
-        def first_layer(h):
-            acc = psum.tile([P, 4, P], F32, name="uv%d" % h, tag="mm")
-            for t in range(4):
-                nc.tensor.matmul_mx(
-                    out=acc[:, t, :],
-                    lhsT=w0_c[h][:, 128 * t : 128 * t + 128].bitcast(FP8X4),
-                    lhsT_scale=w0_s[h][:, 128 * t : 128 * t + 128],
-                    rhs=x_c[:].bitcast(FP8X4),
-                    rhs_scale=x_s[:],
-                    start=True,
-                    stop=True,
-                )
-            return acc[:].rearrange("p t n -> p n t")
-
-        lay_w0(nc.vector.tensor_copy, 0, 0, W0_V)
-        lay_w0(nc.scalar.copy, 0, W0_V, 4)
-        nc.vector.tensor_copy(out=xg[:].rearrange("p n t -> p (n t)").bitcast(F32).rearrange("p (n u) -> p n u", u=2), in_=xt[:].rearrange("p u n -> p n u"))
-        nc.vector.quantize_mx(out=w0_c[0][:].bitcast(FP8X4), scales=w0_s[0][:], in_=w0_g[0][:])
-        nc.vector.quantize_mx(out=x_c[:].bitcast(FP8X4), scales=x_s[:], in_=xg[:].rearrange("p n t -> p (n t)"))
-        lay_w0(nc.vector.tensor_copy, 1, 0, W0B_V)
-        lay_w0(nc.scalar.copy, 1, W0B_V, 4)
-        u_ps = first_layer(0)
-        nc.vector.quantize_mx(out=w0_c[1][:].bitcast(FP8X4), scales=w0_s[1][:], in_=w0_g[1][:])
-        v_ps = first_layer(1)
-        u_sb = keep.tile([P, P, 4], F32, name="u_sb")
-        v_sb = keep.tile([P, P, 4], F32, name="v_sb")
-        nc.vector.tensor_tensor(out=u_sb[:], in0=u_ps, in1=b0_sb[:].unsqueeze(1).to_broadcast([P, P, 4]), op=ALU.add)
-        b1_t = psum.tile([P, P], BF16, name="b1_t", tag="tp")
-        nc.tensor.transpose(b1_t[:], b1_rows[:], identb[:])
-        b1_a = keep.tile([P, 8], F32, name="b1_a")
-
-        zpre = {}
-        e1 = {}
-        codes = {}
-
-        def e1_add(k, g0, g1, v):
-            b, i0, ni = k // 2, 16 * (k % 2) + 8 * g0, 8 * (g1 - g0)
-            if g0 == 0:
-                zpre[k] = work.tile([P, 16, 32, 4], F32, name="zpre", tag="zpre")
-            nc.vector.tensor_tensor(
-                out=zpre[k][:, 8 * g0 : 8 * g1],
-                in0=u_sb[:, 32 * b + i0 : 32 * b + i0 + ni, :].unsqueeze(2).to_broadcast([P, ni, 32, 4]),
-                in1=v[:, 32 * b : 32 * b + 32, :].unsqueeze(1).to_broadcast([P, ni, 32, 4]),
-                op=ALU.add,
+        def product(acc, lhs, lhs_cols, rhs, rhs_cols):
+            nc.tensor.matmul_mx(
+                out=acc,
+                lhsT=lhs[0][:, lhs_cols].bitcast(FP8X4),
+                lhsT_scale=lhs[1][:, lhs_cols],
+                rhs=rhs[0][:, rhs_cols].bitcast(FP8X4),
+                rhs_scale=rhs[1][:, rhs_cols],
+                start=True,
+                stop=True,
             )
 
-        def e1_lrelu(k, g0, g1):
-            if g0 == 0:
-                e1[k] = work.tile([P, 2048], BF16, name="e1", tag="e1", align_bytes=64)
-            z = zpre[k][:, 8 * g0 : 8 * g1].rearrange("p i j t -> p (i j t)")
-            nc.vector.scalar_tensor_tensor(out=e1[k][:, 1024 * g0 : 1024 * g1], in0=z, scalar=ALPHA, in1=z, op0=ALU.mult, op1=ALU.max)
+        def mx_operand(pool, name, width, bufs):
+            codes = pool.tile([P, width], U32, name=name + "_codes", bufs=bufs, align_bytes=64)
+            scales = pool.tile([P, width], U8, name=name + "_scales", bufs=bufs, align_bytes=64)
+            return codes, scales
 
-        def e1_quant(k):
-            c = work.tile([P, TOK], U32, name="e1_c", tag="e1_c", bufs=3, align_bytes=64)
-            s = work.tile([P, TOK], U8, name="e1_s", tag="e1_s", bufs=3, align_bytes=64)
-            nc.vector.quantize_mx(out=c[:].bitcast(FP8X4), scales=s[:], in_=e1[k][:])
-            codes[k] = (c, s)
+        x_words = x_sb[:].bitcast(F32)
+        x_turned = psum.tile([P, 2, P], F32, name="x_turned", tag="product")
+        for u in range(2):
+            nc.tensor.transpose(x_turned[:, u, :], x_words[:, u:256:2], ident[:])
+        x_laid = keep.tile([P, 4 * P], BF16, name="x_laid", align_bytes=64)
+        x_mx = mx_operand(keep, "x", P, 1)
+        w0_laid = [keep.tile([P, 2048], BF16, name="w0_laid%d" % h, align_bytes=64) for h in range(2)]
+        w0_mx = [mx_operand(keep, "w0_%d" % h, 512, 1) for h in range(2)]
 
-        last = CHUNKS - 1
+        def w0_lay(h):
+            dst = w0_laid[h][:].rearrange("p (t m j) -> p t m j", t=4, j=4)
+            src = w0_raw[h][:].rearrange("p j (m t) -> p t m j", t=4)
+            nc.vector.tensor_copy(out=dst[:, :, 0:W0_ON_VECTOR], in_=src[:, :, 0:W0_ON_VECTOR])
+            nc.scalar.copy(out=dst[:, :, W0_ON_VECTOR:128], in_=src[:, :, W0_ON_VECTOR:128])
 
-        def direct_tiles(k):
-            return 4 if k == last else D_PEN if k == last - 1 else 0 if k < N_ZERO else 1
+        def first_layer(h, tag, bufs):
+            acc = psum.tile([P, 4, P], F32, name="first%d" % h, tag=tag, bufs=bufs)
+            for t in range(4):
+                product(acc[:, t, :], w0_mx[h], slice(128 * t, 128 * t + 128), x_mx, slice(0, P))
+            return acc[:].rearrange("p t n -> p n t")
+
+        w0_lay(0)
+        nc.vector.tensor_copy(out=x_laid[:].bitcast(F32).rearrange("p (n u) -> p n u", u=2), in_=x_turned[:].rearrange("p u n -> p n u"))
+        quantise(w0_mx[0][0][:], w0_mx[0][1][:], w0_laid[0][:])
+        quantise(x_mx[0][:], x_mx[1][:], x_laid[:])
+        w0_lay(1)
+        u_psum = first_layer(0, "product", 4)
+        quantise(w0_mx[1][0][:], w0_mx[1][1][:], w0_laid[1][:])
+        v_psum = first_layer(1, "product", 4)
+        u_sb = keep.tile([P, P, 4], F32, name="u_sb")
+        v_sb = keep.tile([P, P, 4], F32, name="v_sb")
+        nc.vector.tensor_tensor(out=u_sb[:], in0=u_psum, in1=b0_sb[:].unsqueeze(1).to_broadcast([P, P, 4]), op=ALU.add)
+        b1_turned = psum.tile([P, P], BF16, name="b1_turned", tag="turned", bufs=TURN_BANKS)
+        nc.tensor.transpose(b1_turned[:], b1_rows[:], ident_bf[:])
+        b1_fifth = keep.tile([P, 8], F32, name="b1_fifth")
+
+        w1_planes = [keep.tile([P, 4, 512], BF16, name="w1_planes%d" % q, align_bytes=64) for q in range(2)]
+        w1_laid = [keep.tile([P, 512, 4], BF16, name="w1_laid%d" % q, align_bytes=64) for q in range(2)]
+        w1_mx = [mx_operand(keep, "w1_%d" % q, 512, 1) for q in range(2)]
+        w1_woven = {}
+
+        def w1_widen(q):
+            for t in range(4):
+                n0 = 1024 * (t % 2) + 512 * q
+                nc.scalar.activation(out=w1_planes[q][:, t, :], in_=w1_bytes[t // 2][:, n0 : n0 + 512].bitcast(FP8), func=ACT.Copy, scale=w1_scale[:, t : t + 1])
+
+        def w1_weave(q, g):
+            acc = psum.tile([P, 2, 128, 4], BF16, name="w1_woven", tag="turned", bufs=TURN_BANKS)
+            for m in range(2):
+                n0 = 256 * g + 128 * m
+                nc.tensor.matmul(acc[:, m], lhsT=ident_bf[:], rhs=w1_planes[q][:, :, n0 : n0 + 128].rearrange("p t n -> p n t"), start=True, stop=True)
+            w1_woven[q, g] = acc
+
+        def w1_leave(q, g):
+            nc.scalar.copy(out=w1_laid[q][:, 256 * g : 256 * g + 256, :].rearrange("p n t -> p (n t)"), in_=w1_woven[q, g][:].rearrange("p m n t -> p (m n t)"))
+
+        def w1_lay(q, g):
+            cols = slice(256 * g, 256 * g + 256)
+            nc.scalar.copy(out=w1_laid[q][:, cols, :].rearrange("p (c i) t -> p c t i", i=4), in_=w1_planes[q][:, :, cols].rearrange("p t (c i) -> p c t i", i=4))
+
+        def w1_quantise(q):
+            quantise(w1_mx[q][0][:], w1_mx[q][1][:], w1_laid[q][:].rearrange("p n t -> p (n t)"))
+
+        i_ranges = [(0, I_SPLIT), (I_SPLIT, 16)]
+        pair_sums = {}
+        e1 = {}
+        e1_mx = {}
+
+        def e1_add(k, g, v):
+            i0, i1 = i_ranges[g]
+            graph, ni = k // 2, i1 - i0
+            n0 = 32 * graph + 16 * (k % 2) + i0
+            z = work.tile([P, ni, 32, 4], F32, name="pair_sums%d" % g)
+            nc.vector.tensor_tensor(
+                out=z[:],
+                in0=u_sb[:, n0 : n0 + ni, :].unsqueeze(2).to_broadcast([P, ni, 32, 4]),
+                in1=v[:, 32 * graph : 32 * graph + 32, :].unsqueeze(1).to_broadcast([P, ni, 32, 4]),
+                op=ALU.add,
+            )
+            pair_sums[k, g] = z
+
+        def e1_lrelu(k, g):
+            i0, i1 = i_ranges[g]
+            if g == 0:
+                e1[k] = work.tile([P, 4 * PAIRS], BF16, name="e1", align_bytes=64)
+            z = pair_sums[k, g][:].rearrange("p i j t -> p (i j t)")
+            nc.vector.scalar_tensor_tensor(out=e1[k][:, 128 * i0 : 128 * i1], in0=z, scalar=ALPHA, in1=z, op0=ALU.mult, op1=ALU.max)
+
+        def e1_quantise(k):
+            e1_mx[k] = mx_operand(work, "e1", PAIRS, 3)
+            quantise(e1_mx[k][0][:], e1_mx[k][1][:], e1[k][:])
 
         rounds = []
         for k in range(CHUNKS):
             nd = direct_tiles(k)
-            parts = [(k, s * (4 // nd), (s + 1) * (4 // nd), 512 - 128 * nd) for s in range(nd)]
+            parts = [(k, m * 4 // nd, (m + 1) * 4 // nd, 512 - 128 * nd) for m in range(nd)]
             if k < last:
                 rounds.append(([(k, c) for c in range(4)], []))
                 rounds.append(([(k, c) for c in range(4, 8 - nd)], parts))
             else:
                 rounds.append(([(k, 0), (k, 1)], parts[0:2]))
                 rounds.append(([(k, 2), (k, 3)], parts[2:4]))
-        nr = len(rounds)
-        pt = {}
-        at = {}
-        rt = {}
-        tp = {}
-        o_sb = {}
-        p1 = {}
-        zp = {}
+        n_rounds = len(rounds)
+        tile_psum = {}
+        part_psum = {}
+        a_sb = {}
+        r_sb = {}
+        turned = {}
+        part_sums = {}
+        out_sb = {}
 
-        def out_tile(k, h):
-            if (k, h) not in o_sb:
-                o_sb[k, h] = work.tile([P, 4, 512], F32, name="o_sb", tag="o_sb", bufs=4)
-            return o_sb[k, h]
+        def out_half(k, h):
+            if (k, h) not in out_sb:
+                out_sb[k, h] = work.tile([P, 4, 512], F32, name="out_sb", bufs=4)
+            return out_sb[k, h]
 
-        def store(k, h, c0, c1):
-            dst = rows[TOK * k : TOK * k + TOK, 512 * h + c0 : 512 * h + c1].rearrange("(s p) c -> p s c", p=P)
-            nc.sync.dma_start(out=dst, in_=o_sb[k, h][:, :, c0:c1])
+        def store_columns(k, h, c0, c1):
+            dst = rows[PAIRS * k : PAIRS * k + PAIRS, 512 * h + c0 : 512 * h + c1].rearrange("(s p) c -> p s c", p=P)
+            nc.sync.dma_start(out=dst, in_=out_sb[k, h][:, :, c0:c1])
 
-        def products(tiles):
-            for k, c in tiles:
-                m0 = 128 * (c % 4)
-                acc = psum.tile([P, TOK], F32, name="pt", tag="mm")
-                nc.tensor.matmul_mx(
-                    out=acc[:],
-                    lhsT=w1_c[c // 4][:, m0 : m0 + 128].bitcast(FP8X4),
-                    lhsT_scale=w1_s[c // 4][:, m0 : m0 + 128],
-                    rhs=codes[k][0][:].bitcast(FP8X4),
-                    rhs_scale=codes[k][1][:],
-                    start=True,
-                    stop=True,
-                )
-                pt[k, c] = acc
+        def tile_products(r):
+            for k, c in rounds[r][0]:
+                acc = psum.tile([P, PAIRS], F32, name="tile_psum", tag="product")
+                product(acc[:], w1_mx[c // 4], slice(128 * (c % 4), 128 * (c % 4) + 128), e1_mx[k], slice(0, PAIRS))
+                tile_psum[k, c] = acc
 
-        def direct_products(parts, tag):
-            for k, s0, s1, n0 in parts:
-                acc = psum.tile([P, s1 - s0, 512 - n0], F32, name="p1", tag=tag)
+        def part_products(r):
+            for k, s0, s1, n0 in rounds[r][1]:
+                acc = psum.tile([P, s1 - s0, 512 - n0], F32, name="part_psum", tag="product")
                 for s in range(s0, s1):
-                    nc.tensor.matmul_mx(
-                        out=acc[:, s - s0, :],
-                        lhsT=codes[k][0][:, 128 * s : 128 * s + 128].bitcast(FP8X4),
-                        lhsT_scale=codes[k][1][:, 128 * s : 128 * s + 128],
-                        rhs=w1_c[1][:, n0:512].bitcast(FP8X4),
-                        rhs_scale=w1_s[1][:, n0:512],
-                        start=True,
-                        stop=True,
-                    )
-                p1[k, s0] = acc
+                    product(acc[:, s - s0, :], e1_mx[k], slice(128 * s, 128 * s + 128), w1_mx[1], slice(n0, 512))
+                part_psum[k, s0] = acc
 
-        def lin(r, i):
-            if i == 0:
-                at[r] = work.tile([P, 4, TOK], F32, name="at", tag="at", bufs=3)
-                rt[r] = work.tile([P, 4, TOK], F32, name="rt", tag="rt", bufs=3)
-            k, c = rounds[r][0][i]
-            nc.scalar.activation(out=at[r][:, i, :], in_=pt[k, c][:], func=ACT.Identity, bias=b1_a[:, c : c + 1], scale=ALPHA)
+        def affine(r):
+            a_sb[r] = work.tile([P, 4, PAIRS], F32, name="a_sb", bufs=3)
+            r_sb[r] = work.tile([P, 4, PAIRS], F32, name="r_sb", bufs=3)
+            for i, (k, c) in enumerate(rounds[r][0]):
+                nc.scalar.activation(out=a_sb[r][:, i, :], in_=tile_psum[k, c][:], func=ACT.Identity, bias=b1_fifth[:, c : c + 1], scale=ALPHA)
 
-        def relu(r, i0, i1):
-            nc.vector.tensor_scalar(out=rt[r][:, i0:i1, :], in0=at[r][:, i0:i1, :], scalar1=4.0, scalar2=0.0, op0=ALU.mult, op1=ALU.max)
+        def relu(engine, r, i0, i1):
+            engine.tensor_scalar(out=r_sb[r][:, i0:i1, :], in0=a_sb[r][:, i0:i1, :], scalar1=4.0, scalar2=0.0, op0=ALU.mult, op1=ALU.max)
 
         def turn(r, i):
-            acc = psum.tile([P, 4, P], F32, name="tp", tag="tp")
+            acc = psum.tile([P, 4, P], F32, name="turned", tag="turned", bufs=TURN_BANKS)
             for s in range(4):
-                for n, src in enumerate((at[r], rt[r])):
+                for n, src in enumerate((a_sb[r], r_sb[r])):
                     nc.tensor.matmul(acc[:, s, :], lhsT=src[:, i, 128 * s : 128 * s + 128], rhs=ident[:], is_transpose=True, start=(n == 0), stop=(n == 1))
-            tp[r, i] = acc
+            turned[r, i] = acc
 
         def leave(r, i):
             k, c = rounds[r][0][i]
-            m0 = 128 * (c % 4)
-            copy = nc.vector.tensor_copy if r == nr - 1 and i < VLEAVE else nc.scalar.copy
-            copy(out=out_tile(k, c // 4)[:, :, m0 : m0 + 128], in_=tp[r, i][:])
-            if k == last and c >= 2:
-                store(k, 0, m0, m0 + 128)
-            elif k >= FINE:
-                if c % 2 == 1:
-                    store(k, c // 4, m0 - 128, m0 + 128)
-                elif c == 6:
-                    store(k, 1, 256, 512)
-            elif c == 3 or c == 7 - direct_tiles(k):
-                store(k, c // 4, 0, 512)
+            h, c0 = c // 4, 128 * (c % 4)
+            nc.scalar.copy(out=out_half(k, h)[:, :, c0 : c0 + 128], in_=turned[r, i][:])
+            closes_round = i == len(rounds[r][0]) - 1
+            if r == n_rounds - 1:
+                store_columns(k, h, c0, c0 + 128)
+            elif k < FINE_STORES_FROM:
+                if closes_round:
+                    store_columns(k, h, 0, 512)
+            elif c % 2 == 1:
+                store_columns(k, h, c0 - 128, c0 + 128)
+            elif closes_round:
+                store_columns(k, h, c0, 512)
 
-        def direct_add(k, s0, s1, n0):
-            z = work.tile([P, s1 - s0, 512 - n0], F32, name="zp", tag="zp")
-            nc.vector.tensor_tensor(out=z[:], in0=p1[k, s0][:], in1=b1_bc[:, n0:512].unsqueeze(1).to_broadcast([P, s1 - s0, 512 - n0]), op=ALU.add)
-            zp[k, s0] = z
+        def part_add(k, s0, s1, n0):
+            shape = [P, s1 - s0, 512 - n0]
+            z = work.tile(shape, F32, name="part_sums")
+            nc.vector.tensor_tensor(out=z[:], in0=part_psum[k, s0][:], in1=b1_spread[:, n0:512].unsqueeze(1).to_broadcast(shape), op=ALU.add)
+            part_sums[k, s0] = z
 
-        def direct_lrelu(k, s0, s1, n0):
-            z = zp[k, s0][:]
-            nc.vector.scalar_tensor_tensor(out=out_tile(k, 1)[:, s0:s1, n0:512], in0=z, scalar=ALPHA, in1=z, op0=ALU.mult, op1=ALU.max)
+        def part_lrelu(k, s0, s1, n0):
+            z = part_sums[k, s0][:]
+            nc.vector.scalar_tensor_tensor(out=out_half(k, 1)[:, s0:s1, n0:512], in0=z, scalar=ALPHA, in1=z, op0=ALU.mult, op1=ALU.max)
 
-        def direct_store(k, s0, s1, n0):
+        def part_store(k, s0, s1, n0):
             if k == last:
-                r0 = TOK * k + 128 * s0
-                nc.sync.dma_start(out=rows[r0 : r0 + 128, 512:1024], in_=o_sb[k, 1][:, s0, :])
-            elif n0 == 256 and s1 == 4 and k >= FINE:
-                store(k, 1, 256, 512)
+                r0 = PAIRS * k + 128 * s0
+                nc.sync.dma_start(out=rows[r0 : r0 + 128, 512:1024], in_=out_sb[k, 1][:, s0, :])
+            elif k >= FINE_STORES_FROM and n0 == 256 and s1 == 4:
+                store_columns(k, 1, n0, 512)
 
-        for t in range(4):
-            w1_widen(0, t)
+        w1_widen(0)
         w1_weave(0, 0)
         w1_weave(0, 1)
-        e1_add(0, 0, 1, v_ps)
-        for t in range(4):
-            w1_widen(1, t)
-        nc.scalar.activation(out=b1_a[:], in_=b1_t[:, 0:8], func=ACT.Copy, scale=ALPHA)
+        e1_add(0, 0, v_psum)
+        w1_widen(1)
+        nc.scalar.activation(out=b1_fifth[:], in_=b1_turned[:, 0:8], func=ACT.Copy, scale=ALPHA)
         w1_weave(1, 0)
-        w1_weave(1, 1)
-        e1_add(0, 1, 2, v_ps)
+        e1_add(0, 1, v_psum)
         w1_leave(0, 0)
         w1_leave(0, 1)
-        nc.scalar.copy(out=v_sb[:], in_=v_ps)
+        nc.scalar.copy(out=v_sb[:], in_=v_psum)
+        w1_lay(1, 1)
         w1_leave(1, 0)
-        w1_leave(1, 1)
-        e1_lrelu(0, 0, 1)
-        e1_lrelu(0, 1, 2)
-        w1_quant(0)
-        e1_quant(0)
-        e1_add(1, 0, 1, v_sb)
-        e1_add(1, 1, 2, v_sb)
-        if Q1_PRE:
-            w1_quant(1)
-        products(rounds[0][0])
+        e1_lrelu(0, 0)
+        e1_lrelu(0, 1)
+        w1_quantise(0)
+        e1_quantise(0)
+        e1_add(1, 0, v_sb)
+        e1_add(1, 1, v_sb)
+        w1_quantise(1)
+        tile_products(0)
 
-        for r in range(nr + 1):
-            k, h = divmod(r, 2)
-            tiles, parts = rounds[r] if r < nr else ([], [])
-            n = len(tiles)
+        for r in range(n_rounds + 1):
+            k, second = divmod(r, 2)
             before = len(rounds[r - 1][0]) if r > 0 else 0
             for i in range(before):
                 turn(r - 1, i)
-            for i in range(n):
-                lin(r, i)
-            if r == nr:
-                pass
-            elif k == last:
-                if TAIL == 0:
-                    for part in parts:
-                        direct_add(*part)
-                    relu(r, 0, n)
-                    for part in parts:
-                        direct_lrelu(*part)
-                else:
-                    direct_add(*parts[0])
-                    direct_add(*parts[1])
-                    direct_lrelu(*parts[0])
-                    direct_store(*parts[0])
-                    relu(r, 0, n)
-                    direct_lrelu(*parts[1])
-            elif h == 0 and (r == 0 or not WIDE):
-                e1_lrelu(k + 1, 0, 1)
-                relu(r, 0, 2)
-                if r == 0 and not Q1_PRE:
-                    w1_quant(1)
-                e1_lrelu(k + 1, 1, 2)
-                relu(r, 2, 4)
-                e1_quant(k + 1)
-            elif h == 0:
-                e1_lrelu(k + 1, 0, 2)
-                relu(r, 0, 4)
-                e1_quant(k + 1)
-            else:
+            tiles, parts = rounds[r] if r < n_rounds else ([], [])
+            unstored = parts
+            if r < n_rounds:
+                affine(r)
+            if k < last and not second:
+                e1_lrelu(k + 1, 0)
+                relu(nc.vector, r, 0, 2)
+                e1_lrelu(k + 1, 1)
+                relu(nc.vector, r, 2, 4)
+                e1_quantise(k + 1)
+            elif k < last - 1:
                 for part in parts:
-                    direct_add(*part)
-                if k + 2 <= last:
-                    e1_add(k + 2, 0, 2 if WIDE else 1, v_sb)
-                if WIDE:
-                    relu(r, 0, n)
+                    part_add(*part)
+                e1_add(k + 2, 0, v_sb)
                 for part in parts:
-                    direct_lrelu(*part)
-                if not WIDE:
-                    relu(r, 0, n)
-                    if k + 2 <= last:
-                        e1_add(k + 2, 1, 2, v_sb)
-            if r + 1 < nr:
-                if TAIL and r + 1 >= nr - 2:
-                    direct_products(rounds[r + 1][1], "mm")
-                products(rounds[r + 1][0])
-                if not (TAIL and r + 1 >= nr - 2):
-                    direct_products(rounds[r + 1][1], "mm")
+                    part_lrelu(*part)
+                relu(nc.vector, r, 0, len(tiles))
+                e1_add(k + 2, 1, v_sb)
+            elif r == n_rounds - 2:
+                part_add(*parts[0])
+                part_add(*parts[1])
+                part_lrelu(*parts[0])
+                part_store(*parts[0])
+                relu(nc.vector, r, 0, 2)
+                part_lrelu(*parts[1])
+                unstored = parts[1:]
+            elif r < n_rounds:
+                part_add(*parts[0])
+                part_add(*parts[1])
+                relu(nc.vector, r, 0, 2)
+                part_lrelu(*parts[0])
+                part_lrelu(*parts[1])
+            if r + 1 < n_rounds - 2:
+                tile_products(r + 1)
+                part_products(r + 1)
+            elif r + 1 < n_rounds:
+                part_products(r + 1)
+                tile_products(r + 1)
             for i in range(before):
                 leave(r - 1, i)
-            for part in parts[1 if TAIL and k == last else 0:]:
-                direct_store(*part)
+            for part in unstored:
+                part_store(*part)

@@ -17,26 +17,14 @@ FLOPS = 2 * 128 * 512 * 512 * 2 + 2 * 4096 * 512 * 1024
 ALPHA = 0.2
 CHUNKS = 8
 PAIRS = 512
-W0_ON_VECTOR = 88
-I_SPLIT = 8
-TURN_BANKS = 4
-FINE_STORES_FROM = 5
-
-
-def direct_tiles(k):
-    if k == 0:
-        return 0
-    if k == CHUNKS - 1:
-        return 4
-    if k == CHUNKS - 2:
-        return 2
-    return 1
+DIRECT_FROM = 1
+OUT_BUFFERS = 11
+HALF_DIRECT_FROM = 2 * CHUNKS - 3
 
 
 def tile_graph_gan_pa_kernel(tc, x, fe_w0, fe_b0, fe_w1_bytes, fe_w1_scale, fe_b1, out):
     nc = tc.nc
     rows = out.rearrange("b i j c -> (b i j) c")
-    last = CHUNKS - 1
 
     with ExitStack() as ctx:
         keep = ctx.enter_context(tc.tile_pool(name="keep", bufs=1))
@@ -50,7 +38,7 @@ def tile_graph_gan_pa_kernel(tc, x, fe_w0, fe_b0, fe_w1_bytes, fe_w1_scale, fe_b
         w1_scale = keep.tile([P, 4], F32, name="w1_scale")
         b0_sb = keep.tile([P, 4], BF16, name="b0_sb")
         b1_rows = keep.tile([P, P], BF16, name="b1_rows")
-        b1_spread = keep.tile([P, 512], BF16, name="b1_spread")
+        b1_spread = keep.tile([P, 1024], BF16, name="b1_spread")
         w0_rows = fe_w0.rearrange("(h p t) w -> h p t w", h=2, t=4)
         w1_rows = fe_w1_bytes.rearrange("(p t) n -> p (t n)", t=4)
         nc.sync.dma_start(out=w0_raw[0][:], in_=w0_rows[0])
@@ -66,7 +54,7 @@ def tile_graph_gan_pa_kernel(tc, x, fe_w0, fe_b0, fe_w1_bytes, fe_w1_scale, fe_b
         make_identity(nc, ident[:])
         nc.vector.memset(b1_rows[:], 0.0)
         nc.sync.dma_start(out=b1_rows[0:8, :], in_=fe_b1.rearrange("(c m) -> c m", m=P))
-        nc.sync.dma_start(out=b1_spread[:], in_=fe_b1[512:1024].partition_broadcast(P))
+        nc.sync.dma_start(out=b1_spread[:], in_=fe_b1.partition_broadcast(P))
         nc.scalar.activation(out=ident_bf[:], in_=ident[:], func=ACT.Copy)
 
         def quantise(codes, scales, values):
@@ -100,11 +88,11 @@ def tile_graph_gan_pa_kernel(tc, x, fe_w0, fe_b0, fe_w1_bytes, fe_w1_scale, fe_b
         def w0_lay(h):
             dst = w0_laid[h][:].rearrange("p (t m j) -> p t m j", t=4, j=4)
             src = w0_raw[h][:].rearrange("p j (m t) -> p t m j", t=4)
-            nc.vector.tensor_copy(out=dst[:, :, 0:W0_ON_VECTOR], in_=src[:, :, 0:W0_ON_VECTOR])
-            nc.scalar.copy(out=dst[:, :, W0_ON_VECTOR:128], in_=src[:, :, W0_ON_VECTOR:128])
+            nc.vector.tensor_copy(out=dst[:, 0:2], in_=src[:, 0:2])
+            nc.scalar.copy(out=dst[:, 2:4], in_=src[:, 2:4])
 
-        def first_layer(h, tag, bufs):
-            acc = psum.tile([P, 4, P], F32, name="first%d" % h, tag=tag, bufs=bufs)
+        def first_layer(h):
+            acc = psum.tile([P, 4, P], F32, name="first%d" % h, tag="product")
             for t in range(4):
                 product(acc[:, t, :], w0_mx[h], slice(128 * t, 128 * t + 128), x_mx, slice(0, P))
             return acc[:].rearrange("p t n -> p n t")
@@ -114,13 +102,13 @@ def tile_graph_gan_pa_kernel(tc, x, fe_w0, fe_b0, fe_w1_bytes, fe_w1_scale, fe_b
         quantise(w0_mx[0][0][:], w0_mx[0][1][:], w0_laid[0][:])
         quantise(x_mx[0][:], x_mx[1][:], x_laid[:])
         w0_lay(1)
-        u_psum = first_layer(0, "product", 4)
+        u_psum = first_layer(0)
         quantise(w0_mx[1][0][:], w0_mx[1][1][:], w0_laid[1][:])
-        v_psum = first_layer(1, "product", 4)
+        v_psum = first_layer(1)
         u_sb = keep.tile([P, P, 4], F32, name="u_sb")
         v_sb = keep.tile([P, P, 4], F32, name="v_sb")
         nc.vector.tensor_tensor(out=u_sb[:], in0=u_psum, in1=b0_sb[:].unsqueeze(1).to_broadcast([P, P, 4]), op=ALU.add)
-        b1_turned = psum.tile([P, P], BF16, name="b1_turned", tag="turned", bufs=TURN_BANKS)
+        b1_turned = psum.tile([P, P], BF16, name="b1_turned", tag="turned")
         nc.tensor.transpose(b1_turned[:], b1_rows[:], ident_bf[:])
         b1_fifth = keep.tile([P, 8], F32, name="b1_fifth")
 
@@ -135,7 +123,7 @@ def tile_graph_gan_pa_kernel(tc, x, fe_w0, fe_b0, fe_w1_bytes, fe_w1_scale, fe_b
                 nc.scalar.activation(out=w1_planes[q][:, t, :], in_=w1_bytes[t // 2][:, n0 : n0 + 512].bitcast(FP8), func=ACT.Copy, scale=w1_scale[:, t : t + 1])
 
         def w1_weave(q, g):
-            acc = psum.tile([P, 2, 128, 4], BF16, name="w1_woven", tag="turned", bufs=TURN_BANKS)
+            acc = psum.tile([P, 2, 128, 4], BF16, name="w1_woven", tag="turned")
             for m in range(2):
                 n0 = 256 * g + 128 * m
                 nc.tensor.matmul(acc[:, m], lhsT=ident_bf[:], rhs=w1_planes[q][:, :, n0 : n0 + 128].rearrange("p t n -> p n t"), start=True, stop=True)
@@ -151,30 +139,27 @@ def tile_graph_gan_pa_kernel(tc, x, fe_w0, fe_b0, fe_w1_bytes, fe_w1_scale, fe_b
         def w1_quantise(q):
             quantise(w1_mx[q][0][:], w1_mx[q][1][:], w1_laid[q][:].rearrange("p n t -> p (n t)"))
 
-        i_ranges = [(0, I_SPLIT), (I_SPLIT, 16)]
         pair_sums = {}
         e1 = {}
         e1_mx = {}
 
         def e1_add(k, g, v):
-            i0, i1 = i_ranges[g]
-            graph, ni = k // 2, i1 - i0
-            n0 = 32 * graph + 16 * (k % 2) + i0
-            z = work.tile([P, ni, 32, 4], F32, name="pair_sums%d" % g)
+            graph = k // 2
+            n0 = 32 * graph + 16 * (k % 2) + 8 * g
+            z = work.tile([P, 8, 32, 4], F32, name="pair_sums%d" % g)
             nc.vector.tensor_tensor(
                 out=z[:],
-                in0=u_sb[:, n0 : n0 + ni, :].unsqueeze(2).to_broadcast([P, ni, 32, 4]),
-                in1=v[:, 32 * graph : 32 * graph + 32, :].unsqueeze(1).to_broadcast([P, ni, 32, 4]),
+                in0=u_sb[:, n0 : n0 + 8, :].unsqueeze(2).to_broadcast([P, 8, 32, 4]),
+                in1=v[:, 32 * graph : 32 * graph + 32, :].unsqueeze(1).to_broadcast([P, 8, 32, 4]),
                 op=ALU.add,
             )
             pair_sums[k, g] = z
 
         def e1_lrelu(k, g):
-            i0, i1 = i_ranges[g]
             if g == 0:
                 e1[k] = work.tile([P, 4 * PAIRS], BF16, name="e1", align_bytes=64)
             z = pair_sums[k, g][:].rearrange("p i j t -> p (i j t)")
-            nc.vector.scalar_tensor_tensor(out=e1[k][:, 128 * i0 : 128 * i1], in0=z, scalar=ALPHA, in1=z, op0=ALU.mult, op1=ALU.max)
+            nc.vector.scalar_tensor_tensor(out=e1[k][:, 1024 * g : 1024 * g + 1024], in0=z, scalar=ALPHA, in1=z, op0=ALU.mult, op1=ALU.max)
 
         def e1_quantise(k):
             e1_mx[k] = mx_operand(work, "e1", PAIRS, 3)
@@ -182,14 +167,13 @@ def tile_graph_gan_pa_kernel(tc, x, fe_w0, fe_b0, fe_w1_bytes, fe_w1_scale, fe_b
 
         rounds = []
         for k in range(CHUNKS):
-            nd = direct_tiles(k)
-            parts = [(k, m * 4 // nd, (m + 1) * 4 // nd, 512 - 128 * nd) for m in range(nd)]
-            if k < last:
-                rounds.append(([(k, c) for c in range(4)], []))
-                rounds.append(([(k, c) for c in range(4, 8 - nd)], parts))
-            else:
-                rounds.append(([(k, 0), (k, 1)], parts[0:2]))
-                rounds.append(([(k, 2), (k, 3)], parts[2:4]))
+            for h in range(2):
+                if 2 * k + h >= HALF_DIRECT_FROM:
+                    rounds.append((k, h, 4, 2, [(2, 3, 0), (3, 4, 0)]))
+                elif h == 1 and k >= DIRECT_FROM:
+                    rounds.append((k, h, 3, 4, [(0, 4, 384)]))
+                else:
+                    rounds.append((k, h, 4, 4, []))
         n_rounds = len(rounds)
         tile_psum = {}
         part_psum = {}
@@ -199,75 +183,70 @@ def tile_graph_gan_pa_kernel(tc, x, fe_w0, fe_b0, fe_w1_bytes, fe_w1_scale, fe_b
         part_sums = {}
         out_sb = {}
 
-        def out_half(k, h):
-            if (k, h) not in out_sb:
-                out_sb[k, h] = work.tile([P, 4, 512], F32, name="out_sb", bufs=4)
-            return out_sb[k, h]
+        def out_half(r):
+            if r not in out_sb:
+                out_sb[r] = work.tile([P, 4, 512], F32, name="out_sb", bufs=OUT_BUFFERS)
+            return out_sb[r]
 
-        def store_columns(k, h, c0, c1):
-            dst = rows[PAIRS * k : PAIRS * k + PAIRS, 512 * h + c0 : 512 * h + c1].rearrange("(s p) c -> p s c", p=P)
-            nc.sync.dma_start(out=dst, in_=out_sb[k, h][:, :, c0:c1])
+        def store(r, s):
+            k, h = rounds[r][0:2]
+            r0 = PAIRS * k + 128 * s
+            nc.sync.dma_start(out=rows[r0 : r0 + 128, 512 * h : 512 * h + 512], in_=out_sb[r][:, s, :])
 
         def tile_products(r):
-            for k, c in rounds[r][0]:
-                acc = psum.tile([P, PAIRS], F32, name="tile_psum", tag="product")
-                product(acc[:], w1_mx[c // 4], slice(128 * (c % 4), 128 * (c % 4) + 128), e1_mx[k], slice(0, PAIRS))
-                tile_psum[k, c] = acc
+            k, h, n, nb, parts = rounds[r]
+            per_bank = 4 // nb
+            for i0 in range(0, n, per_bank):
+                acc = psum.tile([P, per_bank, 128 * nb], F32, name="tile_psum", tag="product")
+                for i in range(i0, i0 + per_bank):
+                    product(acc[:, i - i0, :], w1_mx[h], slice(128 * i, 128 * i + 128), e1_mx[k], slice(0, 128 * nb))
+                    tile_psum[r, i] = acc[:, i - i0, :]
 
         def part_products(r):
-            for k, s0, s1, n0 in rounds[r][1]:
+            k, h, n, nb, parts = rounds[r]
+            for s0, s1, n0 in parts:
                 acc = psum.tile([P, s1 - s0, 512 - n0], F32, name="part_psum", tag="product")
                 for s in range(s0, s1):
-                    product(acc[:, s - s0, :], e1_mx[k], slice(128 * s, 128 * s + 128), w1_mx[1], slice(n0, 512))
-                part_psum[k, s0] = acc
+                    product(acc[:, s - s0, :], e1_mx[k], slice(128 * s, 128 * s + 128), w1_mx[h], slice(n0, 512))
+                part_psum[r, s0] = acc
 
         def affine(r):
-            a_sb[r] = work.tile([P, 4, PAIRS], F32, name="a_sb", bufs=3)
-            r_sb[r] = work.tile([P, 4, PAIRS], F32, name="r_sb", bufs=3)
-            for i, (k, c) in enumerate(rounds[r][0]):
-                nc.scalar.activation(out=a_sb[r][:, i, :], in_=tile_psum[k, c][:], func=ACT.Identity, bias=b1_fifth[:, c : c + 1], scale=ALPHA)
+            k, h, n, nb, parts = rounds[r]
+            a_sb[r] = work.tile([P, n, 128 * nb], F32, name="a_sb", bufs=3)
+            r_sb[r] = work.tile([P, n, 128 * nb], F32, name="r_sb", bufs=3)
+            for i in range(n):
+                c = 4 * h + i
+                nc.scalar.activation(out=a_sb[r][:, i, :], in_=tile_psum[r, i], func=ACT.Identity, bias=b1_fifth[:, c : c + 1], scale=ALPHA)
 
-        def relu(engine, r, i0, i1):
-            engine.tensor_scalar(out=r_sb[r][:, i0:i1, :], in0=a_sb[r][:, i0:i1, :], scalar1=4.0, scalar2=0.0, op0=ALU.mult, op1=ALU.max)
+        def relu(r, i0, i1):
+            nc.vector.tensor_scalar(out=r_sb[r][:, i0:i1, :], in0=a_sb[r][:, i0:i1, :], scalar1=4.0, scalar2=0.0, op0=ALU.mult, op1=ALU.max)
 
-        def turn(r, i):
-            acc = psum.tile([P, 4, P], F32, name="turned", tag="turned", bufs=TURN_BANKS)
-            for s in range(4):
-                for n, src in enumerate((a_sb[r], r_sb[r])):
-                    nc.tensor.matmul(acc[:, s, :], lhsT=src[:, i, 128 * s : 128 * s + 128], rhs=ident[:], is_transpose=True, start=(n == 0), stop=(n == 1))
-            turned[r, i] = acc
+        def turn(r, s):
+            n = rounds[r][2]
+            acc = psum.tile([P, n, P], F32, name="turned", tag="turned")
+            for i in range(n):
+                for m, src in enumerate((a_sb[r], r_sb[r])):
+                    nc.tensor.matmul(acc[:, i, :], lhsT=src[:, i, 128 * s : 128 * s + 128], rhs=ident[:], is_transpose=True, start=(m == 0), stop=(m == 1))
+            turned[r, s] = acc
 
-        def leave(r, i):
-            k, c = rounds[r][0][i]
-            h, c0 = c // 4, 128 * (c % 4)
-            nc.scalar.copy(out=out_half(k, h)[:, :, c0 : c0 + 128], in_=turned[r, i][:])
-            closes_round = i == len(rounds[r][0]) - 1
-            if r == n_rounds - 1:
-                store_columns(k, h, c0, c0 + 128)
-            elif k < FINE_STORES_FROM:
-                if closes_round:
-                    store_columns(k, h, 0, 512)
-            elif c % 2 == 1:
-                store_columns(k, h, c0 - 128, c0 + 128)
-            elif closes_round:
-                store_columns(k, h, c0, 512)
+        def leave(r, s):
+            n = rounds[r][2]
+            nc.scalar.copy(out=out_half(r)[:, s, 0 : 128 * n], in_=turned[r, s][:].rearrange("p i c -> p (i c)"))
+            store(r, s)
 
-        def part_add(k, s0, s1, n0):
+        def part_add(r, s0, s1, n0):
+            h = rounds[r][1]
             shape = [P, s1 - s0, 512 - n0]
             z = work.tile(shape, F32, name="part_sums")
-            nc.vector.tensor_tensor(out=z[:], in0=part_psum[k, s0][:], in1=b1_spread[:, n0:512].unsqueeze(1).to_broadcast(shape), op=ALU.add)
-            part_sums[k, s0] = z
+            bias = b1_spread[:, 512 * h + n0 : 512 * h + 512]
+            nc.vector.tensor_tensor(out=z[:], in0=part_psum[r, s0][:], in1=bias.unsqueeze(1).to_broadcast(shape), op=ALU.add)
+            part_sums[r, s0] = z
 
-        def part_lrelu(k, s0, s1, n0):
-            z = part_sums[k, s0][:]
-            nc.vector.scalar_tensor_tensor(out=out_half(k, 1)[:, s0:s1, n0:512], in0=z, scalar=ALPHA, in1=z, op0=ALU.mult, op1=ALU.max)
-
-        def part_store(k, s0, s1, n0):
-            if k == last:
-                r0 = PAIRS * k + 128 * s0
-                nc.sync.dma_start(out=rows[r0 : r0 + 128, 512:1024], in_=out_sb[k, 1][:, s0, :])
-            elif k >= FINE_STORES_FROM and n0 == 256 and s1 == 4:
-                store_columns(k, 1, n0, 512)
+        def part_lrelu(r, s0, s1, n0):
+            z = part_sums[r, s0][:]
+            nc.vector.scalar_tensor_tensor(out=out_half(r)[:, s0:s1, n0:512], in0=z, scalar=ALPHA, in1=z, op0=ALU.mult, op1=ALU.max)
+            if n0 == 0:
+                store(r, s0)
 
         w1_widen(0)
         w1_weave(0, 0)
@@ -291,50 +270,54 @@ def tile_graph_gan_pa_kernel(tc, x, fe_w0, fe_b0, fe_w1_bytes, fe_w1_scale, fe_b
         w1_quantise(1)
         tile_products(0)
 
-        for r in range(n_rounds + 1):
-            k, second = divmod(r, 2)
-            before = len(rounds[r - 1][0]) if r > 0 else 0
-            for i in range(before):
-                turn(r - 1, i)
-            tiles, parts = rounds[r] if r < n_rounds else ([], [])
-            unstored = parts
-            if r < n_rounds:
-                affine(r)
-            if k < last and not second:
+        for r in range(n_rounds):
+            k, h, n, nb, parts = rounds[r]
+            blocks_before = rounds[r - 1][3] if r > 0 else 0
+            for s in range(blocks_before):
+                turn(r - 1, s)
+            affine(r)
+            if r == 0:
+                relu(r, 0, 2)
+                relu(r, 2, 4)
                 e1_lrelu(k + 1, 0)
-                relu(nc.vector, r, 0, 2)
                 e1_lrelu(k + 1, 1)
-                relu(nc.vector, r, 2, 4)
                 e1_quantise(k + 1)
-            elif k < last - 1:
+            elif r > HALF_DIRECT_FROM:
+                part_add(r, *parts[0])
+                part_add(r, *parts[1])
+                part_lrelu(r, *parts[0])
+                relu(r, 0, n)
+            elif r == HALF_DIRECT_FROM:
+                part_add(r, *parts[0])
+                part_add(r, *parts[1])
+                relu(r, 0, n)
+            elif h == 0:
+                e1_lrelu(k + 1, 0)
+                relu(r, 0, 2)
+                e1_lrelu(k + 1, 1)
+                relu(r, 2, 4)
+                e1_quantise(k + 1)
+            else:
                 for part in parts:
-                    part_add(*part)
+                    part_add(r, *part)
                 e1_add(k + 2, 0, v_sb)
                 for part in parts:
-                    part_lrelu(*part)
-                relu(nc.vector, r, 0, len(tiles))
+                    part_lrelu(r, *part)
+                relu(r, 0, n)
                 e1_add(k + 2, 1, v_sb)
-            elif r == n_rounds - 2:
-                part_add(*parts[0])
-                part_add(*parts[1])
-                part_lrelu(*parts[0])
-                part_store(*parts[0])
-                relu(nc.vector, r, 0, 2)
-                part_lrelu(*parts[1])
-                unstored = parts[1:]
-            elif r < n_rounds:
-                part_add(*parts[0])
-                part_add(*parts[1])
-                relu(nc.vector, r, 0, 2)
-                part_lrelu(*parts[0])
-                part_lrelu(*parts[1])
-            if r + 1 < n_rounds - 2:
+            if r < HALF_DIRECT_FROM:
                 tile_products(r + 1)
                 part_products(r + 1)
             elif r + 1 < n_rounds:
                 part_products(r + 1)
                 tile_products(r + 1)
-            for i in range(before):
-                leave(r - 1, i)
-            for part in unstored:
-                part_store(*part)
+            for s in range(blocks_before):
+                leave(r - 1, s)
+                if r == HALF_DIRECT_FROM and s == 1:
+                    part_lrelu(r, *parts[0])
+            if r >= HALF_DIRECT_FROM:
+                part_lrelu(r, *parts[1])
+        for s in range(nb):
+            turn(n_rounds - 1, s)
+        for s in range(nb):
+            leave(n_rounds - 1, s)

@@ -19,7 +19,9 @@ CHUNKS = 8
 PAIRS = 512
 DIRECT_FROM = 1
 OUT_BUFFERS = 11
-HALF_DIRECT_FROM = 2 * CHUNKS - 3
+W0_VECTOR = 80
+CUT = 10
+FIRST_CUT = 12
 
 
 def tile_graph_gan_pa_kernel(tc, x, fe_w0, fe_b0, fe_w1_bytes, fe_w1_scale, fe_b1, out):
@@ -41,8 +43,8 @@ def tile_graph_gan_pa_kernel(tc, x, fe_w0, fe_b0, fe_w1_bytes, fe_w1_scale, fe_b
         b1_spread = keep.tile([P, 1024], BF16, name="b1_spread")
         w0_rows = fe_w0.rearrange("(h p t) w -> h p t w", h=2, t=4)
         w1_rows = fe_w1_bytes.rearrange("(p t) n -> p (t n)", t=4)
-        nc.sync.dma_start(out=w0_raw[0][:], in_=w0_rows[0])
         nc.sync.dma_start(out=x_sb[:], in_=x.rearrange("b n d -> (b n) d"))
+        nc.sync.dma_start(out=w0_raw[0][:], in_=w0_rows[0])
         nc.sync.dma_start(out=w0_raw[1][:], in_=w0_rows[1])
         for g in range(2):
             nc.sync.dma_start(out=w1_bytes[g][:], in_=w1_rows[:, 2048 * g : 2048 * g + 2048])
@@ -88,19 +90,22 @@ def tile_graph_gan_pa_kernel(tc, x, fe_w0, fe_b0, fe_w1_bytes, fe_w1_scale, fe_b
         def w0_lay(h):
             dst = w0_laid[h][:].rearrange("p (t m j) -> p t m j", t=4, j=4)
             src = w0_raw[h][:].rearrange("p j (m t) -> p t m j", t=4)
-            nc.vector.tensor_copy(out=dst[:, 0:2], in_=src[:, 0:2])
-            nc.scalar.copy(out=dst[:, 2:4], in_=src[:, 2:4])
+            nc.vector.tensor_copy(out=dst[:, :, 0:W0_VECTOR], in_=src[:, :, 0:W0_VECTOR])
+            nc.scalar.copy(out=dst[:, :, W0_VECTOR:], in_=src[:, :, W0_VECTOR:])
 
         def first_layer(h):
-            acc = psum.tile([P, 4, P], F32, name="first%d" % h, tag="product")
+            if h == 0:
+                acc = psum.tile([P, 4, P], F32, name="first_u", tag="product")
+            else:
+                acc = psum.tile([P, 4, P], F32, name="first_v", tag="v", bufs=1)
             for t in range(4):
                 product(acc[:, t, :], w0_mx[h], slice(128 * t, 128 * t + 128), x_mx, slice(0, P))
             return acc[:].rearrange("p t n -> p n t")
 
-        w0_lay(0)
         nc.vector.tensor_copy(out=x_laid[:].bitcast(F32).rearrange("p (n u) -> p n u", u=2), in_=x_turned[:].rearrange("p u n -> p n u"))
-        quantise(w0_mx[0][0][:], w0_mx[0][1][:], w0_laid[0][:])
+        w0_lay(0)
         quantise(x_mx[0][:], x_mx[1][:], x_laid[:])
+        quantise(w0_mx[0][0][:], w0_mx[0][1][:], w0_laid[0][:])
         w0_lay(1)
         u_psum = first_layer(0)
         quantise(w0_mx[1][0][:], w0_mx[1][1][:], w0_laid[1][:])
@@ -108,8 +113,9 @@ def tile_graph_gan_pa_kernel(tc, x, fe_w0, fe_b0, fe_w1_bytes, fe_w1_scale, fe_b
         u_sb = keep.tile([P, P, 4], F32, name="u_sb")
         v_sb = keep.tile([P, P, 4], F32, name="v_sb")
         nc.vector.tensor_tensor(out=u_sb[:], in0=u_psum, in1=b0_sb[:].unsqueeze(1).to_broadcast([P, P, 4]), op=ALU.add)
-        b1_turned = psum.tile([P, P], BF16, name="b1_turned", tag="turned")
+        b1_turned = psum.tile([P, P], BF16, name="b1_turned", tag="turned", bufs=3)
         nc.tensor.transpose(b1_turned[:], b1_rows[:], ident_bf[:])
+        b1_four_fifths = keep.tile([P, 8], F32, name="b1_four_fifths")
         b1_fifth = keep.tile([P, 8], F32, name="b1_fifth")
 
         w1_planes = [keep.tile([P, 4, 512], BF16, name="w1_planes%d" % q, align_bytes=64) for q in range(2)]
@@ -123,7 +129,7 @@ def tile_graph_gan_pa_kernel(tc, x, fe_w0, fe_b0, fe_w1_bytes, fe_w1_scale, fe_b
                 nc.scalar.activation(out=w1_planes[q][:, t, :], in_=w1_bytes[t // 2][:, n0 : n0 + 512].bitcast(FP8), func=ACT.Copy, scale=w1_scale[:, t : t + 1])
 
         def w1_weave(q, g):
-            acc = psum.tile([P, 2, 128, 4], BF16, name="w1_woven", tag="turned")
+            acc = psum.tile([P, 2, 128, 4], BF16, name="w1_woven", tag="turned", bufs=3)
             for m in range(2):
                 n0 = 256 * g + 128 * m
                 nc.tensor.matmul(acc[:, m], lhsT=ident_bf[:], rhs=w1_planes[q][:, :, n0 : n0 + 128].rearrange("p t n -> p n t"), start=True, stop=True)
@@ -132,48 +138,48 @@ def tile_graph_gan_pa_kernel(tc, x, fe_w0, fe_b0, fe_w1_bytes, fe_w1_scale, fe_b
         def w1_leave(q, g):
             nc.scalar.copy(out=w1_laid[q][:, 256 * g : 256 * g + 256, :].rearrange("p n t -> p (n t)"), in_=w1_woven[q, g][:].rearrange("p m n t -> p (m n t)"))
 
-        def w1_lay(q, g):
-            cols = slice(256 * g, 256 * g + 256)
-            nc.scalar.copy(out=w1_laid[q][:, cols, :].rearrange("p (c i) t -> p c t i", i=4), in_=w1_planes[q][:, :, cols].rearrange("p t (c i) -> p c t i", i=4))
-
         def w1_quantise(q):
             quantise(w1_mx[q][0][:], w1_mx[q][1][:], w1_laid[q][:].rearrange("p n t -> p (n t)"))
 
         pair_sums = {}
-        e1 = {}
         e1_mx = {}
+        shared = [keep.tile([P, 4 * PAIRS], BF16, name="shared%d" % j, align_bytes=64) for j in range(2)]
 
-        def e1_add(k, g, v):
+        def pair_operands(k, i0, i1, v):
             graph = k // 2
-            n0 = 32 * graph + 16 * (k % 2) + 8 * g
-            z = work.tile([P, 8, 32, 4], F32, name="pair_sums%d" % g)
-            nc.vector.tensor_tensor(
-                out=z[:],
-                in0=u_sb[:, n0 : n0 + 8, :].unsqueeze(2).to_broadcast([P, 8, 32, 4]),
-                in1=v[:, 32 * graph : 32 * graph + 32, :].unsqueeze(1).to_broadcast([P, 8, 32, 4]),
-                op=ALU.add,
-            )
-            pair_sums[k, g] = z
+            n0 = 32 * graph + 16 * (k % 2)
+            shape = [P, i1 - i0, 32, 4]
+            return u_sb[:, n0 + i0 : n0 + i1, :].unsqueeze(2).to_broadcast(shape), v[:, 32 * graph : 32 * graph + 32, :].unsqueeze(1).to_broadcast(shape)
 
-        def e1_lrelu(k, g):
-            if g == 0:
-                e1[k] = work.tile([P, 4 * PAIRS], BF16, name="e1", align_bytes=64)
-            z = pair_sums[k, g][:].rearrange("p i j t -> p (i j t)")
-            nc.vector.scalar_tensor_tensor(out=e1[k][:, 1024 * g : 1024 * g + 1024], in0=z, scalar=ALPHA, in1=z, op0=ALU.mult, op1=ALU.max)
+        def e1_add(k, i0, i1):
+            z = work.tile([P, i1 - i0, 32, 4], F32, name="pair_sums")
+            in0, in1 = pair_operands(k, i0, i1, v_psum)
+            nc.vector.tensor_tensor(out=z[:], in0=in0, in1=in1, op=ALU.add)
+            pair_sums[k, i0] = z[:].rearrange("p i j t -> p (i j t)")
 
-        def e1_quantise(k):
-            e1_mx[k] = mx_operand(work, "e1", PAIRS, 3)
-            quantise(e1_mx[k][0][:], e1_mx[k][1][:], e1[k][:])
+        def e1_add_gpsimd(k, i0, i1):
+            z = shared[(k + 1) % 2][:].bitcast(F32)[:, 1024 - 128 * (i1 - i0) : 1024]
+            in0, in1 = pair_operands(k, i0, i1, v_sb)
+            nc.gpsimd.tensor_tensor(out=z.rearrange("p (i j t) -> p i j t", j=32, t=4), in0=in0, in1=in1, op=ALU.add)
+            pair_sums[k, i0] = z
 
-        rounds = []
-        for k in range(CHUNKS):
+        def e1_lrelu(k, i0, i1):
+            z = pair_sums[k, i0]
+            nc.vector.scalar_tensor_tensor(out=shared[k % 2][:, 128 * i0 : 128 * i1], in0=z, scalar=ALPHA, in1=z, op0=ALU.mult, op1=ALU.max)
+
+        def e1_quantise(k, g0, g1):
+            if g0 == 0:
+                e1_mx[k] = mx_operand(work, "e1", PAIRS, 2)
+            cols = slice(256 * g0, 256 * g1)
+            quantise(e1_mx[k][0][:, cols], e1_mx[k][1][:, cols], shared[k % 2][:, 1024 * g0 : 1024 * g1])
+
+        rounds = [(0, 0, 4, 0, 2, []), (0, 1, 4, 0, 2, []), (0, 0, 4, 2, 4, []), (0, 1, 4, 2, 4, [])]
+        for k in range(1, CHUNKS):
             for h in range(2):
-                if 2 * k + h >= HALF_DIRECT_FROM:
-                    rounds.append((k, h, 4, 2, [(2, 3, 0), (3, 4, 0)]))
-                elif h == 1 and k >= DIRECT_FROM:
-                    rounds.append((k, h, 3, 4, [(0, 4, 384)]))
+                if k == CHUNKS - 1:
+                    rounds.append((k, h, 4, 0, 2, [(2, 3, 0), (3, 4, 0)]))
                 else:
-                    rounds.append((k, h, 4, 4, []))
+                    rounds.append((k, h, 3, 0, 4, [(0, 4, 384)]))
         n_rounds = len(rounds)
         tile_psum = {}
         part_psum = {}
@@ -184,26 +190,28 @@ def tile_graph_gan_pa_kernel(tc, x, fe_w0, fe_b0, fe_w1_bytes, fe_w1_scale, fe_b
         out_sb = {}
 
         def out_half(r):
-            if r not in out_sb:
-                out_sb[r] = work.tile([P, 4, 512], F32, name="out_sb", bufs=OUT_BUFFERS)
-            return out_sb[r]
+            key = rounds[r][0:2]
+            if key not in out_sb:
+                out_sb[key] = work.tile([P, 4, 512], F32, name="out_sb", bufs=OUT_BUFFERS)
+            return out_sb[key]
 
-        def store(r, s):
+        def store(r, s0, s1):
             k, h = rounds[r][0:2]
-            r0 = PAIRS * k + 128 * s
-            nc.sync.dma_start(out=rows[r0 : r0 + 128, 512 * h : 512 * h + 512], in_=out_sb[r][:, s, :])
+            dst = rows[PAIRS * k + 128 * s0 : PAIRS * k + 128 * s1, 512 * h : 512 * h + 512]
+            nc.sync.dma_start(out=dst.rearrange("(s p) c -> p s c", p=P), in_=out_half(r)[:, s0:s1, :])
 
         def tile_products(r):
-            k, h, n, nb, parts = rounds[r]
+            k, h, n, b0, b1, parts = rounds[r]
+            nb = b1 - b0
             per_bank = 4 // nb
             for i0 in range(0, n, per_bank):
                 acc = psum.tile([P, per_bank, 128 * nb], F32, name="tile_psum", tag="product")
                 for i in range(i0, i0 + per_bank):
-                    product(acc[:, i - i0, :], w1_mx[h], slice(128 * i, 128 * i + 128), e1_mx[k], slice(0, 128 * nb))
+                    product(acc[:, i - i0, :], w1_mx[h], slice(128 * i, 128 * i + 128), e1_mx[k], slice(128 * b0, 128 * b1))
                     tile_psum[r, i] = acc[:, i - i0, :]
 
         def part_products(r):
-            k, h, n, nb, parts = rounds[r]
+            k, h, n, b0, b1, parts = rounds[r]
             for s0, s1, n0 in parts:
                 acc = psum.tile([P, s1 - s0, 512 - n0], F32, name="part_psum", tag="product")
                 for s in range(s0, s1):
@@ -211,9 +219,9 @@ def tile_graph_gan_pa_kernel(tc, x, fe_w0, fe_b0, fe_w1_bytes, fe_w1_scale, fe_b
                 part_psum[r, s0] = acc
 
         def affine(r):
-            k, h, n, nb, parts = rounds[r]
-            a_sb[r] = work.tile([P, n, 128 * nb], F32, name="a_sb", bufs=3)
-            r_sb[r] = work.tile([P, n, 128 * nb], F32, name="r_sb", bufs=3)
+            k, h, n, b0, b1, parts = rounds[r]
+            a_sb[r] = work.tile([P, n, 128 * (b1 - b0)], F32, name="a_sb", bufs=3)
+            r_sb[r] = work.tile([P, n, 128 * (b1 - b0)], F32, name="r_sb", bufs=3)
             for i in range(n):
                 c = 4 * h + i
                 nc.scalar.activation(out=a_sb[r][:, i, :], in_=tile_psum[r, i], func=ACT.Identity, bias=b1_fifth[:, c : c + 1], scale=ALPHA)
@@ -221,18 +229,31 @@ def tile_graph_gan_pa_kernel(tc, x, fe_w0, fe_b0, fe_w1_bytes, fe_w1_scale, fe_b
         def relu(r, i0, i1):
             nc.vector.tensor_scalar(out=r_sb[r][:, i0:i1, :], in0=a_sb[r][:, i0:i1, :], scalar1=4.0, scalar2=0.0, op0=ALU.mult, op1=ALU.max)
 
-        def turn(r, s):
-            n = rounds[r][2]
-            acc = psum.tile([P, n, P], F32, name="turned", tag="turned")
-            for i in range(n):
-                for m, src in enumerate((a_sb[r], r_sb[r])):
-                    nc.tensor.matmul(acc[:, i, :], lhsT=src[:, i, 128 * s : 128 * s + 128], rhs=ident[:], is_transpose=True, start=(m == 0), stop=(m == 1))
-            turned[r, s] = acc
+        def relu_scalar(r, i):
+            c = 4 * rounds[r][1] + i
+            nc.scalar.activation(out=r_sb[r][:, i, :], in_=tile_psum[r, i], func=ACT.Relu, bias=b1_four_fifths[:, c : c + 1], scale=4 * ALPHA)
 
-        def leave(r, s):
-            n = rounds[r][2]
-            nc.scalar.copy(out=out_half(r)[:, s, 0 : 128 * n], in_=turned[r, s][:].rearrange("p i c -> p (i c)"))
-            store(r, s)
+        def banks(r):
+            n, b0, b1 = rounds[r][2:5]
+            if n == 3:
+                return [[(i, s) for s in range(b0, b1)] for i in range(n)]
+            return [[(i, s) for i in range(n)] for s in range(b0, b1)]
+
+        def turn(r, g):
+            b0 = rounds[r][3]
+            acc = psum.tile([P, 4, P], F32, name="turned", tag="turned", bufs=3)
+            for j, (i, s) in enumerate(banks(r)[g]):
+                for m, src in enumerate((a_sb[r], r_sb[r])):
+                    nc.tensor.matmul(acc[:, j, :], lhsT=src[:, i, 128 * (s - b0) : 128 * (s - b0) + 128], rhs=ident[:], is_transpose=True, start=(m == 0), stop=(m == 1))
+            turned[r, g] = acc
+
+        def leave(r, g, copy=nc.scalar.copy):
+            (i0, s0), (i1, s1) = banks(r)[g][0], banks(r)[g][-1]
+            if s0 == s1:
+                copy(out=out_half(r)[:, s0, :], in_=turned[r, g][:].rearrange("p i c -> p (i c)"))
+                store(r, s0, s0 + 1)
+            else:
+                copy(out=out_half(r)[:, :, 128 * i0 : 128 * i0 + 128], in_=turned[r, g][:])
 
         def part_add(r, s0, s1, n0):
             h = rounds[r][1]
@@ -246,78 +267,104 @@ def tile_graph_gan_pa_kernel(tc, x, fe_w0, fe_b0, fe_w1_bytes, fe_w1_scale, fe_b
             z = part_sums[r, s0][:]
             nc.vector.scalar_tensor_tensor(out=out_half(r)[:, s0:s1, n0:512], in0=z, scalar=ALPHA, in1=z, op0=ALU.mult, op1=ALU.max)
             if n0 == 0:
-                store(r, s0)
+                store(r, s0, s1)
+
 
         w1_widen(0)
         w1_weave(0, 0)
         w1_weave(0, 1)
-        e1_add(0, 0, v_psum)
+        e1_add(0, 0, 8)
         w1_widen(1)
         nc.scalar.activation(out=b1_fifth[:], in_=b1_turned[:, 0:8], func=ACT.Copy, scale=ALPHA)
+        nc.scalar.activation(out=b1_four_fifths[:], in_=b1_turned[:, 0:8], func=ACT.Copy, scale=4 * ALPHA)
         w1_weave(1, 0)
-        e1_add(0, 1, v_psum)
+        e1_add(0, 8, 16)
         w1_leave(0, 0)
         w1_leave(0, 1)
-        nc.scalar.copy(out=v_sb[:], in_=v_psum)
-        w1_lay(1, 1)
-        w1_leave(1, 0)
-        e1_lrelu(0, 0)
-        e1_lrelu(0, 1)
+        w1_weave(1, 1)
+        e1_lrelu(0, 0, 8)
         w1_quantise(0)
-        e1_quantise(0)
-        e1_add(1, 0, v_sb)
-        e1_add(1, 1, v_sb)
-        w1_quantise(1)
+        w1_leave(1, 0)
+        w1_leave(1, 1)
+        nc.scalar.copy(out=v_sb[:], in_=v_psum)
+        e1_quantise(0, 0, 1)
         tile_products(0)
+        e1_lrelu(0, 8, 16)
+        w1_quantise(1)
+        e1_quantise(0, 1, 2)
+        e1_add_gpsimd(1, FIRST_CUT, 16)
+        e1_add(1, 0, FIRST_CUT)
 
+        last = n_rounds - 1
+        leaving = [[], [], [0], [1, 2]] + [[r - 1] for r in range(4, n_rounds)]
         for r in range(n_rounds):
-            k, h, n, nb, parts = rounds[r]
-            blocks_before = rounds[r - 1][3] if r > 0 else 0
-            for s in range(blocks_before):
-                turn(r - 1, s)
+            k, h, n, b0, b1, parts = rounds[r]
             affine(r)
             if r == 0:
-                relu(r, 0, 2)
-                relu(r, 2, 4)
-                e1_lrelu(k + 1, 0)
-                e1_lrelu(k + 1, 1)
-                e1_quantise(k + 1)
-            elif r > HALF_DIRECT_FROM:
+                relu(r, 0, n)
+                e1_lrelu(1, 0, FIRST_CUT)
+            elif r == 1:
+                relu(r, 0, n)
+                e1_lrelu(1, FIRST_CUT, 16)
+            elif r == 2:
+                relu(r, 0, n)
+                e1_quantise(1, 0, 2)
+                e1_add_gpsimd(2, FIRST_CUT, 16)
+                e1_add(2, 0, FIRST_CUT)
+            elif r == 3:
+                relu(r, 0, n)
+            elif r == last:
+                part_add(r, *parts[0])
+                relu(r, 0, n)
+                part_add(r, *parts[1])
+            elif k == CHUNKS - 1:
                 part_add(r, *parts[0])
                 part_add(r, *parts[1])
                 part_lrelu(r, *parts[0])
-                relu(r, 0, n)
-            elif r == HALF_DIRECT_FROM:
-                part_add(r, *parts[0])
-                part_add(r, *parts[1])
+                part_lrelu(r, *parts[1])
                 relu(r, 0, n)
             elif h == 0:
-                e1_lrelu(k + 1, 0)
-                relu(r, 0, 2)
-                e1_lrelu(k + 1, 1)
-                relu(r, 2, 4)
-                e1_quantise(k + 1)
-            else:
-                for part in parts:
-                    part_add(r, *part)
-                e1_add(k + 2, 0, v_sb)
-                for part in parts:
-                    part_lrelu(r, *part)
+                cut = FIRST_CUT if k == 1 else CUT
+                part_add(r, *parts[0])
+                if k > 1:
+                    part_lrelu(r - 1, *rounds[r - 1][5][0])
+                e1_lrelu(k + 1, 0, cut)
                 relu(r, 0, n)
-                e1_add(k + 2, 1, v_sb)
-            if r < HALF_DIRECT_FROM:
-                tile_products(r + 1)
-                part_products(r + 1)
-            elif r + 1 < n_rounds:
-                part_products(r + 1)
-                tile_products(r + 1)
-            for s in range(blocks_before):
-                leave(r - 1, s)
-                if r == HALF_DIRECT_FROM and s == 1:
+                e1_lrelu(k + 1, cut, 16)
+            else:
+                relu_scalar(r, 2)
+                part_lrelu(r - 1, *rounds[r - 1][5][0])
+                relu(r, 0, 2)
+                e1_quantise(k + 1, 0, 2)
+                if k + 2 < CHUNKS:
+                    e1_add_gpsimd(k + 2, CUT, 16)
+                part_add(r, *parts[0])
+                if k + 2 < CHUNKS:
+                    e1_add(k + 2, 0, CUT)
+                else:
                     part_lrelu(r, *parts[0])
-            if r >= HALF_DIRECT_FROM:
+            for q in leaving[r]:
+                for g in range(len(banks(q))):
+                    turn(q, g)
+            if r + 2 == last:
+                part_products(r + 1)
+                tile_products(r + 1)
+            elif r < last:
+                tile_products(r + 1)
+                part_products(r + 1)
+            if r == last:
+                leave(r - 1, 0)
+                part_lrelu(r, *parts[0])
+                leave(r - 1, 1)
                 part_lrelu(r, *parts[1])
-        for s in range(nb):
-            turn(n_rounds - 1, s)
-        for s in range(nb):
-            leave(n_rounds - 1, s)
+            else:
+                for q in leaving[r]:
+                    for g in range(len(banks(q))):
+                        leave(q, g)
+                    if rounds[q][2] == 3:
+                        store(q, 0, 2)
+                        store(q, 2, 4)
+        turn(last, 0)
+        turn(last, 1)
+        leave(last, 0)
+        leave(last, 1, nc.vector.tensor_copy)

@@ -17,11 +17,12 @@ FLOPS = 2 * 128 * 512 * 512 * 2 + 2 * 4096 * 512 * 1024
 ALPHA = 0.2
 CHUNKS = 8
 PAIRS = 512
-DIRECT_FROM = 1
 OUT_BUFFERS = 11
 W0_VECTOR = 80
-CUT = 10
-FIRST_CUT = 12
+CUT = 11
+FIRST_CUT = 13
+SECOND_CUT = 12
+STRIP_ROUNDS = 4
 
 
 def tile_graph_gan_pa_kernel(tc, x, fe_w0, fe_b0, fe_w1_bytes, fe_w1_scale, fe_b1, out):
@@ -119,7 +120,7 @@ def tile_graph_gan_pa_kernel(tc, x, fe_w0, fe_b0, fe_w1_bytes, fe_w1_scale, fe_b
         b1_fifth = keep.tile([P, 8], F32, name="b1_fifth")
 
         w1_planes = [keep.tile([P, 4, 512], BF16, name="w1_planes%d" % q, align_bytes=64) for q in range(2)]
-        w1_laid = [keep.tile([P, 512, 4], BF16, name="w1_laid%d" % q, align_bytes=64) for q in range(2)]
+        w1_laid = [w0_laid[1 - q][:].rearrange("p (n t) -> p n t", t=4) for q in range(2)]
         w1_mx = [mx_operand(keep, "w1_%d" % q, 512, 1) for q in range(2)]
         w1_woven = {}
 
@@ -138,8 +139,16 @@ def tile_graph_gan_pa_kernel(tc, x, fe_w0, fe_b0, fe_w1_bytes, fe_w1_scale, fe_b
         def w1_leave(q, g):
             nc.scalar.copy(out=w1_laid[q][:, 256 * g : 256 * g + 256, :].rearrange("p n t -> p (n t)"), in_=w1_woven[q, g][:].rearrange("p m n t -> p (m n t)"))
 
+        def w1_lay_gpsimd(q, g):
+            cols = slice(256 * g, 256 * g + 256)
+            nc.gpsimd.tensor_scalar(out=w1_laid[q][:, cols, :], in0=w1_planes[q][:, :, cols].rearrange("p t n -> p n t"), scalar1=1.0, scalar2=0.0, op0=ALU.mult, op1=ALU.add)
+
+        def w1_lay(q, g):
+            cols = slice(256 * g, 256 * g + 256)
+            nc.scalar.copy(out=w1_laid[q][:, cols, :].rearrange("p (c i) t -> p c t i", i=4), in_=w1_planes[q][:, :, cols].rearrange("p t (c i) -> p c t i", i=4))
+
         def w1_quantise(q):
-            quantise(w1_mx[q][0][:], w1_mx[q][1][:], w1_laid[q][:].rearrange("p n t -> p (n t)"))
+            quantise(w1_mx[q][0][:], w1_mx[q][1][:], w1_laid[q].rearrange("p n t -> p (n t)"))
 
         pair_sums = {}
         e1_mx = {}
@@ -177,7 +186,7 @@ def tile_graph_gan_pa_kernel(tc, x, fe_w0, fe_b0, fe_w1_bytes, fe_w1_scale, fe_b
         for k in range(1, CHUNKS):
             for h in range(2):
                 if k == CHUNKS - 1:
-                    rounds.append((k, h, 4, 0, 2, [(2, 3, 0), (3, 4, 0)]))
+                    rounds.append((k, h, 4, 0, 2 - h, [(s, s + 1, 0) for s in range(2 - h, 4)]))
                 else:
                     rounds.append((k, h, 3, 0, 4, [(0, 4, 384)]))
         n_rounds = len(rounds)
@@ -220,8 +229,8 @@ def tile_graph_gan_pa_kernel(tc, x, fe_w0, fe_b0, fe_w1_bytes, fe_w1_scale, fe_b
 
         def affine(r):
             k, h, n, b0, b1, parts = rounds[r]
-            a_sb[r] = work.tile([P, n, 128 * (b1 - b0)], F32, name="a_sb", bufs=3)
-            r_sb[r] = work.tile([P, n, 128 * (b1 - b0)], F32, name="r_sb", bufs=3)
+            a_sb[r] = work.tile([P, n, 128 * (b1 - b0)], F32, name="a_sb", bufs=4)
+            r_sb[r] = work.tile([P, n, 128 * (b1 - b0)], F32, name="r_sb", bufs=4)
             for i in range(n):
                 c = 4 * h + i
                 nc.scalar.activation(out=a_sb[r][:, i, :], in_=tile_psum[r, i], func=ACT.Identity, bias=b1_fifth[:, c : c + 1], scale=ALPHA)
@@ -233,15 +242,22 @@ def tile_graph_gan_pa_kernel(tc, x, fe_w0, fe_b0, fe_w1_bytes, fe_w1_scale, fe_b
             c = 4 * rounds[r][1] + i
             nc.scalar.activation(out=r_sb[r][:, i, :], in_=tile_psum[r, i], func=ACT.Relu, bias=b1_four_fifths[:, c : c + 1], scale=4 * ALPHA)
 
+        def relu_scalar_half(r):
+            c = 4 * rounds[r][1] + 2
+            nc.scalar.activation(out=r_sb[r][:, 2, 256:512], in_=tile_psum[r, 2][:, 256:512], func=ACT.Relu, bias=b1_four_fifths[:, c : c + 1], scale=4 * ALPHA)
+
         def banks(r):
             n, b0, b1 = rounds[r][2:5]
-            if n == 3:
+            if n == 3 and r < n_rounds - STRIP_ROUNDS:
                 return [[(i, s) for s in range(b0, b1)] for i in range(n)]
             return [[(i, s) for i in range(n)] for s in range(b0, b1)]
 
         def turn(r, g):
             b0 = rounds[r][3]
-            acc = psum.tile([P, 4, P], F32, name="turned", tag="turned", bufs=3)
+            if g < 3 or len(banks(r)) == 3:
+                acc = psum.tile([P, len(banks(r)[g]), P], F32, name="turned", tag="turned", bufs=3)
+            else:
+                acc = psum.tile([P, len(banks(r)[g]), P], F32, name="turned_last", tag="v", bufs=1)
             for j, (i, s) in enumerate(banks(r)[g]):
                 for m, src in enumerate((a_sb[r], r_sb[r])):
                     nc.tensor.matmul(acc[:, j, :], lhsT=src[:, i, 128 * (s - b0) : 128 * (s - b0) + 128], rhs=ident[:], is_transpose=True, start=(m == 0), stop=(m == 1))
@@ -250,7 +266,7 @@ def tile_graph_gan_pa_kernel(tc, x, fe_w0, fe_b0, fe_w1_bytes, fe_w1_scale, fe_b
         def leave(r, g, copy=nc.scalar.copy):
             (i0, s0), (i1, s1) = banks(r)[g][0], banks(r)[g][-1]
             if s0 == s1:
-                copy(out=out_half(r)[:, s0, :], in_=turned[r, g][:].rearrange("p i c -> p (i c)"))
+                copy(out=out_half(r)[:, s0, 0 : 128 * (i1 + 1)], in_=turned[r, g][:].rearrange("p i c -> p (i c)"))
                 store(r, s0, s0 + 1)
             else:
                 copy(out=out_half(r)[:, :, 128 * i0 : 128 * i0 + 128], in_=turned[r, g][:])
@@ -258,7 +274,7 @@ def tile_graph_gan_pa_kernel(tc, x, fe_w0, fe_b0, fe_w1_bytes, fe_w1_scale, fe_b
         def part_add(r, s0, s1, n0):
             h = rounds[r][1]
             shape = [P, s1 - s0, 512 - n0]
-            z = work.tile(shape, F32, name="part_sums")
+            z = work.tile(shape, F32, name="part_sums", bufs=3)
             bias = b1_spread[:, 512 * h + n0 : 512 * h + 512]
             nc.vector.tensor_tensor(out=z[:], in0=part_psum[r, s0][:], in1=bias.unsqueeze(1).to_broadcast(shape), op=ALU.add)
             part_sums[r, s0] = z
@@ -272,7 +288,7 @@ def tile_graph_gan_pa_kernel(tc, x, fe_w0, fe_b0, fe_w1_bytes, fe_w1_scale, fe_b
 
         w1_widen(0)
         w1_weave(0, 0)
-        w1_weave(0, 1)
+        w1_lay_gpsimd(0, 1)
         e1_add(0, 0, 8)
         w1_widen(1)
         nc.scalar.activation(out=b1_fifth[:], in_=b1_turned[:, 0:8], func=ACT.Copy, scale=ALPHA)
@@ -280,12 +296,10 @@ def tile_graph_gan_pa_kernel(tc, x, fe_w0, fe_b0, fe_w1_bytes, fe_w1_scale, fe_b
         w1_weave(1, 0)
         e1_add(0, 8, 16)
         w1_leave(0, 0)
-        w1_leave(0, 1)
-        w1_weave(1, 1)
+        w1_lay(1, 1)
         e1_lrelu(0, 0, 8)
         w1_quantise(0)
         w1_leave(1, 0)
-        w1_leave(1, 1)
         nc.scalar.copy(out=v_sb[:], in_=v_psum)
         e1_quantise(0, 0, 1)
         tile_products(0)
@@ -296,23 +310,23 @@ def tile_graph_gan_pa_kernel(tc, x, fe_w0, fe_b0, fe_w1_bytes, fe_w1_scale, fe_b
         e1_add(1, 0, FIRST_CUT)
 
         last = n_rounds - 1
-        leaving = [[], [], [0], [1, 2]] + [[r - 1] for r in range(4, n_rounds)]
+        leaving = [[], [], [], [0, 1, 2]] + [[r - 1] for r in range(4, n_rounds)]
         for r in range(n_rounds):
             k, h, n, b0, b1, parts = rounds[r]
             affine(r)
             if r == 0:
                 relu(r, 0, n)
-                e1_lrelu(1, 0, FIRST_CUT)
             elif r == 1:
                 relu(r, 0, n)
-                e1_lrelu(1, FIRST_CUT, 16)
+                e1_lrelu(1, 0, FIRST_CUT)
             elif r == 2:
                 relu(r, 0, n)
-                e1_quantise(1, 0, 2)
-                e1_add_gpsimd(2, FIRST_CUT, 16)
-                e1_add(2, 0, FIRST_CUT)
+                e1_lrelu(1, FIRST_CUT, 16)
             elif r == 3:
                 relu(r, 0, n)
+                e1_quantise(1, 0, 2)
+                e1_add_gpsimd(2, SECOND_CUT, 16)
+                e1_add(2, 0, SECOND_CUT)
             elif r == last:
                 part_add(r, *parts[0])
                 relu(r, 0, n)
@@ -324,24 +338,28 @@ def tile_graph_gan_pa_kernel(tc, x, fe_w0, fe_b0, fe_w1_bytes, fe_w1_scale, fe_b
                 part_lrelu(r, *parts[1])
                 relu(r, 0, n)
             elif h == 0:
-                cut = FIRST_CUT if k == 1 else CUT
+                cut = SECOND_CUT if k == 1 else CUT
                 part_add(r, *parts[0])
                 if k > 1:
                     part_lrelu(r - 1, *rounds[r - 1][5][0])
                 e1_lrelu(k + 1, 0, cut)
-                relu(r, 0, n)
+                relu_scalar_half(r)
+                relu(r, 0, 2)
+                nc.vector.tensor_scalar(out=r_sb[r][:, 2, 0:256], in0=a_sb[r][:, 2, 0:256], scalar1=4.0, scalar2=0.0, op0=ALU.mult, op1=ALU.max)
                 e1_lrelu(k + 1, cut, 16)
             else:
                 relu_scalar(r, 2)
                 part_lrelu(r - 1, *rounds[r - 1][5][0])
-                relu(r, 0, 2)
-                e1_quantise(k + 1, 0, 2)
                 if k + 2 < CHUNKS:
+                    relu(r, 0, 2)
+                    e1_quantise(k + 1, 0, 2)
                     e1_add_gpsimd(k + 2, CUT, 16)
-                part_add(r, *parts[0])
-                if k + 2 < CHUNKS:
+                    part_add(r, *parts[0])
                     e1_add(k + 2, 0, CUT)
                 else:
+                    e1_quantise(k + 1, 0, 2)
+                    part_add(r, *parts[0])
+                    relu(r, 0, 2)
                     part_lrelu(r, *parts[0])
             for q in leaving[r]:
                 for g in range(len(banks(q))):
@@ -355,16 +373,16 @@ def tile_graph_gan_pa_kernel(tc, x, fe_w0, fe_b0, fe_w1_bytes, fe_w1_scale, fe_b
             if r == last:
                 leave(r - 1, 0)
                 part_lrelu(r, *parts[0])
+                part_add(r, *parts[2])
                 leave(r - 1, 1)
                 part_lrelu(r, *parts[1])
             else:
                 for q in leaving[r]:
                     for g in range(len(banks(q))):
                         leave(q, g)
-                    if rounds[q][2] == 3:
+                    if len(banks(q)) == 3:
                         store(q, 0, 2)
                         store(q, 2, 4)
         turn(last, 0)
-        turn(last, 1)
         leave(last, 0)
-        leave(last, 1, nc.vector.tensor_copy)
+        part_lrelu(last, *parts[2])

@@ -19,10 +19,12 @@ CHUNKS = 8
 PAIRS = 512
 OUT_BUFFERS = 11
 W0_VECTOR = 80
-CUT = 11
+CUT = 10
 FIRST_CUT = 13
 SECOND_CUT = 12
 STRIP_ROUNDS = 4
+END_RELU = [2, 4, 4]
+END_BLOCKS = [2, 2, 2]
 
 
 def tile_graph_gan_pa_kernel(tc, x, fe_w0, fe_b0, fe_w1_bytes, fe_w1_scale, fe_b1, out):
@@ -185,8 +187,9 @@ def tile_graph_gan_pa_kernel(tc, x, fe_w0, fe_b0, fe_w1_bytes, fe_w1_scale, fe_b
         rounds = [(0, 0, 4, 0, 2, []), (0, 1, 4, 0, 2, []), (0, 0, 4, 2, 4, []), (0, 1, 4, 2, 4, [])]
         for k in range(1, CHUNKS):
             for h in range(2):
-                if k == CHUNKS - 1:
-                    rounds.append((k, h, 4, 0, 2 - h, [(s, s + 1, 0) for s in range(2 - h, 4)]))
+                if 2 * k + h >= 2 * CHUNKS - 3:
+                    nb = END_BLOCKS[2 * k + h - 2 * CHUNKS + 3]
+                    rounds.append((k, h, 4, 0, nb, [(s, s + 1, 0) for s in range(nb, 4)]))
                 else:
                     rounds.append((k, h, 3, 0, 4, [(0, 4, 384)]))
         n_rounds = len(rounds)
@@ -245,6 +248,13 @@ def tile_graph_gan_pa_kernel(tc, x, fe_w0, fe_b0, fe_w1_bytes, fe_w1_scale, fe_b
         def relu_scalar_half(r):
             c = 4 * rounds[r][1] + 2
             nc.scalar.activation(out=r_sb[r][:, 2, 256:512], in_=tile_psum[r, 2][:, 256:512], func=ACT.Relu, bias=b1_four_fifths[:, c : c + 1], scale=4 * ALPHA)
+
+        def end_relu(r):
+            own = END_RELU[r - n_rounds + 3]
+            for i in range(own, 4):
+                relu_scalar(r, i)
+            if own:
+                relu(r, 0, own)
 
         def banks(r):
             n, b0, b1 = rounds[r][2:5]
@@ -329,14 +339,12 @@ def tile_graph_gan_pa_kernel(tc, x, fe_w0, fe_b0, fe_w1_bytes, fe_w1_scale, fe_b
                 e1_add(2, 0, SECOND_CUT)
             elif r == last:
                 part_add(r, *parts[0])
-                relu(r, 0, n)
+                end_relu(r)
                 part_add(r, *parts[1])
             elif k == CHUNKS - 1:
                 part_add(r, *parts[0])
                 part_add(r, *parts[1])
-                part_lrelu(r, *parts[0])
-                part_lrelu(r, *parts[1])
-                relu(r, 0, n)
+                end_relu(r)
             elif h == 0:
                 cut = SECOND_CUT if k == 1 else CUT
                 part_add(r, *parts[0])
@@ -347,42 +355,36 @@ def tile_graph_gan_pa_kernel(tc, x, fe_w0, fe_b0, fe_w1_bytes, fe_w1_scale, fe_b
                 relu(r, 0, 2)
                 nc.vector.tensor_scalar(out=r_sb[r][:, 2, 0:256], in0=a_sb[r][:, 2, 0:256], scalar1=4.0, scalar2=0.0, op0=ALU.mult, op1=ALU.max)
                 e1_lrelu(k + 1, cut, 16)
-            else:
+            elif k + 2 < CHUNKS:
                 relu_scalar(r, 2)
                 part_lrelu(r - 1, *rounds[r - 1][5][0])
-                if k + 2 < CHUNKS:
-                    relu(r, 0, 2)
-                    e1_quantise(k + 1, 0, 2)
-                    e1_add_gpsimd(k + 2, CUT, 16)
-                    part_add(r, *parts[0])
-                    e1_add(k + 2, 0, CUT)
-                else:
-                    e1_quantise(k + 1, 0, 2)
-                    part_add(r, *parts[0])
-                    relu(r, 0, 2)
-                    part_lrelu(r, *parts[0])
+                e1_quantise(k + 1, 0, 2)
+                e1_add_gpsimd(k + 2, CUT, 16)
+                relu(r, 0, 2)
+                part_add(r, *parts[0])
+                e1_add(k + 2, 0, CUT)
+            else:
+                part_lrelu(r - 1, *rounds[r - 1][5][0])
+                e1_quantise(k + 1, 0, 2)
+                part_add(r, *parts[0])
+                part_add(r, *parts[1])
+                end_relu(r)
             for q in leaving[r]:
                 for g in range(len(banks(q))):
                     turn(q, g)
-            if r + 2 == last:
-                part_products(r + 1)
-                tile_products(r + 1)
-            elif r < last:
+            if r < last:
                 tile_products(r + 1)
                 part_products(r + 1)
-            if r == last:
-                leave(r - 1, 0)
+            for q in leaving[r]:
+                for g in range(len(banks(q))):
+                    leave(q, g)
+                if len(banks(q)) == 3:
+                    store(q, 0, 2)
+                    store(q, 2, 4)
+            if r >= last - 2:
                 part_lrelu(r, *parts[0])
-                part_add(r, *parts[2])
-                leave(r - 1, 1)
                 part_lrelu(r, *parts[1])
-            else:
-                for q in leaving[r]:
-                    for g in range(len(banks(q))):
-                        leave(q, g)
-                    if len(banks(q)) == 3:
-                        store(q, 0, 2)
-                        store(q, 2, 4)
         turn(last, 0)
+        turn(last, 1)
         leave(last, 0)
-        part_lrelu(last, *parts[2])
+        leave(last, 1)

@@ -17,14 +17,11 @@ FLOPS = 2 * 128 * 512 * 512 * 2 + 2 * 4096 * 512 * 1024
 ALPHA = 0.2
 CHUNKS = 8
 PAIRS = 512
+ROWS = 16
+OWN_ROWS = 10
+OWN_ROWS_AT_START = 13
+SCALAR_RELU = (256, 512)
 OUT_BUFFERS = 11
-W0_VECTOR = 80
-CUT = 10
-FIRST_CUT = 13
-SECOND_CUT = 12
-STRIP_ROUNDS = 4
-END_RELU = [2, 4, 4]
-END_BLOCKS = [2, 2, 2]
 
 
 def tile_graph_gan_pa_kernel(tc, x, fe_w0, fe_b0, fe_w1_bytes, fe_w1_scale, fe_b1, out):
@@ -90,11 +87,14 @@ def tile_graph_gan_pa_kernel(tc, x, fe_w0, fe_b0, fe_w1_bytes, fe_w1_scale, fe_b
         w0_laid = [keep.tile([P, 2048], BF16, name="w0_laid%d" % h, align_bytes=64) for h in range(2)]
         w0_mx = [mx_operand(keep, "w0_%d" % h, 512, 1) for h in range(2)]
 
-        def w0_lay(h):
+        def w0_lay(h, t0, t1, copy):
             dst = w0_laid[h][:].rearrange("p (t m j) -> p t m j", t=4, j=4)
             src = w0_raw[h][:].rearrange("p j (m t) -> p t m j", t=4)
-            nc.vector.tensor_copy(out=dst[:, :, 0:W0_VECTOR], in_=src[:, :, 0:W0_VECTOR])
-            nc.scalar.copy(out=dst[:, :, W0_VECTOR:], in_=src[:, :, W0_VECTOR:])
+            copy(out=dst[:, t0:t1], in_=src[:, t0:t1])
+
+        def w0_quantise(h, t0):
+            cols = slice(128 * t0, 128 * t0 + 256)
+            quantise(w0_mx[h][0][:, cols], w0_mx[h][1][:, cols], w0_laid[h][:, 512 * t0 : 512 * t0 + 1024])
 
         def first_layer(h):
             if h == 0:
@@ -106,12 +106,17 @@ def tile_graph_gan_pa_kernel(tc, x, fe_w0, fe_b0, fe_w1_bytes, fe_w1_scale, fe_b
             return acc[:].rearrange("p t n -> p n t")
 
         nc.vector.tensor_copy(out=x_laid[:].bitcast(F32).rearrange("p (n u) -> p n u", u=2), in_=x_turned[:].rearrange("p u n -> p n u"))
-        w0_lay(0)
+        w0_lay(0, 2, 4, nc.scalar.copy)
+        w0_lay(1, 3, 4, nc.scalar.copy)
+        w0_lay(0, 0, 2, nc.vector.tensor_copy)
         quantise(x_mx[0][:], x_mx[1][:], x_laid[:])
-        quantise(w0_mx[0][0][:], w0_mx[0][1][:], w0_laid[0][:])
-        w0_lay(1)
+        w0_quantise(0, 0)
+        w0_lay(1, 0, 2, nc.vector.tensor_copy)
+        w0_quantise(0, 2)
+        w0_lay(1, 2, 3, nc.vector.tensor_copy)
         u_psum = first_layer(0)
-        quantise(w0_mx[1][0][:], w0_mx[1][1][:], w0_laid[1][:])
+        w0_quantise(1, 0)
+        w0_quantise(1, 2)
         v_psum = first_layer(1)
         u_sb = keep.tile([P, P, 4], F32, name="u_sb")
         v_sb = keep.tile([P, P, 4], F32, name="v_sb")
@@ -145,7 +150,7 @@ def tile_graph_gan_pa_kernel(tc, x, fe_w0, fe_b0, fe_w1_bytes, fe_w1_scale, fe_b
             cols = slice(256 * g, 256 * g + 256)
             nc.gpsimd.tensor_scalar(out=w1_laid[q][:, cols, :], in0=w1_planes[q][:, :, cols].rearrange("p t n -> p n t"), scalar1=1.0, scalar2=0.0, op0=ALU.mult, op1=ALU.add)
 
-        def w1_lay(q, g):
+        def w1_lay_scalar(q, g):
             cols = slice(256 * g, 256 * g + 256)
             nc.scalar.copy(out=w1_laid[q][:, cols, :].rearrange("p (c i) t -> p c t i", i=4), in_=w1_planes[q][:, :, cols].rearrange("p t (c i) -> p c t i", i=4))
 
@@ -154,13 +159,17 @@ def tile_graph_gan_pa_kernel(tc, x, fe_w0, fe_b0, fe_w1_bytes, fe_w1_scale, fe_b
 
         pair_sums = {}
         e1_mx = {}
-        shared = [keep.tile([P, 4 * PAIRS], BF16, name="shared%d" % j, align_bytes=64) for j in range(2)]
+        e1_tiles = [keep.tile([P, 4 * PAIRS], BF16, name="e1_tile%d" % j, align_bytes=64) for j in range(2)]
+
+        def own_rows(k):
+            return OWN_ROWS_AT_START if k <= 2 else OWN_ROWS
 
         def pair_operands(k, i0, i1, v):
             graph = k // 2
-            n0 = 32 * graph + 16 * (k % 2)
+            n0 = 32 * graph + ROWS * (k % 2)
             shape = [P, i1 - i0, 32, 4]
-            return u_sb[:, n0 + i0 : n0 + i1, :].unsqueeze(2).to_broadcast(shape), v[:, 32 * graph : 32 * graph + 32, :].unsqueeze(1).to_broadcast(shape)
+            u_rows = u_sb[:, n0 + i0 : n0 + i1, :].unsqueeze(2).to_broadcast(shape)
+            return u_rows, v[:, 32 * graph : 32 * graph + 32, :].unsqueeze(1).to_broadcast(shape)
 
         def e1_add(k, i0, i1):
             z = work.tile([P, i1 - i0, 32, 4], F32, name="pair_sums")
@@ -168,31 +177,34 @@ def tile_graph_gan_pa_kernel(tc, x, fe_w0, fe_b0, fe_w1_bytes, fe_w1_scale, fe_b
             nc.vector.tensor_tensor(out=z[:], in0=in0, in1=in1, op=ALU.add)
             pair_sums[k, i0] = z[:].rearrange("p i j t -> p (i j t)")
 
-        def e1_add_gpsimd(k, i0, i1):
-            z = shared[(k + 1) % 2][:].bitcast(F32)[:, 1024 - 128 * (i1 - i0) : 1024]
-            in0, in1 = pair_operands(k, i0, i1, v_sb)
+        def e1_add_gpsimd(k):
+            i0 = own_rows(k)
+            z = e1_tiles[(k - 1) % 2][:].bitcast(F32)[:, 2 * PAIRS - 128 * (ROWS - i0) : 2 * PAIRS]
+            in0, in1 = pair_operands(k, i0, ROWS, v_sb)
             nc.gpsimd.tensor_tensor(out=z.rearrange("p (i j t) -> p i j t", j=32, t=4), in0=in0, in1=in1, op=ALU.add)
             pair_sums[k, i0] = z
 
         def e1_lrelu(k, i0, i1):
             z = pair_sums[k, i0]
-            nc.vector.scalar_tensor_tensor(out=shared[k % 2][:, 128 * i0 : 128 * i1], in0=z, scalar=ALPHA, in1=z, op0=ALU.mult, op1=ALU.max)
+            nc.vector.scalar_tensor_tensor(out=e1_tiles[k % 2][:, 128 * i0 : 128 * i1], in0=z, scalar=ALPHA, in1=z, op0=ALU.mult, op1=ALU.max)
 
-        def e1_quantise(k, g0, g1):
-            if g0 == 0:
+        def e1_quantise(k, i0, i1):
+            if i0 == 0:
                 e1_mx[k] = mx_operand(work, "e1", PAIRS, 2)
-            cols = slice(256 * g0, 256 * g1)
-            quantise(e1_mx[k][0][:, cols], e1_mx[k][1][:, cols], shared[k % 2][:, 1024 * g0 : 1024 * g1])
+            cols = slice(32 * i0, 32 * i1)
+            quantise(e1_mx[k][0][:, cols], e1_mx[k][1][:, cols], e1_tiles[k % 2][:, 128 * i0 : 128 * i1])
 
-        rounds = [(0, 0, 4, 0, 2, []), (0, 1, 4, 0, 2, []), (0, 0, 4, 2, 4, []), (0, 1, 4, 2, 4, [])]
+        opening = 4
+        closing = 3
+        rounds = [(0, h, 4, b0, b0 + 2, []) for b0 in (0, 2) for h in range(2)]
         for k in range(1, CHUNKS):
             for h in range(2):
-                if 2 * k + h >= 2 * CHUNKS - 3:
-                    nb = END_BLOCKS[2 * k + h - 2 * CHUNKS + 3]
-                    rounds.append((k, h, 4, 0, nb, [(s, s + 1, 0) for s in range(nb, 4)]))
-                else:
+                if 2 * k + h < 2 * CHUNKS - closing:
                     rounds.append((k, h, 3, 0, 4, [(0, 4, 384)]))
-        n_rounds = len(rounds)
+                else:
+                    rounds.append((k, h, 4, 0, 2, [(2, 3, 0), (3, 4, 0)]))
+        last = len(rounds) - 1
+        v_done = last - closing - 1
         tile_psum = {}
         part_psum = {}
         a_sb = {}
@@ -212,179 +224,167 @@ def tile_graph_gan_pa_kernel(tc, x, fe_w0, fe_b0, fe_w1_bytes, fe_w1_scale, fe_b
             dst = rows[PAIRS * k + 128 * s0 : PAIRS * k + 128 * s1, 512 * h : 512 * h + 512]
             nc.sync.dma_start(out=dst.rearrange("(s p) c -> p s c", p=P), in_=out_half(r)[:, s0:s1, :])
 
-        def tile_products(r):
+        def products(r):
             k, h, n, b0, b1, parts = rounds[r]
-            nb = b1 - b0
-            per_bank = 4 // nb
+            per_bank = 4 // (b1 - b0)
             for i0 in range(0, n, per_bank):
-                acc = psum.tile([P, per_bank, 128 * nb], F32, name="tile_psum", tag="product")
+                acc = psum.tile([P, per_bank, 128 * (b1 - b0)], F32, name="tile_psum", tag="product")
                 for i in range(i0, i0 + per_bank):
                     product(acc[:, i - i0, :], w1_mx[h], slice(128 * i, 128 * i + 128), e1_mx[k], slice(128 * b0, 128 * b1))
                     tile_psum[r, i] = acc[:, i - i0, :]
-
-        def part_products(r):
-            k, h, n, b0, b1, parts = rounds[r]
             for s0, s1, n0 in parts:
                 acc = psum.tile([P, s1 - s0, 512 - n0], F32, name="part_psum", tag="product")
                 for s in range(s0, s1):
                     product(acc[:, s - s0, :], e1_mx[k], slice(128 * s, 128 * s + 128), w1_mx[h], slice(n0, 512))
                 part_psum[r, s0] = acc
 
+        def tile_width(r):
+            return 128 * (rounds[r][4] - rounds[r][3])
+
         def affine(r):
-            k, h, n, b0, b1, parts = rounds[r]
-            a_sb[r] = work.tile([P, n, 128 * (b1 - b0)], F32, name="a_sb", bufs=4)
-            r_sb[r] = work.tile([P, n, 128 * (b1 - b0)], F32, name="r_sb", bufs=4)
+            k, h, n = rounds[r][0:3]
+            w = tile_width(r)
+            a_sb[r] = work.tile([P, n * w], F32, name="a_sb", bufs=opening)
+            r_sb[r] = work.tile([P, n * w], F32, name="r_sb", bufs=opening)
             for i in range(n):
                 c = 4 * h + i
-                nc.scalar.activation(out=a_sb[r][:, i, :], in_=tile_psum[r, i], func=ACT.Identity, bias=b1_fifth[:, c : c + 1], scale=ALPHA)
+                nc.scalar.activation(out=a_sb[r][:, w * i : w * i + w], in_=tile_psum[r, i], func=ACT.Identity, bias=b1_fifth[:, c : c + 1], scale=ALPHA)
 
-        def relu(r, i0, i1):
-            nc.vector.tensor_scalar(out=r_sb[r][:, i0:i1, :], in0=a_sb[r][:, i0:i1, :], scalar1=4.0, scalar2=0.0, op0=ALU.mult, op1=ALU.max)
+        def relu_vector(r, end):
+            nc.vector.tensor_scalar(out=r_sb[r][:, 0:end], in0=a_sb[r][:, 0:end], scalar1=4.0, scalar2=0.0, op0=ALU.mult, op1=ALU.max)
 
-        def relu_scalar(r, i):
+        def relu_scalar(r, i, width):
             c = 4 * rounds[r][1] + i
-            nc.scalar.activation(out=r_sb[r][:, i, :], in_=tile_psum[r, i], func=ACT.Relu, bias=b1_four_fifths[:, c : c + 1], scale=4 * ALPHA)
-
-        def relu_scalar_half(r):
-            c = 4 * rounds[r][1] + 2
-            nc.scalar.activation(out=r_sb[r][:, 2, 256:512], in_=tile_psum[r, 2][:, 256:512], func=ACT.Relu, bias=b1_four_fifths[:, c : c + 1], scale=4 * ALPHA)
-
-        def end_relu(r):
-            own = END_RELU[r - n_rounds + 3]
-            for i in range(own, 4):
-                relu_scalar(r, i)
-            if own:
-                relu(r, 0, own)
+            w = tile_width(r)
+            nc.scalar.activation(out=r_sb[r][:, w * i + w - width : w * i + w], in_=tile_psum[r, i][:, w - width : w], func=ACT.Relu, bias=b1_four_fifths[:, c : c + 1], scale=4 * ALPHA)
 
         def banks(r):
             n, b0, b1 = rounds[r][2:5]
-            if n == 3 and r < n_rounds - STRIP_ROUNDS:
-                return [[(i, s) for s in range(b0, b1)] for i in range(n)]
+            if b1 - b0 == 4 and r < v_done:
+                return [[(i, s) for s in (0, 1) for i in (0, 1)], [(2, s) for s in range(4)], [(i, s) for s in (2, 3) for i in (0, 1)]]
             return [[(i, s) for i in range(n)] for s in range(b0, b1)]
 
         def turn(r, g):
             b0 = rounds[r][3]
-            if g < 3 or len(banks(r)) == 3:
-                acc = psum.tile([P, len(banks(r)[g]), P], F32, name="turned", tag="turned", bufs=3)
+            held = banks(r)[g]
+            if g < 3:
+                acc = psum.tile([P, len(held), P], F32, name="turned", tag="turned", bufs=3)
             else:
-                acc = psum.tile([P, len(banks(r)[g]), P], F32, name="turned_last", tag="v", bufs=1)
-            for j, (i, s) in enumerate(banks(r)[g]):
+                acc = psum.tile([P, len(held), P], F32, name="turned_fourth", tag="v", bufs=1)
+            for j, (i, s) in enumerate(held):
+                c0 = tile_width(r) * i + 128 * (s - b0)
                 for m, src in enumerate((a_sb[r], r_sb[r])):
-                    nc.tensor.matmul(acc[:, j, :], lhsT=src[:, i, 128 * (s - b0) : 128 * (s - b0) + 128], rhs=ident[:], is_transpose=True, start=(m == 0), stop=(m == 1))
+                    nc.tensor.matmul(acc[:, j, :], lhsT=src[:, c0 : c0 + 128], rhs=ident[:], is_transpose=True, start=(m == 0), stop=(m == 1))
             turned[r, g] = acc
 
-        def leave(r, g, copy=nc.scalar.copy):
+        def leave(r, g):
             (i0, s0), (i1, s1) = banks(r)[g][0], banks(r)[g][-1]
+            bank = turned[r, g][:].rearrange("p j c -> p (j c)").rearrange("p (s c) -> p s c", s=s1 + 1 - s0)
+            nc.scalar.copy(out=out_half(r)[:, s0 : s1 + 1, 128 * i0 : 128 * i1 + 128], in_=bank)
             if s0 == s1:
-                copy(out=out_half(r)[:, s0, 0 : 128 * (i1 + 1)], in_=turned[r, g][:].rearrange("p i c -> p (i c)"))
                 store(r, s0, s0 + 1)
-            else:
-                copy(out=out_half(r)[:, :, 128 * i0 : 128 * i0 + 128], in_=turned[r, g][:])
+            elif g > 0:
+                store(r, 2 * g - 2, 2 * g)
 
-        def part_add(r, s0, s1, n0):
+        def part_add(r, j):
+            s0, s1, n0 = rounds[r][5][j]
             h = rounds[r][1]
             shape = [P, s1 - s0, 512 - n0]
             z = work.tile(shape, F32, name="part_sums", bufs=3)
             bias = b1_spread[:, 512 * h + n0 : 512 * h + 512]
             nc.vector.tensor_tensor(out=z[:], in0=part_psum[r, s0][:], in1=bias.unsqueeze(1).to_broadcast(shape), op=ALU.add)
-            part_sums[r, s0] = z
+            part_sums[r, j] = z
 
-        def part_lrelu(r, s0, s1, n0):
-            z = part_sums[r, s0][:]
+        def part_lrelu(r, j):
+            s0, s1, n0 = rounds[r][5][j]
+            z = part_sums[r, j][:]
             nc.vector.scalar_tensor_tensor(out=out_half(r)[:, s0:s1, n0:512], in0=z, scalar=ALPHA, in1=z, op0=ALU.mult, op1=ALU.max)
             if n0 == 0:
                 store(r, s0, s1)
 
-
+        half = ROWS // 2
         w1_widen(0)
         w1_weave(0, 0)
         w1_lay_gpsimd(0, 1)
-        e1_add(0, 0, 8)
+        e1_add(0, 0, half)
         w1_widen(1)
         nc.scalar.activation(out=b1_fifth[:], in_=b1_turned[:, 0:8], func=ACT.Copy, scale=ALPHA)
         nc.scalar.activation(out=b1_four_fifths[:], in_=b1_turned[:, 0:8], func=ACT.Copy, scale=4 * ALPHA)
         w1_weave(1, 0)
-        e1_add(0, 8, 16)
+        e1_add(0, half, ROWS)
         w1_leave(0, 0)
-        w1_lay(1, 1)
-        e1_lrelu(0, 0, 8)
+        w1_lay_scalar(1, 1)
+        e1_lrelu(0, 0, half)
         w1_quantise(0)
         w1_leave(1, 0)
         nc.scalar.copy(out=v_sb[:], in_=v_psum)
-        e1_quantise(0, 0, 1)
-        tile_products(0)
-        e1_lrelu(0, 8, 16)
+        e1_quantise(0, 0, half)
+        products(0)
+        e1_lrelu(0, half, ROWS)
         w1_quantise(1)
-        e1_quantise(0, 1, 2)
-        e1_add_gpsimd(1, FIRST_CUT, 16)
-        e1_add(1, 0, FIRST_CUT)
+        e1_quantise(0, half, ROWS)
+        e1_add_gpsimd(1)
+        e1_add(1, 0, own_rows(1))
 
-        last = n_rounds - 1
-        leaving = [[], [], [], [0, 1, 2]] + [[r - 1] for r in range(4, n_rounds)]
-        for r in range(n_rounds):
-            k, h, n, b0, b1, parts = rounds[r]
+        leaving = [[] for r in range(opening - 1)] + [list(range(opening - 1))] + [[r - 1] for r in range(opening, last + 1)]
+        for r in range(last + 1):
+            k, h, n = rounds[r][0:3]
+            width = n * tile_width(r)
             affine(r)
-            if r == 0:
-                relu(r, 0, n)
-            elif r == 1:
-                relu(r, 0, n)
-                e1_lrelu(1, 0, FIRST_CUT)
-            elif r == 2:
-                relu(r, 0, n)
-                e1_lrelu(1, FIRST_CUT, 16)
-            elif r == 3:
-                relu(r, 0, n)
-                e1_quantise(1, 0, 2)
-                e1_add_gpsimd(2, SECOND_CUT, 16)
-                e1_add(2, 0, SECOND_CUT)
-            elif r == last:
-                part_add(r, *parts[0])
-                end_relu(r)
-                part_add(r, *parts[1])
-            elif k == CHUNKS - 1:
-                part_add(r, *parts[0])
-                part_add(r, *parts[1])
-                end_relu(r)
-            elif h == 0:
-                cut = SECOND_CUT if k == 1 else CUT
-                part_add(r, *parts[0])
-                if k > 1:
-                    part_lrelu(r - 1, *rounds[r - 1][5][0])
-                e1_lrelu(k + 1, 0, cut)
-                relu_scalar_half(r)
-                relu(r, 0, 2)
-                nc.vector.tensor_scalar(out=r_sb[r][:, 2, 0:256], in0=a_sb[r][:, 2, 0:256], scalar1=4.0, scalar2=0.0, op0=ALU.mult, op1=ALU.max)
-                e1_lrelu(k + 1, cut, 16)
-            elif k + 2 < CHUNKS:
-                relu_scalar(r, 2)
-                part_lrelu(r - 1, *rounds[r - 1][5][0])
-                e1_quantise(k + 1, 0, 2)
-                e1_add_gpsimd(k + 2, CUT, 16)
-                relu(r, 0, 2)
-                part_add(r, *parts[0])
-                e1_add(k + 2, 0, CUT)
+            if r < opening:
+                relu_vector(r, width)
+                if r == 1:
+                    e1_lrelu(1, 0, own_rows(1))
+                elif r == 2:
+                    e1_lrelu(1, own_rows(1), ROWS)
+                elif r == 3:
+                    e1_quantise(1, 0, ROWS)
+                    e1_add_gpsimd(2)
+                    e1_add(2, 0, own_rows(2))
+            elif r <= last - closing and h == 0:
+                part_add(r, 0)
+                if r > opening:
+                    part_lrelu(r - 1, 0)
+                e1_lrelu(k + 1, 0, own_rows(k + 1))
+                relu_scalar(r, n - 1, SCALAR_RELU[h])
+                relu_vector(r, width - SCALAR_RELU[h])
+                e1_lrelu(k + 1, own_rows(k + 1), ROWS)
+            elif r <= last - closing:
+                relu_scalar(r, n - 1, SCALAR_RELU[h])
+                part_lrelu(r - 1, 0)
+                e1_quantise(k + 1, 0, ROWS)
+                e1_add_gpsimd(k + 2)
+                relu_vector(r, width - SCALAR_RELU[h])
+                part_add(r, 0)
+                e1_add(k + 2, 0, own_rows(k + 2))
+            elif r == last - 2:
+                part_lrelu(r - 1, 0)
+                e1_quantise(k + 1, 0, ROWS)
+                part_add(r, 0)
+                part_add(r, 1)
+                relu_vector(r, width)
+            elif r == last - 1:
+                part_add(r, 0)
+                part_add(r, 1)
+                relu_scalar(r, 2, tile_width(r))
+                relu_scalar(r, 3, tile_width(r))
+                relu_vector(r, width // 2)
             else:
-                part_lrelu(r - 1, *rounds[r - 1][5][0])
-                e1_quantise(k + 1, 0, 2)
-                part_add(r, *parts[0])
-                part_add(r, *parts[1])
-                end_relu(r)
+                part_add(r, 0)
+                relu_vector(r, width)
+                part_add(r, 1)
             for q in leaving[r]:
                 for g in range(len(banks(q))):
                     turn(q, g)
             if r < last:
-                tile_products(r + 1)
-                part_products(r + 1)
+                products(r + 1)
             for q in leaving[r]:
                 for g in range(len(banks(q))):
                     leave(q, g)
-                if len(banks(q)) == 3:
-                    store(q, 0, 2)
-                    store(q, 2, 4)
-            if r >= last - 2:
-                part_lrelu(r, *parts[0])
-                part_lrelu(r, *parts[1])
-        turn(last, 0)
-        turn(last, 1)
-        leave(last, 0)
-        leave(last, 1)
+            if r > last - closing:
+                part_lrelu(r, 0)
+                part_lrelu(r, 1)
+        for g in range(len(banks(last))):
+            turn(last, g)
+        for g in range(len(banks(last))):
+            leave(last, g)

@@ -18,9 +18,9 @@ ALPHA = 0.2
 CHUNKS = 8
 PAIRS = 512
 ROWS = 16
-OWN_ROWS = 10
+OWN_ROWS = 8
 OWN_ROWS_AT_START = 13
-SCALAR_RELU = (256, 512)
+SCALAR_RELU = 640
 OUT_BUFFERS = 11
 
 
@@ -199,8 +199,10 @@ def tile_graph_gan_pa_kernel(tc, x, fe_w0, fe_b0, fe_w1_bytes, fe_w1_scale, fe_b
         rounds = [(0, h, 4, b0, b0 + 2, []) for b0 in (0, 2) for h in range(2)]
         for k in range(1, CHUNKS):
             for h in range(2):
-                if 2 * k + h < 2 * CHUNKS - closing:
+                if 2 * k + h < 2 * CHUNKS - closing and h == 0:
                     rounds.append((k, h, 3, 0, 4, [(0, 4, 384)]))
+                elif 2 * k + h < 2 * CHUNKS - closing:
+                    rounds.append((k, h, 2, 0, 4, [(0, 2, 256), (2, 4, 256)]))
                 else:
                     rounds.append((k, h, 4, 0, 2, [(2, 3, 0), (3, 4, 0)]))
         last = len(rounds) - 1
@@ -260,6 +262,8 @@ def tile_graph_gan_pa_kernel(tc, x, fe_w0, fe_b0, fe_w1_bytes, fe_w1_scale, fe_b
 
         def banks(r):
             n, b0, b1 = rounds[r][2:5]
+            if n == 2:
+                return [[(i, s) for s in (s0, s0 + 1) for i in (0, 1)] for s0 in (0, 2)]
             if b1 - b0 == 4 and r < v_done:
                 return [[(i, s) for s in (0, 1) for i in (0, 1)], [(2, s) for s in range(4)], [(i, s) for s in (2, 3) for i in (0, 1)]]
             return [[(i, s) for i in range(n)] for s in range(b0, b1)]
@@ -283,6 +287,8 @@ def tile_graph_gan_pa_kernel(tc, x, fe_w0, fe_b0, fe_w1_bytes, fe_w1_scale, fe_b
             nc.scalar.copy(out=out_half(r)[:, s0 : s1 + 1, 128 * i0 : 128 * i1 + 128], in_=bank)
             if s0 == s1:
                 store(r, s0, s0 + 1)
+            elif rounds[r][2] == 2:
+                store(r, s0, s1 + 1)
             elif g > 0:
                 store(r, 2 * g - 2, 2 * g)
 
@@ -290,7 +296,7 @@ def tile_graph_gan_pa_kernel(tc, x, fe_w0, fe_b0, fe_w1_bytes, fe_w1_scale, fe_b
             s0, s1, n0 = rounds[r][5][j]
             h = rounds[r][1]
             shape = [P, s1 - s0, 512 - n0]
-            z = work.tile(shape, F32, name="part_sums", bufs=3)
+            z = work.tile(shape, F32, name="part_sums", bufs=4)
             bias = b1_spread[:, 512 * h + n0 : 512 * h + 512]
             nc.vector.tensor_tensor(out=z[:], in0=part_psum[r, s0][:], in1=bias.unsqueeze(1).to_broadcast(shape), op=ALU.add)
             part_sums[r, j] = z
@@ -345,17 +351,22 @@ def tile_graph_gan_pa_kernel(tc, x, fe_w0, fe_b0, fe_w1_bytes, fe_w1_scale, fe_b
                 part_add(r, 0)
                 if r > opening:
                     part_lrelu(r - 1, 0)
-                e1_lrelu(k + 1, 0, own_rows(k + 1))
-                relu_scalar(r, n - 1, SCALAR_RELU[h])
-                relu_vector(r, width - SCALAR_RELU[h])
                 e1_lrelu(k + 1, own_rows(k + 1), ROWS)
+                if SCALAR_RELU > 512:
+                    relu_scalar(r, 1, SCALAR_RELU - 512)
+                relu_scalar(r, 2, min(SCALAR_RELU, 512))
+                relu_vector(r, width - SCALAR_RELU)
+                e1_lrelu(k + 1, 0, own_rows(k + 1))
+                if r > opening:
+                    part_lrelu(r - 1, 1)
             elif r <= last - closing:
-                relu_scalar(r, n - 1, SCALAR_RELU[h])
-                part_lrelu(r - 1, 0)
+                relu_scalar(r, 0, 512)
+                relu_scalar(r, 1, 512)
                 e1_quantise(k + 1, 0, ROWS)
                 e1_add_gpsimd(k + 2)
-                relu_vector(r, width - SCALAR_RELU[h])
+                part_lrelu(r - 1, 0)
                 part_add(r, 0)
+                part_add(r, 1)
                 e1_add(k + 2, 0, own_rows(k + 2))
             elif r == last - 2:
                 part_lrelu(r - 1, 0)

@@ -19,7 +19,17 @@ CHUNKS = 8
 PAIRS = 512
 ROWS = 16
 OWN_ROWS = 8
-OWN_ROWS_AT_START = 13
+OWN1 = 9
+OWN2 = 10
+R0_RELU = 1024
+R1_RELU = 0
+R14_RELU = 640
+R15_RELU = 0
+R16_RELU = 512
+R17_RELU = 0
+LAST_TURNED = 2
+EARLY14 = 3
+RELU_FIRST = 0
 SCALAR_RELU = 640
 OUT_BUFFERS = 11
 
@@ -162,7 +172,7 @@ def tile_graph_gan_pa_kernel(tc, x, fe_w0, fe_b0, fe_w1_bytes, fe_w1_scale, fe_b
         e1_tiles = [keep.tile([P, 4 * PAIRS], BF16, name="e1_tile%d" % j, align_bytes=64) for j in range(2)]
 
         def own_rows(k):
-            return OWN_ROWS_AT_START if k <= 2 else OWN_ROWS
+            return OWN1 if k == 1 else (OWN2 if k == 2 else OWN_ROWS)
 
         def pair_operands(k, i0, i1, v):
             graph = k // 2
@@ -179,7 +189,8 @@ def tile_graph_gan_pa_kernel(tc, x, fe_w0, fe_b0, fe_w1_bytes, fe_w1_scale, fe_b
 
         def e1_add_gpsimd(k):
             i0 = own_rows(k)
-            z = e1_tiles[(k - 1) % 2][:].bitcast(F32)[:, 2 * PAIRS - 128 * (ROWS - i0) : 2 * PAIRS]
+            home = w0_laid[0] if k == 1 else e1_tiles[(k - 1) % 2]
+            z = home[:].bitcast(F32)[:, 2 * PAIRS - 128 * (ROWS - i0) : 2 * PAIRS]
             in0, in1 = pair_operands(k, i0, ROWS, v_sb)
             nc.gpsimd.tensor_tensor(out=z.rearrange("p (i j t) -> p i j t", j=32, t=4), in0=in0, in1=in1, op=ALU.add)
             pair_sums[k, i0] = z
@@ -194,19 +205,16 @@ def tile_graph_gan_pa_kernel(tc, x, fe_w0, fe_b0, fe_w1_bytes, fe_w1_scale, fe_b
             cols = slice(32 * i0, 32 * i1)
             quantise(e1_mx[k][0][:, cols], e1_mx[k][1][:, cols], e1_tiles[k % 2][:, 128 * i0 : 128 * i1])
 
-        opening = 4
-        closing = 3
-        rounds = [(0, h, 4, b0, b0 + 2, []) for b0 in (0, 2) for h in range(2)]
-        for k in range(1, CHUNKS):
-            for h in range(2):
-                if 2 * k + h < 2 * CHUNKS - closing and h == 0:
-                    rounds.append((k, h, 3, 0, 4, [(0, 4, 384)]))
-                elif 2 * k + h < 2 * CHUNKS - closing:
-                    rounds.append((k, h, 2, 0, 4, [(0, 2, 256), (2, 4, 256)]))
-                else:
-                    rounds.append((k, h, 4, 0, 2, [(2, 3, 0), (3, 4, 0)]))
+        opening = 3
+        rounds = [(0, 0, 4, 0, 2, [(0, 2, 3, 0), (0, 3, 4, 0)]), (0, 1, 4, 0, 2, []), (0, 1, 4, 2, 4, [])]
+        for k in range(1, CHUNKS - 1):
+            rounds.append((k, 0, 3, 0, 4, [(0, 0, 4, 384)]))
+            rounds.append((k, 1, 2, 0, 4, [(1, 0, 2, 256), (1, 2, 4, 256)]))
+        rounds[-1] = (CHUNKS - 2, 1, 4, 0, 2, [(1, 2, 3, 0), (1, 3, 4, 0)])
+        rounds.append((CHUNKS - 1, 0, 4, 0, 2, [(1, 0, 1, 0), (1, 1, 2, 0)]))
+        rounds.append((CHUNKS - 1, 0, 4, 2, 2 + LAST_TURNED, [(0, s, s + 1, 0) for s in range(2 + LAST_TURNED, 4)] + [(1, 2, 3, 0), (1, 3, 4, 0)]))
         last = len(rounds) - 1
-        v_done = last - closing - 1
+        v_done = last - 3
         tile_psum = {}
         part_psum = {}
         a_sb = {}
@@ -215,18 +223,16 @@ def tile_graph_gan_pa_kernel(tc, x, fe_w0, fe_b0, fe_w1_bytes, fe_w1_scale, fe_b
         part_sums = {}
         out_sb = {}
 
-        def out_half(r):
-            key = rounds[r][0:2]
-            if key not in out_sb:
-                out_sb[key] = work.tile([P, 4, 512], F32, name="out_sb", bufs=OUT_BUFFERS)
-            return out_sb[key]
+        def out_half(k, h):
+            if (k, h) not in out_sb:
+                out_sb[k, h] = work.tile([P, 4, 512], F32, name="out_sb", bufs=OUT_BUFFERS)
+            return out_sb[k, h]
 
-        def store(r, s0, s1):
-            k, h = rounds[r][0:2]
+        def store(k, h, s0, s1):
             dst = rows[PAIRS * k + 128 * s0 : PAIRS * k + 128 * s1, 512 * h : 512 * h + 512]
-            nc.sync.dma_start(out=dst.rearrange("(s p) c -> p s c", p=P), in_=out_half(r)[:, s0:s1, :])
+            nc.sync.dma_start(out=dst.rearrange("(s p) c -> p s c", p=P), in_=out_half(k, h)[:, s0:s1, :])
 
-        def products(r):
+        def tile_products(r):
             k, h, n, b0, b1, parts = rounds[r]
             per_bank = 4 // (b1 - b0)
             for i0 in range(0, n, per_bank):
@@ -234,25 +240,35 @@ def tile_graph_gan_pa_kernel(tc, x, fe_w0, fe_b0, fe_w1_bytes, fe_w1_scale, fe_b
                 for i in range(i0, i0 + per_bank):
                     product(acc[:, i - i0, :], w1_mx[h], slice(128 * i, 128 * i + 128), e1_mx[k], slice(128 * b0, 128 * b1))
                     tile_psum[r, i] = acc[:, i - i0, :]
-            for s0, s1, n0 in parts:
+
+        def part_products(r):
+            k = rounds[r][0]
+            for j, (h, s0, s1, n0) in enumerate(rounds[r][5]):
                 acc = psum.tile([P, s1 - s0, 512 - n0], F32, name="part_psum", tag="product")
                 for s in range(s0, s1):
                     product(acc[:, s - s0, :], e1_mx[k], slice(128 * s, 128 * s + 128), w1_mx[h], slice(n0, 512))
-                part_psum[r, s0] = acc
+                part_psum[r, j] = acc
+
+        def products(r):
+            tile_products(r)
+            part_products(r)
 
         def tile_width(r):
             return 128 * (rounds[r][4] - rounds[r][3])
 
-        def affine(r):
+        def affine(r, i0, i1):
             k, h, n = rounds[r][0:3]
             w = tile_width(r)
-            a_sb[r] = work.tile([P, n * w], F32, name="a_sb", bufs=opening)
-            r_sb[r] = work.tile([P, n * w], F32, name="r_sb", bufs=opening)
-            for i in range(n):
+            if i0 == 0:
+                a_sb[r] = work.tile([P, n * w], F32, name="a_sb", bufs=3)
+                r_sb[r] = work.tile([P, n * w], F32, name="r_sb", bufs=3)
+            for i in range(i0, i1):
                 c = 4 * h + i
                 nc.scalar.activation(out=a_sb[r][:, w * i : w * i + w], in_=tile_psum[r, i], func=ACT.Identity, bias=b1_fifth[:, c : c + 1], scale=ALPHA)
 
         def relu_vector(r, end):
+            if end == 0:
+                return
             nc.vector.tensor_scalar(out=r_sb[r][:, 0:end], in0=a_sb[r][:, 0:end], scalar1=4.0, scalar2=0.0, op0=ALU.mult, op1=ALU.max)
 
         def relu_scalar(r, i, width):
@@ -284,29 +300,46 @@ def tile_graph_gan_pa_kernel(tc, x, fe_w0, fe_b0, fe_w1_bytes, fe_w1_scale, fe_b
         def leave(r, g):
             (i0, s0), (i1, s1) = banks(r)[g][0], banks(r)[g][-1]
             bank = turned[r, g][:].rearrange("p j c -> p (j c)").rearrange("p (s c) -> p s c", s=s1 + 1 - s0)
-            nc.scalar.copy(out=out_half(r)[:, s0 : s1 + 1, 128 * i0 : 128 * i1 + 128], in_=bank)
+            k, h, n = rounds[r][0:3]
+            nc.scalar.copy(out=out_half(k, h)[:, s0 : s1 + 1, 128 * i0 : 128 * i1 + 128], in_=bank)
             if s0 == s1:
-                store(r, s0, s0 + 1)
-            elif rounds[r][2] == 2:
-                store(r, s0, s1 + 1)
+                store(k, h, s0, s0 + 1)
+            elif n == 2:
+                store(k, h, s0, s1 + 1)
             elif g > 0:
-                store(r, 2 * g - 2, 2 * g)
+                store(k, h, 2 * g - 2, 2 * g)
 
         def part_add(r, j):
-            s0, s1, n0 = rounds[r][5][j]
-            h = rounds[r][1]
+            h, s0, s1, n0 = rounds[r][5][j]
             shape = [P, s1 - s0, 512 - n0]
             z = work.tile(shape, F32, name="part_sums", bufs=4)
             bias = b1_spread[:, 512 * h + n0 : 512 * h + 512]
-            nc.vector.tensor_tensor(out=z[:], in0=part_psum[r, s0][:], in1=bias.unsqueeze(1).to_broadcast(shape), op=ALU.add)
+            nc.vector.tensor_tensor(out=z[:], in0=part_psum[r, j][:], in1=bias.unsqueeze(1).to_broadcast(shape), op=ALU.add)
             part_sums[r, j] = z
 
         def part_lrelu(r, j):
-            s0, s1, n0 = rounds[r][5][j]
+            k = rounds[r][0]
+            h, s0, s1, n0 = rounds[r][5][j]
             z = part_sums[r, j][:]
-            nc.vector.scalar_tensor_tensor(out=out_half(r)[:, s0:s1, n0:512], in0=z, scalar=ALPHA, in1=z, op0=ALU.mult, op1=ALU.max)
+            nc.vector.scalar_tensor_tensor(out=out_half(k, h)[:, s0:s1, n0:512], in0=z, scalar=ALPHA, in1=z, op0=ALU.mult, op1=ALU.max)
             if n0 == 0:
-                store(r, s0, s1)
+                store(k, h, s0, s1)
+
+        def turn_all(r):
+            for g in range(len(banks(r))):
+                turn(r, g)
+
+        def leave_all(r):
+            for g in range(len(banks(r))):
+                leave(r, g)
+
+        def relu_last(r, columns):
+            n, w = rounds[r][2], tile_width(r)
+            for i in range(n):
+                width = min(w, columns - w * (n - 1 - i))
+                if width > 0:
+                    relu_scalar(r, i, width)
+            return n * w - columns
 
         half = ROWS // 2
         w1_widen(0)
@@ -325,77 +358,124 @@ def tile_graph_gan_pa_kernel(tc, x, fe_w0, fe_b0, fe_w1_bytes, fe_w1_scale, fe_b
         w1_leave(1, 0)
         nc.scalar.copy(out=v_sb[:], in_=v_psum)
         e1_quantise(0, 0, half)
-        products(0)
+        tile_products(0)
         e1_lrelu(0, half, ROWS)
         w1_quantise(1)
-        e1_quantise(0, half, ROWS)
         e1_add_gpsimd(1)
+        e1_quantise(0, half, ROWS)
+        part_products(0)
         e1_add(1, 0, own_rows(1))
+        for i0 in (0, 2):
+            affine(0, i0, i0 + 2)
+            relu_scalar(0, i0, 256)
+            relu_scalar(0, i0 + 1, 256)
+        products(1)
+        part_add(0, 0)
+        part_add(0, 1)
+        turn_all(0)
+        products(2)
+        affine(1, 0, 4)
+        rest = relu_last(1, R1_RELU)
+        e1_lrelu(1, 0, own_rows(1))
+        relu_vector(1, rest)
+        e1_lrelu(1, own_rows(1), ROWS)
+        leave_all(0)
+        turn_all(1)
+        affine(2, 0, 4)
+        part_lrelu(0, 0)
+        e1_quantise(1, 0, ROWS)
+        e1_add_gpsimd(2)
+        relu_vector(2, 1024)
+        e1_add(2, 0, own_rows(2))
+        products(3)
+        leave_all(1)
 
-        leaving = [[] for r in range(opening - 1)] + [list(range(opening - 1))] + [[r - 1] for r in range(opening, last + 1)]
-        for r in range(last + 1):
+        for r in range(opening, last - 3):
             k, h, n = rounds[r][0:3]
-            width = n * tile_width(r)
-            affine(r)
-            if r < opening:
-                relu_vector(r, width)
-                if r == 1:
-                    e1_lrelu(1, 0, own_rows(1))
-                elif r == 2:
-                    e1_lrelu(1, own_rows(1), ROWS)
-                elif r == 3:
-                    e1_quantise(1, 0, ROWS)
-                    e1_add_gpsimd(2)
-                    e1_add(2, 0, own_rows(2))
-            elif r <= last - closing and h == 0:
+            affine(r, 0, n)
+            if h == 0:
                 part_add(r, 0)
                 if r > opening:
                     part_lrelu(r - 1, 0)
+                else:
+                    part_lrelu(0, 1)
                 e1_lrelu(k + 1, own_rows(k + 1), ROWS)
-                if SCALAR_RELU > 512:
-                    relu_scalar(r, 1, SCALAR_RELU - 512)
-                relu_scalar(r, 2, min(SCALAR_RELU, 512))
-                relu_vector(r, width - SCALAR_RELU)
+                relu_vector(r, relu_last(r, SCALAR_RELU))
                 e1_lrelu(k + 1, 0, own_rows(k + 1))
                 if r > opening:
                     part_lrelu(r - 1, 1)
-            elif r <= last - closing:
-                relu_scalar(r, 0, 512)
-                relu_scalar(r, 1, 512)
+            else:
+                relu_last(r, 1024)
                 e1_quantise(k + 1, 0, ROWS)
                 e1_add_gpsimd(k + 2)
                 part_lrelu(r - 1, 0)
                 part_add(r, 0)
                 part_add(r, 1)
                 e1_add(k + 2, 0, own_rows(k + 2))
-            elif r == last - 2:
-                part_lrelu(r - 1, 0)
-                e1_quantise(k + 1, 0, ROWS)
-                part_add(r, 0)
-                part_add(r, 1)
-                relu_vector(r, width)
-            elif r == last - 1:
-                part_add(r, 0)
-                part_add(r, 1)
-                relu_scalar(r, 2, tile_width(r))
-                relu_scalar(r, 3, tile_width(r))
-                relu_vector(r, width // 2)
-            else:
-                part_add(r, 0)
-                relu_vector(r, width)
-                part_add(r, 1)
-            for q in leaving[r]:
-                for g in range(len(banks(q))):
-                    turn(q, g)
-            if r < last:
-                products(r + 1)
-            for q in leaving[r]:
-                for g in range(len(banks(q))):
-                    leave(q, g)
-            if r > last - closing:
-                part_lrelu(r, 0)
-                part_lrelu(r, 1)
-        for g in range(len(banks(last))):
-            turn(last, g)
-        for g in range(len(banks(last))):
-            leave(last, g)
+            turn_all(r - 1)
+            products(r + 1)
+            leave_all(r - 1)
+
+        k = CHUNKS - 1
+        r = last - 3
+        part_add(r, 0)
+        part_lrelu(r - 1, 0)
+        part_lrelu(r - 1, 1)
+        turn_all(r - 1)
+        affine(r, 0, EARLY14)
+        leave_all(r - 1)
+        affine(r, EARLY14, 3)
+        rest = relu_last(r, R14_RELU)
+        e1_lrelu(k, 0, half)
+        relu_vector(r, rest)
+        products(r + 1)
+        part_lrelu(r, 0)
+        e1_quantise(k, 0, half)
+        r = last - 2
+        affine(r, 0, 4)
+        turn_all(r - 1)
+        part_add(r, 0)
+        part_add(r, 1)
+        rest = relu_last(r, R15_RELU)
+        products(r + 1)
+        relu_vector(r, rest)
+        leave(r - 1, 0)
+        leave(r - 1, 1)
+        leave(r - 1, 2)
+        part_lrelu(r, 0)
+        leave(r - 1, 3)
+        part_lrelu(r, 1)
+        e1_lrelu(k, half, ROWS)
+        r = last - 1
+        affine(r, 0, 4)
+        turn_all(r - 1)
+        part_add(r, 0)
+        e1_quantise(k, half, ROWS)
+        part_add(r, 1)
+        rest = relu_last(r, R16_RELU)
+        products(r + 1)
+        relu_vector(r, rest)
+        leave_all(r - 1)
+        part_lrelu(r, 0)
+        part_lrelu(r, 1)
+        r = last
+        affine(r, 0, 4)
+        turn_all(r - 1)
+        rest = relu_last(r, R17_RELU)
+        if RELU_FIRST:
+            relu_vector(r, rest)
+        part_add(r, 0)
+        if not RELU_FIRST:
+            relu_vector(r, rest)
+        turn_all(r)
+        part_add(r, 1)
+        leave_all(r - 1)
+        part_lrelu(r, 0)
+        if LAST_TURNED == 1:
+            part_add(r, 2)
+        leave(r, 0)
+        part_lrelu(r, 1)
+        if LAST_TURNED == 1:
+            part_lrelu(r, 2)
+        else:
+            leave(r, 1)

@@ -22,15 +22,18 @@ OWN_ROWS = 8
 OWN1 = 9
 OWN2 = 10
 R0_RELU = 1024
-R1_RELU = 0
-R14_RELU = 640
+R1_RELU = 512
+R14_RELU = 768
 R15_RELU = 0
 R16_RELU = 512
 R17_RELU = 0
 LAST_TURNED = 2
 EARLY14 = 3
-RELU_FIRST = 0
-SCALAR_RELU = 640
+RELU_AFTER = 0
+SPLIT15 = 2
+RELU14_FIRST = 1
+L7B_EARLY = 1
+SCALAR_RELU = 768
 OUT_BUFFERS = 11
 
 
@@ -133,7 +136,6 @@ def tile_graph_gan_pa_kernel(tc, x, fe_w0, fe_b0, fe_w1_bytes, fe_w1_scale, fe_b
         nc.vector.tensor_tensor(out=u_sb[:], in0=u_psum, in1=b0_sb[:].unsqueeze(1).to_broadcast([P, P, 4]), op=ALU.add)
         b1_turned = psum.tile([P, P], BF16, name="b1_turned", tag="turned", bufs=3)
         nc.tensor.transpose(b1_turned[:], b1_rows[:], ident_bf[:])
-        b1_four_fifths = keep.tile([P, 8], F32, name="b1_four_fifths")
         b1_fifth = keep.tile([P, 8], F32, name="b1_fifth")
 
         w1_planes = [keep.tile([P, 4, 512], BF16, name="w1_planes%d" % q, align_bytes=64) for q in range(2)]
@@ -271,17 +273,16 @@ def tile_graph_gan_pa_kernel(tc, x, fe_w0, fe_b0, fe_w1_bytes, fe_w1_scale, fe_b
                 return
             nc.vector.tensor_scalar(out=r_sb[r][:, 0:end], in0=a_sb[r][:, 0:end], scalar1=4.0, scalar2=0.0, op0=ALU.mult, op1=ALU.max)
 
-        def relu_scalar(r, i, width):
-            c = 4 * rounds[r][1] + i
-            w = tile_width(r)
-            nc.scalar.activation(out=r_sb[r][:, w * i + w - width : w * i + w], in_=tile_psum[r, i][:, w - width : w], func=ACT.Relu, bias=b1_four_fifths[:, c : c + 1], scale=4 * ALPHA)
+        def relu_scalar(r, start, end):
+            if end > start:
+                nc.scalar.activation(out=r_sb[r][:, start:end], in_=a_sb[r][:, start:end], func=ACT.Relu, scale=4.0)
 
         def banks(r):
             n, b0, b1 = rounds[r][2:5]
             if n == 2:
                 return [[(i, s) for s in (s0, s0 + 1) for i in (0, 1)] for s0 in (0, 2)]
             if b1 - b0 == 4 and r < v_done:
-                return [[(i, s) for s in (0, 1) for i in (0, 1)], [(2, s) for s in range(4)], [(i, s) for s in (2, 3) for i in (0, 1)]]
+                return [[(0, s) for s in range(4)], [(i, s) for s in (0, 1) for i in (1, 2)], [(i, s) for s in (2, 3) for i in (1, 2)]]
             return [[(i, s) for i in range(n)] for s in range(b0, b1)]
 
         def turn(r, g):
@@ -333,14 +334,6 @@ def tile_graph_gan_pa_kernel(tc, x, fe_w0, fe_b0, fe_w1_bytes, fe_w1_scale, fe_b
             for g in range(len(banks(r))):
                 leave(r, g)
 
-        def relu_last(r, columns):
-            n, w = rounds[r][2], tile_width(r)
-            for i in range(n):
-                width = min(w, columns - w * (n - 1 - i))
-                if width > 0:
-                    relu_scalar(r, i, width)
-            return n * w - columns
-
         half = ROWS // 2
         w1_widen(0)
         w1_weave(0, 0)
@@ -348,7 +341,6 @@ def tile_graph_gan_pa_kernel(tc, x, fe_w0, fe_b0, fe_w1_bytes, fe_w1_scale, fe_b
         e1_add(0, 0, half)
         w1_widen(1)
         nc.scalar.activation(out=b1_fifth[:], in_=b1_turned[:, 0:8], func=ACT.Copy, scale=ALPHA)
-        nc.scalar.activation(out=b1_four_fifths[:], in_=b1_turned[:, 0:8], func=ACT.Copy, scale=4 * ALPHA)
         w1_weave(1, 0)
         e1_add(0, half, ROWS)
         w1_leave(0, 0)
@@ -362,24 +354,25 @@ def tile_graph_gan_pa_kernel(tc, x, fe_w0, fe_b0, fe_w1_bytes, fe_w1_scale, fe_b
         e1_lrelu(0, half, ROWS)
         w1_quantise(1)
         e1_add_gpsimd(1)
+        products(1)
         e1_quantise(0, half, ROWS)
+        affine(0, 0, 4)
         part_products(0)
         e1_add(1, 0, own_rows(1))
-        for i0 in (0, 2):
-            affine(0, i0, i0 + 2)
-            relu_scalar(0, i0, 256)
-            relu_scalar(0, i0 + 1, 256)
-        products(1)
+        relu_scalar(0, 0, 512)
+        affine(1, 0, 2)
+        relu_scalar(0, 512, 1024)
+        affine(1, 2, 4)
         part_add(0, 0)
         part_add(0, 1)
         turn_all(0)
         products(2)
-        affine(1, 0, 4)
-        rest = relu_last(1, R1_RELU)
         e1_lrelu(1, 0, own_rows(1))
-        relu_vector(1, rest)
+        relu_vector(1, 1024 - R1_RELU)
         e1_lrelu(1, own_rows(1), ROWS)
-        leave_all(0)
+        leave(0, 0)
+        relu_scalar(1, 1024 - R1_RELU, 1024)
+        leave(0, 1)
         turn_all(1)
         affine(2, 0, 4)
         part_lrelu(0, 0)
@@ -392,21 +385,21 @@ def tile_graph_gan_pa_kernel(tc, x, fe_w0, fe_b0, fe_w1_bytes, fe_w1_scale, fe_b
 
         for r in range(opening, last - 3):
             k, h, n = rounds[r][0:3]
+            width = n * tile_width(r)
             affine(r, 0, n)
             if h == 0:
                 part_add(r, 0)
                 if r > opening:
                     part_lrelu(r - 1, 0)
+                    part_lrelu(r - 1, 1)
                 else:
                     part_lrelu(0, 1)
-                e1_lrelu(k + 1, own_rows(k + 1), ROWS)
-                relu_vector(r, relu_last(r, SCALAR_RELU))
+                relu_vector(r, width - SCALAR_RELU)
                 e1_lrelu(k + 1, 0, own_rows(k + 1))
-                if r > opening:
-                    part_lrelu(r - 1, 1)
+                e1_lrelu(k + 1, own_rows(k + 1), ROWS)
             else:
-                relu_last(r, 1024)
-                e1_quantise(k + 1, 0, ROWS)
+                e1_quantise(k + 1, 0, half)
+                e1_quantise(k + 1, half, ROWS)
                 e1_add_gpsimd(k + 2)
                 part_lrelu(r - 1, 0)
                 part_add(r, 0)
@@ -414,7 +407,10 @@ def tile_graph_gan_pa_kernel(tc, x, fe_w0, fe_b0, fe_w1_bytes, fe_w1_scale, fe_b
                 e1_add(k + 2, 0, own_rows(k + 2))
             turn_all(r - 1)
             products(r + 1)
-            leave_all(r - 1)
+            for g in range(len(banks(r - 1))):
+                leave(r - 1, g)
+                if g == min(RELU_AFTER, len(banks(r - 1)) - 1):
+                    relu_scalar(r, width - SCALAR_RELU if h == 0 else 0, width)
 
         k = CHUNKS - 1
         r = last - 3
@@ -422,51 +418,52 @@ def tile_graph_gan_pa_kernel(tc, x, fe_w0, fe_b0, fe_w1_bytes, fe_w1_scale, fe_b
         part_lrelu(r - 1, 0)
         part_lrelu(r - 1, 1)
         turn_all(r - 1)
-        affine(r, 0, EARLY14)
-        leave_all(r - 1)
-        affine(r, EARLY14, 3)
-        rest = relu_last(r, R14_RELU)
-        e1_lrelu(k, 0, half)
-        relu_vector(r, rest)
+        affine(r, 0, 3)
         products(r + 1)
+        leave(r - 1, 0)
+        relu_scalar(r, 1536 - R14_RELU, 1536)
+        leave(r - 1, 1)
+        if RELU14_FIRST:
+            relu_vector(r, 1536 - R14_RELU)
+        e1_lrelu(k, 0, half)
+        if not RELU14_FIRST:
+            relu_vector(r, 1536 - R14_RELU)
         part_lrelu(r, 0)
         e1_quantise(k, 0, half)
         r = last - 2
-        affine(r, 0, 4)
+        affine(r, 0, SPLIT15)
         turn_all(r - 1)
         part_add(r, 0)
         part_add(r, 1)
-        rest = relu_last(r, R15_RELU)
-        products(r + 1)
-        relu_vector(r, rest)
         leave(r - 1, 0)
         leave(r - 1, 1)
-        leave(r - 1, 2)
+        affine(r, SPLIT15, 4)
+        products(r + 1)
         part_lrelu(r, 0)
+        leave(r - 1, 2)
+        relu_vector(r, 1024 - R15_RELU)
         leave(r - 1, 3)
-        part_lrelu(r, 1)
+        relu_scalar(r, 1024 - R15_RELU, 1024)
         e1_lrelu(k, half, ROWS)
+        part_lrelu(r, 1)
+        e1_quantise(k, half, ROWS)
         r = last - 1
         affine(r, 0, 4)
         turn_all(r - 1)
         part_add(r, 0)
-        e1_quantise(k, half, ROWS)
         part_add(r, 1)
-        rest = relu_last(r, R16_RELU)
         products(r + 1)
-        relu_vector(r, rest)
-        leave_all(r - 1)
+        relu_vector(r, 1024 - R16_RELU)
+        leave(r - 1, 0)
+        relu_scalar(r, 1024 - R16_RELU, 1024)
+        leave(r - 1, 1)
         part_lrelu(r, 0)
         part_lrelu(r, 1)
         r = last
         affine(r, 0, 4)
         turn_all(r - 1)
-        rest = relu_last(r, R17_RELU)
-        if RELU_FIRST:
-            relu_vector(r, rest)
         part_add(r, 0)
-        if not RELU_FIRST:
-            relu_vector(r, rest)
+        relu_vector(r, 512 * LAST_TURNED)
         turn_all(r)
         part_add(r, 1)
         leave_all(r - 1)

@@ -22,8 +22,8 @@ OWN_ROWS = 8
 OWN1 = 9
 OWN2 = 10
 R0_RELU = 1024
-R1_RELU = 512
-R14_RELU = 768
+R1_RELU = 0
+R14_RELU = 704
 R15_RELU = 0
 R16_RELU = 512
 R17_RELU = 0
@@ -32,8 +32,9 @@ EARLY14 = 3
 RELU_AFTER = 0
 SPLIT15 = 2
 RELU14_FIRST = 1
-L7B_EARLY = 1
-SCALAR_RELU = 768
+R2_RELU = 1024
+PARTS_FIRST = 2
+SCALAR_RELU = 704
 OUT_BUFFERS = 11
 
 
@@ -243,9 +244,9 @@ def tile_graph_gan_pa_kernel(tc, x, fe_w0, fe_b0, fe_w1_bytes, fe_w1_scale, fe_b
                     product(acc[:, i - i0, :], w1_mx[h], slice(128 * i, 128 * i + 128), e1_mx[k], slice(128 * b0, 128 * b1))
                     tile_psum[r, i] = acc[:, i - i0, :]
 
-        def part_products(r):
+        def part_products(r, j0=0, j1=3):
             k = rounds[r][0]
-            for j, (h, s0, s1, n0) in enumerate(rounds[r][5]):
+            for j, (h, s0, s1, n0) in list(enumerate(rounds[r][5]))[j0:j1]:
                 acc = psum.tile([P, s1 - s0, 512 - n0], F32, name="part_psum", tag="product")
                 for s in range(s0, s1):
                     product(acc[:, s - s0, :], e1_mx[k], slice(128 * s, 128 * s + 128), w1_mx[h], slice(n0, 512))
@@ -376,12 +377,15 @@ def tile_graph_gan_pa_kernel(tc, x, fe_w0, fe_b0, fe_w1_bytes, fe_w1_scale, fe_b
         turn_all(1)
         affine(2, 0, 4)
         part_lrelu(0, 0)
+        relu_vector(2, 1024 - R2_RELU)
         e1_quantise(1, 0, ROWS)
         e1_add_gpsimd(2)
-        relu_vector(2, 1024)
+        part_lrelu(0, 1)
         e1_add(2, 0, own_rows(2))
         products(3)
-        leave_all(1)
+        leave(1, 0)
+        relu_scalar(2, 1024 - R2_RELU, 1024)
+        leave(1, 1)
 
         for r in range(opening, last - 3):
             k, h, n = rounds[r][0:3]
@@ -392,8 +396,6 @@ def tile_graph_gan_pa_kernel(tc, x, fe_w0, fe_b0, fe_w1_bytes, fe_w1_scale, fe_b
                 if r > opening:
                     part_lrelu(r - 1, 0)
                     part_lrelu(r - 1, 1)
-                else:
-                    part_lrelu(0, 1)
                 relu_vector(r, width - SCALAR_RELU)
                 e1_lrelu(k + 1, 0, own_rows(k + 1))
                 e1_lrelu(k + 1, own_rows(k + 1), ROWS)
@@ -452,7 +454,8 @@ def tile_graph_gan_pa_kernel(tc, x, fe_w0, fe_b0, fe_w1_bytes, fe_w1_scale, fe_b
         turn_all(r - 1)
         part_add(r, 0)
         part_add(r, 1)
-        products(r + 1)
+        tile_products(last)
+        part_products(last, 0, PARTS_FIRST)
         relu_vector(r, 1024 - R16_RELU)
         leave(r - 1, 0)
         relu_scalar(r, 1024 - R16_RELU, 1024)
@@ -462,12 +465,20 @@ def tile_graph_gan_pa_kernel(tc, x, fe_w0, fe_b0, fe_w1_bytes, fe_w1_scale, fe_b
         r = last
         affine(r, 0, 4)
         turn_all(r - 1)
-        part_add(r, 0)
+        part_products(last, PARTS_FIRST, 3)
+        if PARTS_FIRST > 0:
+            part_add(r, 0)
         relu_vector(r, 512 * LAST_TURNED)
         turn_all(r)
-        part_add(r, 1)
         leave_all(r - 1)
-        part_lrelu(r, 0)
+        if PARTS_FIRST == 0:
+            part_add(r, 0)
+        if PARTS_FIRST == 1 and LAST_TURNED == 2:
+            part_lrelu(r, 0)
+            part_add(r, 1)
+        else:
+            part_add(r, 1)
+            part_lrelu(r, 0)
         if LAST_TURNED == 1:
             part_add(r, 2)
         leave(r, 0)

@@ -18,13 +18,13 @@ ALPHA = 0.2
 CHUNKS = 8
 PAIRS = 512
 ROWS = 16
-OWN_ROWS = 8
+OWN_ROWS = 7
 OWN1 = 9
 OWN2 = 10
 R0_RELU = 1024
 R1_RELU = 0
 R14_RELU = 704
-R15_RELU = 0
+R15_RELU = 256
 R16_RELU = 512
 R17_RELU = 0
 LAST_TURNED = 2
@@ -34,6 +34,11 @@ SPLIT15 = 2
 RELU14_FIRST = 1
 R2_RELU = 1024
 PARTS_FIRST = 2
+BY_TILES = 1
+RELU16_EARLY = 0
+R3_RELU = 384
+PAIR_TURNED = ()
+PAIR_DIRECT = ()
 SCALAR_RELU = 704
 OUT_BUFFERS = 11
 
@@ -172,10 +177,10 @@ def tile_graph_gan_pa_kernel(tc, x, fe_w0, fe_b0, fe_w1_bytes, fe_w1_scale, fe_b
 
         pair_sums = {}
         e1_mx = {}
-        e1_tiles = [keep.tile([P, 4 * PAIRS], BF16, name="e1_tile%d" % j, align_bytes=64) for j in range(2)]
+        e1_tiles = [keep.tile([P, 5 * PAIRS], BF16, name="e1_tile%d" % j, align_bytes=64) for j in range(2)]
 
         def own_rows(k):
-            return OWN1 if k == 1 else (OWN2 if k == 2 else OWN_ROWS)
+            return OWN1 if k == 1 else (OWN2 if k == 2 else (8 if k == CHUNKS - 1 else OWN_ROWS))
 
         def pair_operands(k, i0, i1, v):
             graph = k // 2
@@ -193,7 +198,8 @@ def tile_graph_gan_pa_kernel(tc, x, fe_w0, fe_b0, fe_w1_bytes, fe_w1_scale, fe_b
         def e1_add_gpsimd(k):
             i0 = own_rows(k)
             home = w0_laid[0] if k == 1 else e1_tiles[(k - 1) % 2]
-            z = home[:].bitcast(F32)[:, 2 * PAIRS - 128 * (ROWS - i0) : 2 * PAIRS]
+            end = home.shape[1] // 2
+            z = home[:].bitcast(F32)[:, end - 128 * (ROWS - i0) : end]
             in0, in1 = pair_operands(k, i0, ROWS, v_sb)
             nc.gpsimd.tensor_tensor(out=z.rearrange("p (i j t) -> p i j t", j=32, t=4), in0=in0, in1=in1, op=ALU.add)
             pair_sums[k, i0] = z
@@ -203,7 +209,7 @@ def tile_graph_gan_pa_kernel(tc, x, fe_w0, fe_b0, fe_w1_bytes, fe_w1_scale, fe_b
             nc.vector.scalar_tensor_tensor(out=e1_tiles[k % 2][:, 128 * i0 : 128 * i1], in0=z, scalar=ALPHA, in1=z, op0=ALU.mult, op1=ALU.max)
 
         def e1_quantise(k, i0, i1):
-            if i0 == 0:
+            if k not in e1_mx:
                 e1_mx[k] = mx_operand(work, "e1", PAIRS, 2)
             cols = slice(32 * i0, 32 * i1)
             quantise(e1_mx[k][0][:, cols], e1_mx[k][1][:, cols], e1_tiles[k % 2][:, 128 * i0 : 128 * i1])
@@ -269,10 +275,10 @@ def tile_graph_gan_pa_kernel(tc, x, fe_w0, fe_b0, fe_w1_bytes, fe_w1_scale, fe_b
                 c = 4 * h + i
                 nc.scalar.activation(out=a_sb[r][:, w * i : w * i + w], in_=tile_psum[r, i], func=ACT.Identity, bias=b1_fifth[:, c : c + 1], scale=ALPHA)
 
-        def relu_vector(r, end):
-            if end == 0:
+        def relu_vector(r, end, start=0):
+            if end == start:
                 return
-            nc.vector.tensor_scalar(out=r_sb[r][:, 0:end], in0=a_sb[r][:, 0:end], scalar1=4.0, scalar2=0.0, op0=ALU.mult, op1=ALU.max)
+            nc.vector.tensor_scalar(out=r_sb[r][:, start:end], in0=a_sb[r][:, start:end], scalar1=4.0, scalar2=0.0, op0=ALU.mult, op1=ALU.max)
 
         def relu_scalar(r, start, end):
             if end > start:
@@ -280,6 +286,8 @@ def tile_graph_gan_pa_kernel(tc, x, fe_w0, fe_b0, fe_w1_bytes, fe_w1_scale, fe_b
 
         def banks(r):
             n, b0, b1 = rounds[r][2:5]
+            if r == last and BY_TILES:
+                return [[(i, s) for s in (2, 3) for i in (i0, i0 + 1)] for i0 in (0, 2)]
             if n == 2:
                 return [[(i, s) for s in (s0, s0 + 1) for i in (0, 1)] for s0 in (0, 2)]
             if b1 - b0 == 4 and r < v_done:
@@ -304,7 +312,13 @@ def tile_graph_gan_pa_kernel(tc, x, fe_w0, fe_b0, fe_w1_bytes, fe_w1_scale, fe_b
             bank = turned[r, g][:].rearrange("p j c -> p (j c)").rearrange("p (s c) -> p s c", s=s1 + 1 - s0)
             k, h, n = rounds[r][0:3]
             nc.scalar.copy(out=out_half(k, h)[:, s0 : s1 + 1, 128 * i0 : 128 * i1 + 128], in_=bank)
-            if s0 == s1:
+            if r == last and BY_TILES:
+                if g == 1:
+                    store(k, h, 2, 4)
+            elif s0 == s1 and last - r in PAIR_TURNED:
+                if s0 % 2 == 1:
+                    store(k, h, s0 - 1, s0 + 1)
+            elif s0 == s1:
                 store(k, h, s0, s0 + 1)
             elif n == 2:
                 store(k, h, s0, s1 + 1)
@@ -324,7 +338,10 @@ def tile_graph_gan_pa_kernel(tc, x, fe_w0, fe_b0, fe_w1_bytes, fe_w1_scale, fe_b
             h, s0, s1, n0 = rounds[r][5][j]
             z = part_sums[r, j][:]
             nc.vector.scalar_tensor_tensor(out=out_half(k, h)[:, s0:s1, n0:512], in0=z, scalar=ALPHA, in1=z, op0=ALU.mult, op1=ALU.max)
-            if n0 == 0:
+            if n0 == 0 and last - r in PAIR_DIRECT:
+                if s0 % 2 == 1:
+                    store(k, h, s0 - 1, s1)
+            elif n0 == 0:
                 store(k, h, s0, s1)
 
         def turn_all(r):
@@ -396,12 +413,24 @@ def tile_graph_gan_pa_kernel(tc, x, fe_w0, fe_b0, fe_w1_bytes, fe_w1_scale, fe_b
                 if r > opening:
                     part_lrelu(r - 1, 0)
                     part_lrelu(r - 1, 1)
-                relu_vector(r, width - SCALAR_RELU)
-                e1_lrelu(k + 1, 0, own_rows(k + 1))
-                e1_lrelu(k + 1, own_rows(k + 1), ROWS)
+                share = SCALAR_RELU if r > opening else R3_RELU
+                if r > opening:
+                    relu_vector(r, width - share)
+                if own_rows(k + 1) < half:
+                    e1_lrelu(k + 1, own_rows(k + 1), ROWS)
+                    e1_lrelu(k + 1, 0, own_rows(k + 1))
+                else:
+                    e1_lrelu(k + 1, 0, own_rows(k + 1))
+                    if r == opening:
+                        relu_vector(r, width - share)
+                    e1_lrelu(k + 1, own_rows(k + 1), ROWS)
             else:
-                e1_quantise(k + 1, 0, half)
-                e1_quantise(k + 1, half, ROWS)
+                if own_rows(k + 1) < half:
+                    e1_quantise(k + 1, half, ROWS)
+                    e1_quantise(k + 1, 0, half)
+                else:
+                    e1_quantise(k + 1, 0, half)
+                    e1_quantise(k + 1, half, ROWS)
                 e1_add_gpsimd(k + 2)
                 part_lrelu(r - 1, 0)
                 part_add(r, 0)
@@ -412,7 +441,7 @@ def tile_graph_gan_pa_kernel(tc, x, fe_w0, fe_b0, fe_w1_bytes, fe_w1_scale, fe_b
             for g in range(len(banks(r - 1))):
                 leave(r - 1, g)
                 if g == min(RELU_AFTER, len(banks(r - 1)) - 1):
-                    relu_scalar(r, width - SCALAR_RELU if h == 0 else 0, width)
+                    relu_scalar(r, width - share if h == 0 else 0, width)
 
         k = CHUNKS - 1
         r = last - 3
@@ -453,37 +482,36 @@ def tile_graph_gan_pa_kernel(tc, x, fe_w0, fe_b0, fe_w1_bytes, fe_w1_scale, fe_b
         affine(r, 0, 4)
         turn_all(r - 1)
         part_add(r, 0)
+        if RELU16_EARLY:
+            relu_vector(r, 1024 - R16_RELU)
         part_add(r, 1)
-        tile_products(last)
-        part_products(last, 0, PARTS_FIRST)
-        relu_vector(r, 1024 - R16_RELU)
+        products(last)
+        if not RELU16_EARLY:
+            relu_vector(r, 1024 - R16_RELU)
         leave(r - 1, 0)
         relu_scalar(r, 1024 - R16_RELU, 1024)
         leave(r - 1, 1)
         part_lrelu(r, 0)
-        part_lrelu(r, 1)
         r = last
         affine(r, 0, 4)
         turn_all(r - 1)
-        part_products(last, PARTS_FIRST, 3)
-        if PARTS_FIRST > 0:
+        if BY_TILES:
+            part_lrelu(r - 1, 1)
+            relu_vector(r, 512)
             part_add(r, 0)
-        relu_vector(r, 512 * LAST_TURNED)
+            relu_vector(r, 1024, 512)
+        else:
+            part_lrelu(r - 1, 1)
+            part_add(r, 0)
+            relu_vector(r, 1024)
         turn_all(r)
+        part_add(r, 1)
         leave_all(r - 1)
-        if PARTS_FIRST == 0:
-            part_add(r, 0)
-        if PARTS_FIRST == 1 and LAST_TURNED == 2:
-            part_lrelu(r, 0)
-            part_add(r, 1)
-        else:
-            part_add(r, 1)
-            part_lrelu(r, 0)
-        if LAST_TURNED == 1:
-            part_add(r, 2)
+        part_lrelu(r, 0)
         leave(r, 0)
-        part_lrelu(r, 1)
-        if LAST_TURNED == 1:
-            part_lrelu(r, 2)
+        if BY_TILES:
+            leave(r, 1)
+            part_lrelu(r, 1)
         else:
+            part_lrelu(r, 1)
             leave(r, 1)

@@ -37,9 +37,11 @@ PARTS_FIRST = 2
 BY_TILES = 1
 RELU16_EARLY = 0
 R3_RELU = 384
+LATE_FROM = 12
+MODE14 = 1
 PAIR_TURNED = ()
 PAIR_DIRECT = ()
-SCALAR_RELU = 704
+SCALAR_RELU = 640
 OUT_BUFFERS = 11
 
 
@@ -440,7 +442,7 @@ def tile_graph_gan_pa_kernel(tc, x, fe_w0, fe_b0, fe_w1_bytes, fe_w1_scale, fe_b
             products(r + 1)
             for g in range(len(banks(r - 1))):
                 leave(r - 1, g)
-                if g == min(RELU_AFTER, len(banks(r - 1)) - 1):
+                if g == min(RELU_AFTER if r < LATE_FROM or h == 0 else 2, len(banks(r - 1)) - 1):
                     relu_scalar(r, width - share if h == 0 else 0, width)
 
         k = CHUNKS - 1
@@ -449,11 +451,27 @@ def tile_graph_gan_pa_kernel(tc, x, fe_w0, fe_b0, fe_w1_bytes, fe_w1_scale, fe_b
         part_lrelu(r - 1, 0)
         part_lrelu(r - 1, 1)
         turn_all(r - 1)
-        affine(r, 0, 3)
-        products(r + 1)
-        leave(r - 1, 0)
-        relu_scalar(r, 1536 - R14_RELU, 1536)
-        leave(r - 1, 1)
+        if MODE14 == 0:
+            affine(r, 0, 3)
+            products(r + 1)
+            leave(r - 1, 0)
+            relu_scalar(r, 1536 - R14_RELU, 1536)
+            leave(r - 1, 1)
+        elif MODE14 == 1:
+            affine(r, 0, 2)
+            leave(r - 1, 0)
+            affine(r, 2, 3)
+            products(r + 1)
+            leave(r - 1, 1)
+            relu_scalar(r, 1536 - R14_RELU, 1536)
+        else:
+            affine(r, 0, 1)
+            leave(r - 1, 0)
+            affine(r, 1, 2)
+            leave(r - 1, 1)
+            affine(r, 2, 3)
+            products(r + 1)
+            relu_scalar(r, 1536 - R14_RELU, 1536)
         if RELU14_FIRST:
             relu_vector(r, 1536 - R14_RELU)
         e1_lrelu(k, 0, half)

@@ -37,7 +37,9 @@ PARTS_FIRST = 2
 BY_TILES = 1
 RELU16_EARLY = 0
 R3_RELU = 384
-LATE_FROM = 12
+HALF13 = 2
+T13 = 0
+PART_FIRST = 1
 MODE14 = 1
 PAIR_TURNED = ()
 PAIR_DIRECT = ()
@@ -243,10 +245,10 @@ def tile_graph_gan_pa_kernel(tc, x, fe_w0, fe_b0, fe_w1_bytes, fe_w1_scale, fe_b
             dst = rows[PAIRS * k + 128 * s0 : PAIRS * k + 128 * s1, 512 * h : 512 * h + 512]
             nc.sync.dma_start(out=dst.rearrange("(s p) c -> p s c", p=P), in_=out_half(k, h)[:, s0:s1, :])
 
-        def tile_products(r):
+        def tile_products(r, first=0, end=4):
             k, h, n, b0, b1, parts = rounds[r]
             per_bank = 4 // (b1 - b0)
-            for i0 in range(0, n, per_bank):
+            for i0 in range(first, min(n, end), per_bank):
                 acc = psum.tile([P, per_bank, 128 * (b1 - b0)], F32, name="tile_psum", tag="product")
                 for i in range(i0, i0 + per_bank):
                     product(acc[:, i - i0, :], w1_mx[h], slice(128 * i, 128 * i + 128), e1_mx[k], slice(128 * b0, 128 * b1))
@@ -261,8 +263,12 @@ def tile_graph_gan_pa_kernel(tc, x, fe_w0, fe_b0, fe_w1_bytes, fe_w1_scale, fe_b
                 part_psum[r, j] = acc
 
         def products(r):
-            tile_products(r)
-            part_products(r)
+            if rounds[r][2] == 3 and PART_FIRST:
+                part_products(r)
+                tile_products(r)
+            else:
+                tile_products(r)
+                part_products(r)
 
         def tile_width(r):
             return 128 * (rounds[r][4] - rounds[r][3])
@@ -285,6 +291,11 @@ def tile_graph_gan_pa_kernel(tc, x, fe_w0, fe_b0, fe_w1_bytes, fe_w1_scale, fe_b
         def relu_scalar(r, start, end):
             if end > start:
                 nc.scalar.activation(out=r_sb[r][:, start:end], in_=a_sb[r][:, start:end], func=ACT.Relu, scale=4.0)
+
+        def relu_scalar_blocks(r, s0):
+            a = a_sb[r][:].rearrange("p (i c) -> p i c", i=2)[:, :, 128 * s0 : 128 * s0 + 256]
+            out_r = r_sb[r][:].rearrange("p (i c) -> p i c", i=2)[:, :, 128 * s0 : 128 * s0 + 256]
+            nc.scalar.activation(out=out_r, in_=a, func=ACT.Relu, scale=4.0)
 
         def banks(r):
             n, b0, b1 = rounds[r][2:5]
@@ -439,11 +450,25 @@ def tile_graph_gan_pa_kernel(tc, x, fe_w0, fe_b0, fe_w1_bytes, fe_w1_scale, fe_b
                 part_add(r, 1)
                 e1_add(k + 2, 0, own_rows(k + 2))
             turn_all(r - 1)
-            products(r + 1)
-            for g in range(len(banks(r - 1))):
-                leave(r - 1, g)
-                if g == min(RELU_AFTER if r < LATE_FROM or h == 0 else 2, len(banks(r - 1)) - 1):
-                    relu_scalar(r, width - share if h == 0 else 0, width)
+            if r == last - 4 and T13:
+                part_products(r + 1)
+                tile_products(r + 1, 0, 2)
+            else:
+                products(r + 1)
+            if r == last - 4 and HALF13 == 1:
+                leave(r - 1, 0)
+                relu_scalar_blocks(r, 0)
+                leave(r - 1, 1)
+                leave(r - 1, 2)
+                relu_scalar_blocks(r, 2)
+            elif r == last - 4 and HALF13 == 2:
+                leave_all(r - 1)
+                relu_scalar(r, 0, width)
+            else:
+                leave(r - 1, 0)
+                relu_scalar(r, width - share if h == 0 else 0, width)
+                for g in range(1, len(banks(r - 1))):
+                    leave(r - 1, g)
 
         k = CHUNKS - 1
         r = last - 3
@@ -451,6 +476,8 @@ def tile_graph_gan_pa_kernel(tc, x, fe_w0, fe_b0, fe_w1_bytes, fe_w1_scale, fe_b
         part_lrelu(r - 1, 0)
         part_lrelu(r - 1, 1)
         turn_all(r - 1)
+        if T13:
+            tile_products(r, 2, 3)
         if MODE14 == 0:
             affine(r, 0, 3)
             products(r + 1)

@@ -19,31 +19,10 @@ CHUNKS = 8
 PAIRS = 512
 ROWS = 16
 OWN_ROWS = 7
-OWN1 = 9
-OWN2 = 10
-R0_RELU = 1024
-R1_RELU = 0
-R14_RELU = 704
-R15_RELU = 256
-R16_RELU = 512
-R17_RELU = 0
-LAST_TURNED = 2
-EARLY14 = 3
-RELU_AFTER = 0
-SPLIT15 = 2
-RELU14_FIRST = 1
-R2_RELU = 1024
-PARTS_FIRST = 2
-BY_TILES = 1
-RELU16_EARLY = 0
-R3_RELU = 384
-HALF13 = 2
-T13 = 0
-PART_FIRST = 1
-MODE14 = 1
-PAIR_TURNED = ()
-PAIR_DIRECT = ()
+OWN_ROWS_CHUNK_1 = 9
+OWN_ROWS_CHUNK_2 = 10
 SCALAR_RELU = 640
+SCALAR_RELU_FIRST = 384
 OUT_BUFFERS = 11
 
 
@@ -182,9 +161,12 @@ def tile_graph_gan_pa_kernel(tc, x, fe_w0, fe_b0, fe_w1_bytes, fe_w1_scale, fe_b
         pair_sums = {}
         e1_mx = {}
         e1_tiles = [keep.tile([P, 5 * PAIRS], BF16, name="e1_tile%d" % j, align_bytes=64) for j in range(2)]
+        half = ROWS // 2
 
         def own_rows(k):
-            return OWN1 if k == 1 else (OWN2 if k == 2 else (8 if k == CHUNKS - 1 else OWN_ROWS))
+            if k == CHUNKS - 1:
+                return half
+            return {1: OWN_ROWS_CHUNK_1, 2: OWN_ROWS_CHUNK_2}.get(k, OWN_ROWS)
 
         def pair_operands(k, i0, i1, v):
             graph = k // 2
@@ -218,16 +200,24 @@ def tile_graph_gan_pa_kernel(tc, x, fe_w0, fe_b0, fe_w1_bytes, fe_w1_scale, fe_b
             cols = slice(32 * i0, 32 * i1)
             quantise(e1_mx[k][0][:, cols], e1_mx[k][1][:, cols], e1_tiles[k % 2][:, 128 * i0 : 128 * i1])
 
+        def e1_shares(k):
+            shares = [(0, own_rows(k)), (own_rows(k), ROWS)]
+            halves = [(0, half), (half, ROWS)]
+            if own_rows(k) < half:
+                return shares[::-1], halves[::-1]
+            return shares, halves
+
         opening = 3
         rounds = [(0, 0, 4, 0, 2, [(0, 2, 3, 0), (0, 3, 4, 0)]), (0, 1, 4, 0, 2, []), (0, 1, 4, 2, 4, [])]
         for k in range(1, CHUNKS - 1):
             rounds.append((k, 0, 3, 0, 4, [(0, 0, 4, 384)]))
-            rounds.append((k, 1, 2, 0, 4, [(1, 0, 2, 256), (1, 2, 4, 256)]))
-        rounds[-1] = (CHUNKS - 2, 1, 4, 0, 2, [(1, 2, 3, 0), (1, 3, 4, 0)])
-        rounds.append((CHUNKS - 1, 0, 4, 0, 2, [(1, 0, 1, 0), (1, 1, 2, 0)]))
-        rounds.append((CHUNKS - 1, 0, 4, 2, 2 + LAST_TURNED, [(0, s, s + 1, 0) for s in range(2 + LAST_TURNED, 4)] + [(1, 2, 3, 0), (1, 3, 4, 0)]))
+            if k < CHUNKS - 2:
+                rounds.append((k, 1, 2, 0, 4, [(1, 0, 2, 256), (1, 2, 4, 256)]))
+        rounds.append((CHUNKS - 2, 1, 4, 0, 2, [(1, 2, 3, 0), (1, 3, 4, 0)]))
+        for s0 in (0, 2):
+            rounds.append((CHUNKS - 1, 0, 4, s0, s0 + 2, [(1, s0, s0 + 1, 0), (1, s0 + 1, s0 + 2, 0)]))
         last = len(rounds) - 1
-        v_done = last - 3
+        v_free = last - 3
         tile_psum = {}
         part_psum = {}
         a_sb = {}
@@ -245,33 +235,34 @@ def tile_graph_gan_pa_kernel(tc, x, fe_w0, fe_b0, fe_w1_bytes, fe_w1_scale, fe_b
             dst = rows[PAIRS * k + 128 * s0 : PAIRS * k + 128 * s1, 512 * h : 512 * h + 512]
             nc.sync.dma_start(out=dst.rearrange("(s p) c -> p s c", p=P), in_=out_half(k, h)[:, s0:s1, :])
 
-        def tile_products(r, first=0, end=4):
-            k, h, n, b0, b1, parts = rounds[r]
-            per_bank = 4 // (b1 - b0)
-            for i0 in range(first, min(n, end), per_bank):
-                acc = psum.tile([P, per_bank, 128 * (b1 - b0)], F32, name="tile_psum", tag="product")
+        def tile_width(r):
+            return 128 * (rounds[r][4] - rounds[r][3])
+
+        def tile_products(r, first, end):
+            k, h, n, s0, s1, parts = rounds[r]
+            per_bank = 512 // tile_width(r)
+            for i0 in range(first, end, per_bank):
+                acc = psum.tile([P, per_bank, tile_width(r)], F32, name="tile_psum", tag="product")
                 for i in range(i0, i0 + per_bank):
-                    product(acc[:, i - i0, :], w1_mx[h], slice(128 * i, 128 * i + 128), e1_mx[k], slice(128 * b0, 128 * b1))
+                    product(acc[:, i - i0, :], w1_mx[h], slice(128 * i, 128 * i + 128), e1_mx[k], slice(128 * s0, 128 * s1))
                     tile_psum[r, i] = acc[:, i - i0, :]
 
-        def part_products(r, j0=0, j1=3):
+        def part_products(r):
             k = rounds[r][0]
-            for j, (h, s0, s1, n0) in list(enumerate(rounds[r][5]))[j0:j1]:
+            for j, (h, s0, s1, n0) in enumerate(rounds[r][5]):
                 acc = psum.tile([P, s1 - s0, 512 - n0], F32, name="part_psum", tag="product")
                 for s in range(s0, s1):
                     product(acc[:, s - s0, :], e1_mx[k], slice(128 * s, 128 * s + 128), w1_mx[h], slice(n0, 512))
                 part_psum[r, j] = acc
 
         def products(r):
-            if rounds[r][2] == 3 and PART_FIRST:
+            n, parts = rounds[r][2], rounds[r][5]
+            if len(parts) == 1:
                 part_products(r)
-                tile_products(r)
+                tile_products(r, 0, n)
             else:
-                tile_products(r)
+                tile_products(r, 0, n)
                 part_products(r)
-
-        def tile_width(r):
-            return 128 * (rounds[r][4] - rounds[r][3])
 
         def affine(r, i0, i1):
             k, h, n = rounds[r][0:3]
@@ -283,60 +274,42 @@ def tile_graph_gan_pa_kernel(tc, x, fe_w0, fe_b0, fe_w1_bytes, fe_w1_scale, fe_b
                 c = 4 * h + i
                 nc.scalar.activation(out=a_sb[r][:, w * i : w * i + w], in_=tile_psum[r, i], func=ACT.Identity, bias=b1_fifth[:, c : c + 1], scale=ALPHA)
 
-        def relu_vector(r, end, start=0):
-            if end == start:
-                return
+        def relu_vector(r, start, end):
             nc.vector.tensor_scalar(out=r_sb[r][:, start:end], in0=a_sb[r][:, start:end], scalar1=4.0, scalar2=0.0, op0=ALU.mult, op1=ALU.max)
 
         def relu_scalar(r, start, end):
-            if end > start:
-                nc.scalar.activation(out=r_sb[r][:, start:end], in_=a_sb[r][:, start:end], func=ACT.Relu, scale=4.0)
-
-        def relu_scalar_blocks(r, s0):
-            a = a_sb[r][:].rearrange("p (i c) -> p i c", i=2)[:, :, 128 * s0 : 128 * s0 + 256]
-            out_r = r_sb[r][:].rearrange("p (i c) -> p i c", i=2)[:, :, 128 * s0 : 128 * s0 + 256]
-            nc.scalar.activation(out=out_r, in_=a, func=ACT.Relu, scale=4.0)
+            nc.scalar.activation(out=r_sb[r][:, start:end], in_=a_sb[r][:, start:end], func=ACT.Relu, scale=4.0)
 
         def banks(r):
-            n, b0, b1 = rounds[r][2:5]
-            if r == last and BY_TILES:
-                return [[(i, s) for s in (2, 3) for i in (i0, i0 + 1)] for i0 in (0, 2)]
+            n, s0, s1 = rounds[r][2:5]
+            if r == last:
+                return [[(i, s) for s in range(s0, s1) for i in (i0, i0 + 1)] for i0 in (0, 2)]
             if n == 2:
-                return [[(i, s) for s in (s0, s0 + 1) for i in (0, 1)] for s0 in (0, 2)]
-            if b1 - b0 == 4 and r < v_done:
-                return [[(0, s) for s in range(4)], [(i, s) for s in (0, 1) for i in (1, 2)], [(i, s) for s in (2, 3) for i in (1, 2)]]
-            return [[(i, s) for i in range(n)] for s in range(b0, b1)]
+                return [[(i, s) for s in (b, b + 1) for i in (0, 1)] for b in (0, 2)]
+            if n == 3 and r < v_free:
+                return [[(0, s) for s in range(4)]] + [[(i, s) for s in (b, b + 1) for i in (1, 2)] for b in (0, 2)]
+            return [[(i, s) for i in range(n)] for s in range(s0, s1)]
 
-        def turn(r, g):
-            b0 = rounds[r][3]
-            held = banks(r)[g]
-            if g < 3:
-                acc = psum.tile([P, len(held), P], F32, name="turned", tag="turned", bufs=3)
-            else:
-                acc = psum.tile([P, len(held), P], F32, name="turned_fourth", tag="v", bufs=1)
-            for j, (i, s) in enumerate(held):
-                c0 = tile_width(r) * i + 128 * (s - b0)
-                for m, src in enumerate((a_sb[r], r_sb[r])):
-                    nc.tensor.matmul(acc[:, j, :], lhsT=src[:, c0 : c0 + 128], rhs=ident[:], is_transpose=True, start=(m == 0), stop=(m == 1))
-            turned[r, g] = acc
+        def turn(r):
+            for g, held in enumerate(banks(r)):
+                if g < 3:
+                    acc = psum.tile([P, len(held), P], F32, name="turned", tag="turned", bufs=3)
+                else:
+                    acc = psum.tile([P, len(held), P], F32, name="turned_fourth", tag="v", bufs=1)
+                for j, (i, s) in enumerate(held):
+                    c0 = tile_width(r) * i + 128 * (s - rounds[r][3])
+                    for m, src in enumerate((a_sb[r], r_sb[r])):
+                        nc.tensor.matmul(acc[:, j, :], lhsT=src[:, c0 : c0 + 128], rhs=ident[:], is_transpose=True, start=(m == 0), stop=(m == 1))
+                turned[r, g] = acc
 
-        def leave(r, g):
-            (i0, s0), (i1, s1) = banks(r)[g][0], banks(r)[g][-1]
-            bank = turned[r, g][:].rearrange("p j c -> p (j c)").rearrange("p (s c) -> p s c", s=s1 + 1 - s0)
+        def leave(r, g0, g1):
             k, h, n = rounds[r][0:3]
-            nc.scalar.copy(out=out_half(k, h)[:, s0 : s1 + 1, 128 * i0 : 128 * i1 + 128], in_=bank)
-            if r == last and BY_TILES:
-                if g == 1:
-                    store(k, h, 2, 4)
-            elif s0 == s1 and last - r in PAIR_TURNED:
-                if s0 % 2 == 1:
-                    store(k, h, s0 - 1, s0 + 1)
-            elif s0 == s1:
-                store(k, h, s0, s0 + 1)
-            elif n == 2:
-                store(k, h, s0, s1 + 1)
-            elif g > 0:
-                store(k, h, 2 * g - 2, 2 * g)
+            for g in range(g0, g1):
+                (i0, s0), (i1, s1) = banks(r)[g][0], banks(r)[g][-1]
+                bank = turned[r, g][:].rearrange("p j c -> p (j c)").rearrange("p (s c) -> p s c", s=s1 + 1 - s0)
+                nc.scalar.copy(out=out_half(k, h)[:, s0 : s1 + 1, 128 * i0 : 128 * i1 + 128], in_=bank)
+                if i1 == n - 1:
+                    store(k, h, s0, s1 + 1)
 
         def part_add(r, j):
             h, s0, s1, n0 = rounds[r][5][j]
@@ -351,21 +324,9 @@ def tile_graph_gan_pa_kernel(tc, x, fe_w0, fe_b0, fe_w1_bytes, fe_w1_scale, fe_b
             h, s0, s1, n0 = rounds[r][5][j]
             z = part_sums[r, j][:]
             nc.vector.scalar_tensor_tensor(out=out_half(k, h)[:, s0:s1, n0:512], in0=z, scalar=ALPHA, in1=z, op0=ALU.mult, op1=ALU.max)
-            if n0 == 0 and last - r in PAIR_DIRECT:
-                if s0 % 2 == 1:
-                    store(k, h, s0 - 1, s1)
-            elif n0 == 0:
+            if n0 == 0:
                 store(k, h, s0, s1)
 
-        def turn_all(r):
-            for g in range(len(banks(r))):
-                turn(r, g)
-
-        def leave_all(r):
-            for g in range(len(banks(r))):
-                leave(r, g)
-
-        half = ROWS // 2
         w1_widen(0)
         w1_weave(0, 0)
         w1_lay_gpsimd(0, 1)
@@ -381,182 +342,133 @@ def tile_graph_gan_pa_kernel(tc, x, fe_w0, fe_b0, fe_w1_bytes, fe_w1_scale, fe_b
         w1_leave(1, 0)
         nc.scalar.copy(out=v_sb[:], in_=v_psum)
         e1_quantise(0, 0, half)
-        tile_products(0)
+        tile_products(0, 0, 4)
         e1_lrelu(0, half, ROWS)
         w1_quantise(1)
         e1_add_gpsimd(1)
-        products(1)
+        tile_products(1, 0, 2)
         e1_quantise(0, half, ROWS)
+
+        wide = 4 * tile_width(0)
         affine(0, 0, 4)
         part_products(0)
+        tile_products(1, 2, 4)
         e1_add(1, 0, own_rows(1))
-        relu_scalar(0, 0, 512)
-        affine(1, 0, 2)
-        relu_scalar(0, 512, 1024)
-        affine(1, 2, 4)
+        relu_scalar(0, 0, wide // 2)
+        relu_scalar(0, wide // 2, wide)
+        affine(1, 0, 4)
         part_add(0, 0)
         part_add(0, 1)
-        turn_all(0)
+        turn(0)
         products(2)
-        e1_lrelu(1, 0, own_rows(1))
-        relu_vector(1, 1024 - R1_RELU)
-        e1_lrelu(1, own_rows(1), ROWS)
-        leave(0, 0)
-        relu_scalar(1, 1024 - R1_RELU, 1024)
-        leave(0, 1)
-        turn_all(1)
-        affine(2, 0, 4)
         part_lrelu(0, 0)
-        relu_vector(2, 1024 - R2_RELU)
-        e1_quantise(1, 0, ROWS)
+        relu_vector(1, 0, wide)
+        shares, halves = e1_shares(1)
+        for i0, i1 in shares:
+            e1_lrelu(1, i0, i1)
+        leave(0, 0, 2)
+        turn(1)
+        affine(2, 0, 4)
+        for i0, i1 in halves:
+            e1_quantise(1, i0, i1)
         e1_add_gpsimd(2)
         part_lrelu(0, 1)
         e1_add(2, 0, own_rows(2))
         products(3)
-        leave(1, 0)
-        relu_scalar(2, 1024 - R2_RELU, 1024)
-        leave(1, 1)
+        leave(1, 0, 1)
+        relu_scalar(2, 0, wide)
+        leave(1, 1, 2)
 
-        for r in range(opening, last - 3):
+        for r in range(opening, v_free):
             k, h, n = rounds[r][0:3]
             width = n * tile_width(r)
+            shares, halves = e1_shares(k + 1)
             affine(r, 0, n)
             if h == 0:
                 part_add(r, 0)
-                if r > opening:
+                if r == opening:
+                    split = width - SCALAR_RELU_FIRST
+                    e1_lrelu(k + 1, *shares[0])
+                    relu_vector(r, 0, split)
+                else:
+                    split = width - SCALAR_RELU
                     part_lrelu(r - 1, 0)
                     part_lrelu(r - 1, 1)
-                share = SCALAR_RELU if r > opening else R3_RELU
-                if r > opening:
-                    relu_vector(r, width - share)
-                if own_rows(k + 1) < half:
-                    e1_lrelu(k + 1, own_rows(k + 1), ROWS)
-                    e1_lrelu(k + 1, 0, own_rows(k + 1))
-                else:
-                    e1_lrelu(k + 1, 0, own_rows(k + 1))
-                    if r == opening:
-                        relu_vector(r, width - share)
-                    e1_lrelu(k + 1, own_rows(k + 1), ROWS)
+                    relu_vector(r, 0, split)
+                    e1_lrelu(k + 1, *shares[0])
+                e1_lrelu(k + 1, *shares[1])
             else:
-                if own_rows(k + 1) < half:
-                    e1_quantise(k + 1, half, ROWS)
-                    e1_quantise(k + 1, 0, half)
-                else:
-                    e1_quantise(k + 1, 0, half)
-                    e1_quantise(k + 1, half, ROWS)
+                split = 0
+                for i0, i1 in halves:
+                    e1_quantise(k + 1, i0, i1)
                 e1_add_gpsimd(k + 2)
                 part_lrelu(r - 1, 0)
                 part_add(r, 0)
                 part_add(r, 1)
                 e1_add(k + 2, 0, own_rows(k + 2))
-            turn_all(r - 1)
-            if r == last - 4 and T13:
-                part_products(r + 1)
-                tile_products(r + 1, 0, 2)
-            else:
-                products(r + 1)
-            if r == last - 4 and HALF13 == 1:
-                leave(r - 1, 0)
-                relu_scalar_blocks(r, 0)
-                leave(r - 1, 1)
-                leave(r - 1, 2)
-                relu_scalar_blocks(r, 2)
-            elif r == last - 4 and HALF13 == 2:
-                leave_all(r - 1)
-                relu_scalar(r, 0, width)
-            else:
-                leave(r - 1, 0)
-                relu_scalar(r, width - share if h == 0 else 0, width)
-                for g in range(1, len(banks(r - 1))):
-                    leave(r - 1, g)
+            turn(r - 1)
+            products(r + 1)
+            ahead = 1 if r < v_free - 1 else len(banks(r - 1))
+            leave(r - 1, 0, ahead)
+            relu_scalar(r, split, width)
+            leave(r - 1, ahead, len(banks(r - 1)))
 
         k = CHUNKS - 1
-        r = last - 3
+        r = v_free
+        split = 3 * tile_width(r) - SCALAR_RELU
         part_add(r, 0)
         part_lrelu(r - 1, 0)
         part_lrelu(r - 1, 1)
-        turn_all(r - 1)
-        if T13:
-            tile_products(r, 2, 3)
-        if MODE14 == 0:
-            affine(r, 0, 3)
-            products(r + 1)
-            leave(r - 1, 0)
-            relu_scalar(r, 1536 - R14_RELU, 1536)
-            leave(r - 1, 1)
-        elif MODE14 == 1:
-            affine(r, 0, 2)
-            leave(r - 1, 0)
-            affine(r, 2, 3)
-            products(r + 1)
-            leave(r - 1, 1)
-            relu_scalar(r, 1536 - R14_RELU, 1536)
-        else:
-            affine(r, 0, 1)
-            leave(r - 1, 0)
-            affine(r, 1, 2)
-            leave(r - 1, 1)
-            affine(r, 2, 3)
-            products(r + 1)
-            relu_scalar(r, 1536 - R14_RELU, 1536)
-        if RELU14_FIRST:
-            relu_vector(r, 1536 - R14_RELU)
+        turn(r - 1)
+        affine(r, 0, 2)
+        leave(r - 1, 0, 1)
+        affine(r, 2, 3)
+        products(r + 1)
+        leave(r - 1, 1, 2)
+        relu_scalar(r, split, 3 * tile_width(r))
+        relu_vector(r, 0, split)
         e1_lrelu(k, 0, half)
-        if not RELU14_FIRST:
-            relu_vector(r, 1536 - R14_RELU)
         part_lrelu(r, 0)
         e1_quantise(k, 0, half)
+
         r = last - 2
-        affine(r, 0, SPLIT15)
-        turn_all(r - 1)
+        affine(r, 0, 2)
+        turn(r - 1)
         part_add(r, 0)
         part_add(r, 1)
-        leave(r - 1, 0)
-        leave(r - 1, 1)
-        affine(r, SPLIT15, 4)
+        leave(r - 1, 0, 2)
+        affine(r, 2, 4)
         products(r + 1)
         part_lrelu(r, 0)
-        leave(r - 1, 2)
-        relu_vector(r, 1024 - R15_RELU)
-        leave(r - 1, 3)
-        relu_scalar(r, 1024 - R15_RELU, 1024)
+        leave(r - 1, 2, 3)
+        relu_vector(r, 0, wide)
+        leave(r - 1, 3, 4)
         e1_lrelu(k, half, ROWS)
         part_lrelu(r, 1)
         e1_quantise(k, half, ROWS)
+
         r = last - 1
         affine(r, 0, 4)
-        turn_all(r - 1)
+        turn(r - 1)
         part_add(r, 0)
-        if RELU16_EARLY:
-            relu_vector(r, 1024 - R16_RELU)
         part_add(r, 1)
         products(last)
-        if not RELU16_EARLY:
-            relu_vector(r, 1024 - R16_RELU)
-        leave(r - 1, 0)
-        relu_scalar(r, 1024 - R16_RELU, 1024)
-        leave(r - 1, 1)
+        relu_vector(r, 0, wide // 2)
+        leave(r - 1, 0, 1)
+        relu_scalar(r, wide // 2, wide)
+        leave(r - 1, 1, 2)
         part_lrelu(r, 0)
+
         r = last
         affine(r, 0, 4)
-        turn_all(r - 1)
-        if BY_TILES:
-            part_lrelu(r - 1, 1)
-            relu_vector(r, 512)
-            part_add(r, 0)
-            relu_vector(r, 1024, 512)
-        else:
-            part_lrelu(r - 1, 1)
-            part_add(r, 0)
-            relu_vector(r, 1024)
-        turn_all(r)
+        turn(r - 1)
+        part_lrelu(r - 1, 1)
+        relu_vector(r, 0, wide // 2)
+        part_add(r, 0)
+        relu_vector(r, wide // 2, wide)
+        turn(r)
         part_add(r, 1)
-        leave_all(r - 1)
+        leave(r - 1, 0, 2)
         part_lrelu(r, 0)
-        leave(r, 0)
-        if BY_TILES:
-            leave(r, 1)
-            part_lrelu(r, 1)
-        else:
-            part_lrelu(r, 1)
-            leave(r, 1)
+        leave(r, 0, 2)
+        part_lrelu(r, 1)

@@ -19,11 +19,8 @@ CHUNKS = 8
 PAIRS = 512
 ROWS = 16
 OWN_ROWS = 7
-OWN_ROWS_CHUNK_1 = 9
-OWN_ROWS_CHUNK_2 = 10
-SCALAR_RELU = 640
-SCALAR_RELU_FIRST = 384
-OUT_BUFFERS = 11
+SCALAR_RELU = 704
+OUT_BUFFERS = 5
 
 
 def tile_graph_gan_pa_kernel(tc, x, fe_w0, fe_b0, fe_w1_bytes, fe_w1_scale, fe_b1, out):
@@ -127,46 +124,29 @@ def tile_graph_gan_pa_kernel(tc, x, fe_w0, fe_b0, fe_w1_bytes, fe_w1_scale, fe_b
         nc.tensor.transpose(b1_turned[:], b1_rows[:], ident_bf[:])
         b1_fifth = keep.tile([P, 8], F32, name="b1_fifth")
 
-        w1_planes = [keep.tile([P, 4, 512], BF16, name="w1_planes%d" % q, align_bytes=64) for q in range(2)]
-        w1_laid = [w0_laid[1 - q][:].rearrange("p (n t) -> p n t", t=4) for q in range(2)]
-        w1_mx = [mx_operand(keep, "w1_%d" % q, 512, 1) for q in range(2)]
-        w1_woven = {}
+        w1_planes = keep.tile([P, 4, 4, 256], BF16, name="w1_planes", align_bytes=64)
+        w1_homes = [w0_laid[0][:, 0:1024], w0_laid[0][:, 1024:2048], w0_laid[1][:, 1024:2048], w0_laid[1][:, 0:1024]]
+        w1_mx = mx_operand(keep, "w1", 1024, 1)
 
         def w1_widen(q):
             for t in range(4):
-                n0 = 1024 * (t % 2) + 512 * q
-                nc.scalar.activation(out=w1_planes[q][:, t, :], in_=w1_bytes[t // 2][:, n0 : n0 + 512].bitcast(FP8), func=ACT.Copy, scale=w1_scale[:, t : t + 1])
+                n0 = 1024 * (t % 2) + 256 * q
+                nc.scalar.activation(out=w1_planes[:, q, t, :], in_=w1_bytes[t // 2][:, n0 : n0 + 256].bitcast(FP8), func=ACT.Copy, scale=w1_scale[:, t : t + 1])
 
-        def w1_weave(q, g):
-            acc = psum.tile([P, 2, 128, 4], BF16, name="w1_woven", tag="turned", bufs=3)
-            for m in range(2):
-                n0 = 256 * g + 128 * m
-                nc.tensor.matmul(acc[:, m], lhsT=ident_bf[:], rhs=w1_planes[q][:, :, n0 : n0 + 128].rearrange("p t n -> p n t"), start=True, stop=True)
-            w1_woven[q, g] = acc
+        def w1_lay_gpsimd(q):
+            nc.gpsimd.tensor_scalar(out=w1_homes[q].rearrange("p (n t) -> p n t", t=4), in0=w1_planes[:, q].rearrange("p t n -> p n t"), scalar1=1.0, scalar2=0.0, op0=ALU.mult, op1=ALU.add)
 
-        def w1_leave(q, g):
-            nc.scalar.copy(out=w1_laid[q][:, 256 * g : 256 * g + 256, :].rearrange("p n t -> p (n t)"), in_=w1_woven[q, g][:].rearrange("p m n t -> p (m n t)"))
-
-        def w1_lay_gpsimd(q, g):
-            cols = slice(256 * g, 256 * g + 256)
-            nc.gpsimd.tensor_scalar(out=w1_laid[q][:, cols, :], in0=w1_planes[q][:, :, cols].rearrange("p t n -> p n t"), scalar1=1.0, scalar2=0.0, op0=ALU.mult, op1=ALU.add)
-
-        def w1_lay_scalar(q, g):
-            cols = slice(256 * g, 256 * g + 256)
-            nc.scalar.copy(out=w1_laid[q][:, cols, :].rearrange("p (c i) t -> p c t i", i=4), in_=w1_planes[q][:, :, cols].rearrange("p t (c i) -> p c t i", i=4))
+        def w1_lay_scalar(q):
+            nc.scalar.copy(out=w1_homes[q].rearrange("p (c i t) -> p c t i", i=4, t=4), in_=w1_planes[:, q].rearrange("p t (c i) -> p c t i", i=4))
 
         def w1_quantise(q):
-            quantise(w1_mx[q][0][:], w1_mx[q][1][:], w1_laid[q].rearrange("p n t -> p (n t)"))
+            cols = slice(256 * q, 256 * q + 256)
+            quantise(w1_mx[0][:, cols], w1_mx[1][:, cols], w1_homes[q])
 
         pair_sums = {}
         e1_mx = {}
         e1_tiles = [keep.tile([P, 5 * PAIRS], BF16, name="e1_tile%d" % j, align_bytes=64) for j in range(2)]
         half = ROWS // 2
-
-        def own_rows(k):
-            if k == CHUNKS - 1:
-                return half
-            return {1: OWN_ROWS_CHUNK_1, 2: OWN_ROWS_CHUNK_2}.get(k, OWN_ROWS)
 
         def pair_operands(k, i0, i1, v):
             graph = k // 2
@@ -181,12 +161,11 @@ def tile_graph_gan_pa_kernel(tc, x, fe_w0, fe_b0, fe_w1_bytes, fe_w1_scale, fe_b
             nc.vector.tensor_tensor(out=z[:], in0=in0, in1=in1, op=ALU.add)
             pair_sums[k, i0] = z[:].rearrange("p i j t -> p (i j t)")
 
-        def e1_add_gpsimd(k):
-            i0 = own_rows(k)
-            home = w0_laid[0] if k == 1 else e1_tiles[(k - 1) % 2]
+        def e1_add_gpsimd(k, i0, i1):
+            home = e1_tiles[(k - 1) % 2]
             end = home.shape[1] // 2
-            z = home[:].bitcast(F32)[:, end - 128 * (ROWS - i0) : end]
-            in0, in1 = pair_operands(k, i0, ROWS, v_sb)
+            z = home[:].bitcast(F32)[:, end - 128 * (i1 - i0) : end]
+            in0, in1 = pair_operands(k, i0, i1, v_sb)
             nc.gpsimd.tensor_tensor(out=z.rearrange("p (i j t) -> p i j t", j=32, t=4), in0=in0, in1=in1, op=ALU.add)
             pair_sums[k, i0] = z
 
@@ -200,24 +179,6 @@ def tile_graph_gan_pa_kernel(tc, x, fe_w0, fe_b0, fe_w1_bytes, fe_w1_scale, fe_b
             cols = slice(32 * i0, 32 * i1)
             quantise(e1_mx[k][0][:, cols], e1_mx[k][1][:, cols], e1_tiles[k % 2][:, 128 * i0 : 128 * i1])
 
-        def e1_shares(k):
-            shares = [(0, own_rows(k)), (own_rows(k), ROWS)]
-            halves = [(0, half), (half, ROWS)]
-            if own_rows(k) < half:
-                return shares[::-1], halves[::-1]
-            return shares, halves
-
-        opening = 3
-        rounds = [(0, 0, 4, 0, 2, [(0, 2, 3, 0), (0, 3, 4, 0)]), (0, 1, 4, 0, 2, []), (0, 1, 4, 2, 4, [])]
-        for k in range(1, CHUNKS - 1):
-            rounds.append((k, 0, 3, 0, 4, [(0, 0, 4, 384)]))
-            if k < CHUNKS - 2:
-                rounds.append((k, 1, 2, 0, 4, [(1, 0, 2, 256), (1, 2, 4, 256)]))
-        rounds.append((CHUNKS - 2, 1, 4, 0, 2, [(1, 2, 3, 0), (1, 3, 4, 0)]))
-        for s0 in (0, 2):
-            rounds.append((CHUNKS - 1, 0, 4, s0, s0 + 2, [(1, s0, s0 + 1, 0), (1, s0 + 1, s0 + 2, 0)]))
-        last = len(rounds) - 1
-        v_free = last - 3
         tile_psum = {}
         part_psum = {}
         a_sb = {}
@@ -226,249 +187,220 @@ def tile_graph_gan_pa_kernel(tc, x, fe_w0, fe_b0, fe_w1_bytes, fe_w1_scale, fe_b
         part_sums = {}
         out_sb = {}
 
-        def out_half(k, h):
-            if (k, h) not in out_sb:
-                out_sb[k, h] = work.tile([P, 4, 512], F32, name="out_sb", bufs=OUT_BUFFERS)
-            return out_sb[k, h]
+        def out_rows(k):
+            if k not in out_sb:
+                out_sb[k] = work.tile([P, 4, 1024], F32, name="out_sb", bufs=OUT_BUFFERS)
+            return out_sb[k]
 
-        def store(k, h, s0, s1):
-            dst = rows[PAIRS * k + 128 * s0 : PAIRS * k + 128 * s1, 512 * h : 512 * h + 512]
-            nc.sync.dma_start(out=dst.rearrange("(s p) c -> p s c", p=P), in_=out_half(k, h)[:, s0:s1, :])
+        def store(k, s0, s1, n0, n1):
+            dst = rows[PAIRS * k + 128 * s0 : PAIRS * k + 128 * s1, n0:n1]
+            nc.sync.dma_start(out=dst.rearrange("(s p) c -> p s c", p=P), in_=out_rows(k)[:, s0:s1, n0:n1])
 
-        def tile_width(r):
-            return 128 * (rounds[r][4] - rounds[r][3])
+        def tile_products(group, c0, c1):
+            k, s0, s1 = group[0], group[3], group[4]
+            acc = psum.tile([P, c1 - c0, 128 * (s1 - s0)], F32, name="tile_psum", tag="product")
+            for c in range(c0, c1):
+                product(acc[:, c - c0, :], w1_mx, slice(128 * c, 128 * c + 128), e1_mx[k], slice(128 * s0, 128 * s1))
+                tile_psum[group, c] = acc[:, c - c0, :]
 
-        def tile_products(r, first, end):
-            k, h, n, s0, s1, parts = rounds[r]
-            per_bank = 512 // tile_width(r)
-            for i0 in range(first, end, per_bank):
-                acc = psum.tile([P, per_bank, tile_width(r)], F32, name="tile_psum", tag="product")
-                for i in range(i0, i0 + per_bank):
-                    product(acc[:, i - i0, :], w1_mx[h], slice(128 * i, 128 * i + 128), e1_mx[k], slice(128 * s0, 128 * s1))
-                    tile_psum[r, i] = acc[:, i - i0, :]
+        def part_products(part):
+            k, s0, s1, n0, n1 = part
+            acc = psum.tile([P, s1 - s0, n1 - n0], F32, name="part_psum", tag="product")
+            for s in range(s0, s1):
+                product(acc[:, s - s0, :], e1_mx[k], slice(128 * s, 128 * s + 128), w1_mx, slice(n0, n1))
+            part_psum[part] = acc
 
-        def part_products(r):
-            k = rounds[r][0]
-            for j, (h, s0, s1, n0) in enumerate(rounds[r][5]):
-                acc = psum.tile([P, s1 - s0, 512 - n0], F32, name="part_psum", tag="product")
-                for s in range(s0, s1):
-                    product(acc[:, s - s0, :], e1_mx[k], slice(128 * s, 128 * s + 128), w1_mx[h], slice(n0, 512))
-                part_psum[r, j] = acc
+        def affine(group, c0, c1):
+            w = 128 * (group[4] - group[3])
+            if group not in a_sb:
+                a_sb[group] = work.tile([P, (group[2] - group[1]) * w], F32, name="a_sb", bufs=3)
+                r_sb[group] = work.tile([P, (group[2] - group[1]) * w], F32, name="r_sb", bufs=3)
+            for c in range(c0, c1):
+                i = c - group[1]
+                nc.scalar.activation(out=a_sb[group][:, w * i : w * i + w], in_=tile_psum[group, c], func=ACT.Identity, bias=b1_fifth[:, c : c + 1], scale=ALPHA)
 
-        def products(r):
-            n, parts = rounds[r][2], rounds[r][5]
-            if len(parts) == 1:
-                part_products(r)
-                tile_products(r, 0, n)
-            else:
-                tile_products(r, 0, n)
-                part_products(r)
+        def relu_vector(group, start, end):
+            nc.vector.tensor_scalar(out=r_sb[group][:, start:end], in0=a_sb[group][:, start:end], scalar1=4.0, scalar2=0.0, op0=ALU.mult, op1=ALU.max)
 
-        def affine(r, i0, i1):
-            k, h, n = rounds[r][0:3]
-            w = tile_width(r)
-            if i0 == 0:
-                a_sb[r] = work.tile([P, n * w], F32, name="a_sb", bufs=3)
-                r_sb[r] = work.tile([P, n * w], F32, name="r_sb", bufs=3)
-            for i in range(i0, i1):
-                c = 4 * h + i
-                nc.scalar.activation(out=a_sb[r][:, w * i : w * i + w], in_=tile_psum[r, i], func=ACT.Identity, bias=b1_fifth[:, c : c + 1], scale=ALPHA)
+        def relu_scalar(group, start, end):
+            nc.scalar.activation(out=r_sb[group][:, start:end], in_=a_sb[group][:, start:end], func=ACT.Relu, scale=4.0)
 
-        def relu_vector(r, start, end):
-            nc.vector.tensor_scalar(out=r_sb[r][:, start:end], in0=a_sb[r][:, start:end], scalar1=4.0, scalar2=0.0, op0=ALU.mult, op1=ALU.max)
+        def turn(group, c0, c1, s0, s1, tag="turned"):
+            w = 128 * (group[4] - group[3])
+            acc = psum.tile([P, s1 - s0, c1 - c0, P], F32, name="turned", tag=tag, bufs=3 if tag == "turned" else 1)
+            for s in range(s0, s1):
+                for c in range(c0, c1):
+                    n0 = w * (c - group[1]) + 128 * (s - group[3])
+                    for m, src in enumerate((a_sb[group], r_sb[group])):
+                        nc.tensor.matmul(acc[:, s - s0, c - c0, :], lhsT=src[:, n0 : n0 + 128], rhs=ident[:], is_transpose=True, start=(m == 0), stop=(m == 1))
+            turned[group[0], c0, s0] = (acc, c1, s1)
 
-        def relu_scalar(r, start, end):
-            nc.scalar.activation(out=r_sb[r][:, start:end], in_=a_sb[r][:, start:end], func=ACT.Relu, scale=4.0)
+        def leave(k, c0, s0):
+            acc, c1, s1 = turned[k, c0, s0]
+            nc.scalar.copy(out=out_rows(k)[:, s0:s1, 128 * c0 : 128 * c1], in_=acc[:].rearrange("p s c m -> p s (c m)"))
 
-        def banks(r):
-            n, s0, s1 = rounds[r][2:5]
-            if r == last:
-                return [[(i, s) for s in range(s0, s1) for i in (i0, i0 + 1)] for i0 in (0, 2)]
-            if n == 2:
-                return [[(i, s) for s in (b, b + 1) for i in (0, 1)] for b in (0, 2)]
-            if n == 3 and r < v_free:
-                return [[(0, s) for s in range(4)]] + [[(i, s) for s in (b, b + 1) for i in (1, 2)] for b in (0, 2)]
-            return [[(i, s) for i in range(n)] for s in range(s0, s1)]
-
-        def turn(r):
-            for g, held in enumerate(banks(r)):
-                if g < 3:
-                    acc = psum.tile([P, len(held), P], F32, name="turned", tag="turned", bufs=3)
-                else:
-                    acc = psum.tile([P, len(held), P], F32, name="turned_fourth", tag="v", bufs=1)
-                for j, (i, s) in enumerate(held):
-                    c0 = tile_width(r) * i + 128 * (s - rounds[r][3])
-                    for m, src in enumerate((a_sb[r], r_sb[r])):
-                        nc.tensor.matmul(acc[:, j, :], lhsT=src[:, c0 : c0 + 128], rhs=ident[:], is_transpose=True, start=(m == 0), stop=(m == 1))
-                turned[r, g] = acc
-
-        def leave(r, g0, g1):
-            k, h, n = rounds[r][0:3]
-            for g in range(g0, g1):
-                (i0, s0), (i1, s1) = banks(r)[g][0], banks(r)[g][-1]
-                bank = turned[r, g][:].rearrange("p j c -> p (j c)").rearrange("p (s c) -> p s c", s=s1 + 1 - s0)
-                nc.scalar.copy(out=out_half(k, h)[:, s0 : s1 + 1, 128 * i0 : 128 * i1 + 128], in_=bank)
-                if i1 == n - 1:
-                    store(k, h, s0, s1 + 1)
-
-        def part_add(r, j):
-            h, s0, s1, n0 = rounds[r][5][j]
-            shape = [P, s1 - s0, 512 - n0]
+        def part_add(part):
+            k, s0, s1, n0, n1 = part
+            shape = [P, s1 - s0, n1 - n0]
             z = work.tile(shape, F32, name="part_sums", bufs=4)
-            bias = b1_spread[:, 512 * h + n0 : 512 * h + 512]
-            nc.vector.tensor_tensor(out=z[:], in0=part_psum[r, j][:], in1=bias.unsqueeze(1).to_broadcast(shape), op=ALU.add)
-            part_sums[r, j] = z
+            nc.vector.tensor_tensor(out=z[:], in0=part_psum[part][:], in1=b1_spread[:, n0:n1].unsqueeze(1).to_broadcast(shape), op=ALU.add)
+            part_sums[part] = z
 
-        def part_lrelu(r, j):
-            k = rounds[r][0]
-            h, s0, s1, n0 = rounds[r][5][j]
-            z = part_sums[r, j][:]
-            nc.vector.scalar_tensor_tensor(out=out_half(k, h)[:, s0:s1, n0:512], in0=z, scalar=ALPHA, in1=z, op0=ALU.mult, op1=ALU.max)
-            if n0 == 0:
-                store(k, h, s0, s1)
+        def part_lrelu(part):
+            k, s0, s1, n0, n1 = part
+            z = part_sums[part][:]
+            nc.vector.scalar_tensor_tensor(out=out_rows(k)[:, s0:s1, n0:n1], in0=z, scalar=ALPHA, in1=z, op0=ALU.mult, op1=ALU.max)
 
-        w1_widen(0)
-        w1_weave(0, 0)
-        w1_lay_gpsimd(0, 1)
+        def first(k):
+            return (k, 0, 3, 0, 4)
+
+        def second(k):
+            return (k, 6, 8, 0, 4)
+
+        def own_rows(k):
+            return {1: 8, CHUNKS - 1: half}.get(k, OWN_ROWS)
+
+        def parts(k):
+            return [(k, 0, 2, 512, 768), (k, 2, 4, 512, 768), (k, 0, 4, 384, 512)]
+
+        w1_widen(2)
+        w1_lay_gpsimd(2)
         e1_add(0, 0, half)
-        w1_widen(1)
-        nc.scalar.activation(out=b1_fifth[:], in_=b1_turned[:, 0:8], func=ACT.Copy, scale=ALPHA)
-        w1_weave(1, 0)
+        w1_widen(0)
         e1_add(0, half, ROWS)
-        w1_leave(0, 0)
-        w1_lay_scalar(1, 1)
+        w1_widen(1)
+        w1_lay_scalar(0)
         e1_lrelu(0, 0, half)
-        w1_quantise(0)
-        w1_leave(1, 0)
-        nc.scalar.copy(out=v_sb[:], in_=v_psum)
+        w1_quantise(2)
         e1_quantise(0, 0, half)
-        tile_products(0, 0, 4)
+        part_products(parts(0)[0])
+        w1_lay_scalar(1)
         e1_lrelu(0, half, ROWS)
-        w1_quantise(1)
-        e1_add_gpsimd(1)
-        tile_products(1, 0, 2)
-        e1_quantise(0, half, ROWS)
+        nc.scalar.copy(out=v_sb[:], in_=v_psum)
+        nc.scalar.activation(out=b1_fifth[:], in_=b1_turned[:, 0:8], func=ACT.Copy, scale=ALPHA)
+        w1_quantise(0)
+        w1_widen(3)
+        w1_lay_scalar(3)
 
-        wide = 4 * tile_width(0)
-        affine(0, 0, 4)
-        part_products(0)
-        tile_products(1, 2, 4)
-        e1_add(1, 0, own_rows(1))
-        relu_scalar(0, 0, wide // 2)
-        relu_scalar(0, wide // 2, wide)
-        affine(1, 0, 4)
-        part_add(0, 0)
-        part_add(0, 1)
-        turn(0)
-        products(2)
-        part_lrelu(0, 0)
-        relu_vector(1, 0, wide)
-        shares, halves = e1_shares(1)
-        for i0, i1 in shares:
-            e1_lrelu(1, i0, i1)
-        leave(0, 0, 2)
-        turn(1)
-        affine(2, 0, 4)
-        for i0, i1 in halves:
-            e1_quantise(1, i0, i1)
-        e1_add_gpsimd(2)
-        part_lrelu(0, 1)
-        e1_add(2, 0, own_rows(2))
-        products(3)
-        leave(1, 0, 1)
-        relu_scalar(2, 0, wide)
-        leave(1, 1, 2)
-
-        for r in range(opening, v_free):
-            k, h, n = rounds[r][0:3]
-            width = n * tile_width(r)
-            shares, halves = e1_shares(k + 1)
-            affine(r, 0, n)
-            if h == 0:
-                part_add(r, 0)
-                if r == opening:
-                    split = width - SCALAR_RELU_FIRST
-                    e1_lrelu(k + 1, *shares[0])
-                    relu_vector(r, 0, split)
-                else:
-                    split = width - SCALAR_RELU
-                    part_lrelu(r - 1, 0)
-                    part_lrelu(r - 1, 1)
-                    relu_vector(r, 0, split)
-                    e1_lrelu(k + 1, *shares[0])
-                e1_lrelu(k + 1, *shares[1])
+        for k in range(CHUNKS - 1):
+            x_part, y_part, z_part = parts(k)
+            own = own_rows(k + 1)
+            if k > 0:
+                affine(second(k - 1), 6, 8)
+                e1_quantise(k, half, ROWS)
+                e1_quantise(k, 0, half)
+                e1_add_gpsimd(k + 1, own, ROWS)
+                part_lrelu(parts(k - 1)[2])
+                turn(first(k - 1), 0, 1, 0, 4)
+                turn(first(k - 1), 1, 3, 0, 2)
+                turn(first(k - 1), 1, 3, 2, 4)
+                part_products(x_part)
+                part_products(y_part)
+                part_products(z_part)
+                tile_products(first(k), 0, 1)
             else:
-                split = 0
-                for i0, i1 in halves:
-                    e1_quantise(k + 1, i0, i1)
-                e1_add_gpsimd(k + 2)
-                part_lrelu(r - 1, 0)
-                part_add(r, 0)
-                part_add(r, 1)
-                e1_add(k + 2, 0, own_rows(k + 2))
-            turn(r - 1)
-            products(r + 1)
-            ahead = 1 if r < v_free - 1 else len(banks(r - 1))
-            leave(r - 1, 0, ahead)
-            relu_scalar(r, split, width)
-            leave(r - 1, ahead, len(banks(r - 1)))
+                e1_quantise(k, half, ROWS)
+                e1_add_gpsimd(k + 1, own, ROWS)
+                w1_quantise(1)
+                part_products(y_part)
+                tile_products(first(k), 0, 1)
+                part_products(z_part)
+            e1_add(k + 1, 0, own)
+            if k > 0:
+                leave(k - 1, 0, 0)
+                relu_scalar(second(k - 1), 0, 1024)
+                leave(k - 1, 1, 0)
+                store(k - 1, 0, 2, 0, 512)
+                leave(k - 1, 1, 2)
+                store(k - 1, 2, 4, 0, 512)
+            affine(first(k), 0, 1)
+            part_add(x_part)
+            tile_products(first(k), 1, 2)
+            part_add(y_part)
+            tile_products(first(k), 2, 3)
+            part_add(z_part)
+            affine(first(k), 1, 3)
+            part_lrelu(x_part)
+            part_lrelu(y_part)
+            store(k, 0, 4, 512, 768)
+            if k > 0:
+                turn(second(k - 1), 6, 8, 0, 2)
+                turn(second(k - 1), 6, 8, 2, 4)
+            else:
+                w1_quantise(3)
+            tile_products(second(k), 6, 7)
+            tile_products(second(k), 7, 8)
+            split = 1536 - SCALAR_RELU
+            if k > 0:
+                relu_vector(first(k), 0, split)
+            if k < CHUNKS - 2:
+                e1_lrelu(k + 1, own, ROWS)
+            else:
+                e1_lrelu(k + 1, 0, half)
+            if k > 0:
+                leave(k - 1, 6, 0)
+                relu_scalar(first(k), split, 1536)
+                leave(k - 1, 6, 2)
+                store(k - 1, 0, 4, 768, 1024)
+            else:
+                relu_scalar(first(k), 0, 768)
+                relu_scalar(first(k), 768, 1536)
+            if k < CHUNKS - 2:
+                e1_lrelu(k + 1, 0, own)
 
         k = CHUNKS - 1
-        r = v_free
-        split = 3 * tile_width(r) - SCALAR_RELU
-        part_add(r, 0)
-        part_lrelu(r - 1, 0)
-        part_lrelu(r - 1, 1)
-        turn(r - 1)
-        affine(r, 0, 2)
-        leave(r - 1, 0, 1)
-        affine(r, 2, 3)
-        products(r + 1)
-        leave(r - 1, 1, 2)
-        relu_scalar(r, split, 3 * tile_width(r))
-        relu_vector(r, 0, split)
-        e1_lrelu(k, 0, half)
-        part_lrelu(r, 0)
+        early, late = (k, 0, 4, 0, 2), (k, 0, 2, 2, 4)
+        ends = [(k, 0, 1, 512, 1024), (k, 1, 2, 512, 1024), (k, 2, 4, 256, 512), (k, 2, 3, 512, 1024), (k, 3, 4, 512, 1024)]
+        part_lrelu(parts(k - 1)[2])
         e1_quantise(k, 0, half)
-
-        r = last - 2
-        affine(r, 0, 2)
-        turn(r - 1)
-        part_add(r, 0)
-        part_add(r, 1)
-        leave(r - 1, 0, 2)
-        affine(r, 2, 4)
-        products(r + 1)
-        part_lrelu(r, 0)
-        leave(r - 1, 2, 3)
-        relu_vector(r, 0, wide)
-        leave(r - 1, 3, 4)
+        turn(first(k - 1), 0, 1, 0, 4)
+        affine(second(k - 1), 6, 8)
+        turn(first(k - 1), 1, 3, 0, 2)
+        turn(first(k - 1), 1, 3, 2, 4, "v")
+        tile_products(early, 0, 2)
+        tile_products(early, 2, 4)
+        part_products(ends[0])
+        part_products(ends[1])
         e1_lrelu(k, half, ROWS)
-        part_lrelu(r, 1)
+        leave(k - 1, 0, 0)
+        leave(k - 1, 1, 0)
+        store(k - 1, 0, 2, 0, 512)
+        leave(k - 1, 1, 2)
+        store(k - 1, 2, 4, 0, 512)
+        relu_vector(second(k - 1), 0, 1024)
         e1_quantise(k, half, ROWS)
-
-        r = last - 1
-        affine(r, 0, 4)
-        turn(r - 1)
-        part_add(r, 0)
-        part_add(r, 1)
-        products(last)
-        relu_vector(r, 0, wide // 2)
-        leave(r - 1, 0, 1)
-        relu_scalar(r, wide // 2, wide)
-        leave(r - 1, 1, 2)
-        part_lrelu(r, 0)
-
-        r = last
-        affine(r, 0, 4)
-        turn(r - 1)
-        part_lrelu(r - 1, 1)
-        relu_vector(r, 0, wide // 2)
-        part_add(r, 0)
-        relu_vector(r, wide // 2, wide)
-        turn(r)
-        part_add(r, 1)
-        leave(r - 1, 0, 2)
-        part_lrelu(r, 0)
-        leave(r, 0, 2)
-        part_lrelu(r, 1)
+        part_add(ends[0])
+        part_add(ends[1])
+        affine(early, 0, 4)
+        turn(second(k - 1), 6, 8, 0, 2)
+        turn(second(k - 1), 6, 8, 2, 4)
+        tile_products(late, 0, 2)
+        part_products(ends[2])
+        part_lrelu(ends[0])
+        store(k, 0, 1, 512, 1024)
+        part_products(ends[3])
+        part_products(ends[4])
+        leave(k - 1, 6, 0)
+        affine(late, 0, 2)
+        relu_vector(early, 0, 1024)
+        leave(k - 1, 6, 2)
+        store(k - 1, 0, 4, 768, 1024)
+        part_lrelu(ends[1])
+        store(k, 1, 2, 512, 1024)
+        relu_scalar(late, 0, 512)
+        turn(early, 0, 4, 0, 1)
+        turn(early, 0, 4, 1, 2, "v")
+        turn(late, 0, 2, 2, 4)
+        part_add(ends[2])
+        part_add(ends[3])
+        part_lrelu(ends[2])
+        leave(k, 0, 0)
+        store(k, 0, 1, 0, 512)
+        part_add(ends[4])
+        leave(k, 0, 1)
+        store(k, 1, 2, 0, 512)
+        part_lrelu(ends[3])
+        leave(k, 0, 2)
+        store(k, 2, 3, 0, 1024)
+        part_lrelu(ends[4])
+        store(k, 3, 4, 0, 1024)

@@ -18,8 +18,10 @@ ALPHA = 0.2
 CHUNKS = 8
 PAIRS = 512
 ROWS = 16
+HALF = ROWS // 2
 OWN_ROWS = 7
-SCALAR_RELU = 704
+OWN_ROWS_CHUNK_1 = 10
+SCALAR_RELU = 768
 OUT_BUFFERS = 5
 
 
@@ -40,15 +42,15 @@ def tile_graph_gan_pa_kernel(tc, x, fe_w0, fe_b0, fe_w1_bytes, fe_w1_scale, fe_b
         b0_sb = keep.tile([P, 4], BF16, name="b0_sb")
         b1_rows = keep.tile([P, P], BF16, name="b1_rows")
         b1_spread = keep.tile([P, 1024], BF16, name="b1_spread")
-        w0_rows = fe_w0.rearrange("(h p t) w -> h p t w", h=2, t=4)
+        w0_rows = fe_w0.rearrange("(h p j) w -> h p j w", h=2, j=4)
         w1_rows = fe_w1_bytes.rearrange("(p t) n -> p (t n)", t=4)
         nc.sync.dma_start(out=x_sb[:], in_=x.rearrange("b n d -> (b n) d"))
-        nc.sync.dma_start(out=w0_raw[0][:], in_=w0_rows[0])
-        nc.sync.dma_start(out=w0_raw[1][:], in_=w0_rows[1])
+        for h in range(2):
+            nc.sync.dma_start(out=w0_raw[h][:], in_=w0_rows[h])
+        nc.sync.dma_start(out=w1_scale[:], in_=fe_w1_scale.rearrange("(p t) o -> p (t o)", t=4))
+        nc.sync.dma_start(out=b0_sb[:], in_=fe_b0.rearrange("(p t) -> p t", t=4))
         for g in range(2):
             nc.sync.dma_start(out=w1_bytes[g][:], in_=w1_rows[:, 2048 * g : 2048 * g + 2048])
-        nc.scalar.dma_start(out=w1_scale[:], in_=fe_w1_scale.rearrange("(p t) o -> p (t o)", t=4))
-        nc.scalar.dma_start(out=b0_sb[:], in_=fe_b0.rearrange("(p t) -> p t", t=4))
 
         ident = keep.tile([P, P], F32, name="ident")
         ident_bf = keep.tile([P, P], BF16, name="ident_bf")
@@ -78,7 +80,7 @@ def tile_graph_gan_pa_kernel(tc, x, fe_w0, fe_b0, fe_w1_bytes, fe_w1_scale, fe_b
             return codes, scales
 
         x_words = x_sb[:].bitcast(F32)
-        x_turned = psum.tile([P, 2, P], F32, name="x_turned", tag="product")
+        x_turned = psum.tile([P, 2, P], F32, name="x_turned", tag="turned", bufs=3)
         for u in range(2):
             nc.tensor.transpose(x_turned[:, u, :], x_words[:, u:256:2], ident[:])
         x_laid = keep.tile([P, 4 * P], BF16, name="x_laid", align_bytes=64)
@@ -87,23 +89,20 @@ def tile_graph_gan_pa_kernel(tc, x, fe_w0, fe_b0, fe_w1_bytes, fe_w1_scale, fe_b
         w0_mx = [mx_operand(keep, "w0_%d" % h, 512, 1) for h in range(2)]
 
         def w0_lay(h, t0, t1, copy):
-            dst = w0_laid[h][:].rearrange("p (t m j) -> p t m j", t=4, j=4)
-            src = w0_raw[h][:].rearrange("p j (m t) -> p t m j", t=4)
-            copy(out=dst[:, t0:t1], in_=src[:, t0:t1])
+            dst = w0_laid[h][:].rearrange("p (t c i j) -> p c t i j", t=4, i=2, j=4)
+            src = w0_raw[h][:].rearrange("p j (c i t) -> p c t i j", i=2, t=4)
+            copy(out=dst[:, :, t0:t1], in_=src[:, :, t0:t1])
 
-        def w0_quantise(h, t0):
-            cols = slice(128 * t0, 128 * t0 + 256)
-            quantise(w0_mx[h][0][:, cols], w0_mx[h][1][:, cols], w0_laid[h][:, 512 * t0 : 512 * t0 + 1024])
+        def w0_quantise(h, g):
+            cols = slice(256 * g, 256 * g + 256)
+            quantise(w0_mx[h][0][:, cols], w0_mx[h][1][:, cols], w0_laid[h][:, 1024 * g : 1024 * g + 1024])
 
-        def first_layer(h):
-            if h == 0:
-                acc = psum.tile([P, 4, P], F32, name="first_u", tag="product")
-            else:
-                acc = psum.tile([P, 4, P], F32, name="first_v", tag="v", bufs=1)
-            for t in range(4):
+        def first_layer(h, acc, g):
+            for t in range(2 * g, 2 * g + 2):
                 product(acc[:, t, :], w0_mx[h], slice(128 * t, 128 * t + 128), x_mx, slice(0, P))
-            return acc[:].rearrange("p t n -> p n t")
 
+        u_acc = psum.tile([P, 4, P], F32, name="first_u", tag="turned", bufs=3)
+        v_acc = psum.tile([P, 4, P], F32, name="first_v", tag="v", bufs=1)
         nc.vector.tensor_copy(out=x_laid[:].bitcast(F32).rearrange("p (n u) -> p n u", u=2), in_=x_turned[:].rearrange("p u n -> p n u"))
         w0_lay(0, 2, 4, nc.scalar.copy)
         w0_lay(1, 3, 4, nc.scalar.copy)
@@ -111,12 +110,15 @@ def tile_graph_gan_pa_kernel(tc, x, fe_w0, fe_b0, fe_w1_bytes, fe_w1_scale, fe_b
         quantise(x_mx[0][:], x_mx[1][:], x_laid[:])
         w0_quantise(0, 0)
         w0_lay(1, 0, 2, nc.vector.tensor_copy)
-        w0_quantise(0, 2)
+        w0_quantise(0, 1)
         w0_lay(1, 2, 3, nc.vector.tensor_copy)
-        u_psum = first_layer(0)
-        w0_quantise(1, 0)
-        w0_quantise(1, 2)
-        v_psum = first_layer(1)
+        for g in range(2):
+            first_layer(0, u_acc, g)
+        for g in range(2):
+            w0_quantise(1, g)
+            first_layer(1, v_acc, g)
+        u_psum = u_acc[:].rearrange("p t n -> p n t")
+        v_psum = v_acc[:].rearrange("p t n -> p n t")
         u_sb = keep.tile([P, P, 4], F32, name="u_sb")
         v_sb = keep.tile([P, P, 4], F32, name="v_sb")
         nc.vector.tensor_tensor(out=u_sb[:], in0=u_psum, in1=b0_sb[:].unsqueeze(1).to_broadcast([P, P, 4]), op=ALU.add)
@@ -124,20 +126,20 @@ def tile_graph_gan_pa_kernel(tc, x, fe_w0, fe_b0, fe_w1_bytes, fe_w1_scale, fe_b
         nc.tensor.transpose(b1_turned[:], b1_rows[:], ident_bf[:])
         b1_fifth = keep.tile([P, 8], F32, name="b1_fifth")
 
-        w1_planes = keep.tile([P, 4, 4, 256], BF16, name="w1_planes", align_bytes=64)
-        w1_homes = [w0_laid[0][:, 0:1024], w0_laid[0][:, 1024:2048], w0_laid[1][:, 1024:2048], w0_laid[1][:, 0:1024]]
+        w1_planes = [keep.tile([P, 4, 256], BF16, name="w1_planes%d" % q, align_bytes=64) for q in range(4)]
+        w1_homes = [w0_laid[0][:, 0:1024], w0_laid[1][:, 1024:2048], w0_laid[1][:, 0:1024], w0_laid[0][:, 1024:2048]]
         w1_mx = mx_operand(keep, "w1", 1024, 1)
 
-        def w1_widen(q):
-            for t in range(4):
+        def w1_widen(q, t0=0, t1=4):
+            for t in range(t0, t1):
                 n0 = 1024 * (t % 2) + 256 * q
-                nc.scalar.activation(out=w1_planes[:, q, t, :], in_=w1_bytes[t // 2][:, n0 : n0 + 256].bitcast(FP8), func=ACT.Copy, scale=w1_scale[:, t : t + 1])
+                nc.scalar.activation(out=w1_planes[q][:, t, :], in_=w1_bytes[t // 2][:, n0 : n0 + 256].bitcast(FP8), func=ACT.Copy, scale=w1_scale[:, t : t + 1])
+
+        def w1_lay(q):
+            nc.scalar.copy(out=w1_homes[q].rearrange("p (c i t) -> p c t i", i=4, t=4), in_=w1_planes[q][:].rearrange("p t (c i) -> p c t i", i=4))
 
         def w1_lay_gpsimd(q):
-            nc.gpsimd.tensor_scalar(out=w1_homes[q].rearrange("p (n t) -> p n t", t=4), in0=w1_planes[:, q].rearrange("p t n -> p n t"), scalar1=1.0, scalar2=0.0, op0=ALU.mult, op1=ALU.add)
-
-        def w1_lay_scalar(q):
-            nc.scalar.copy(out=w1_homes[q].rearrange("p (c i t) -> p c t i", i=4, t=4), in_=w1_planes[:, q].rearrange("p t (c i) -> p c t i", i=4))
+            nc.gpsimd.tensor_scalar(out=w1_homes[q].rearrange("p (n t) -> p n t", t=4), in0=w1_planes[q][:].rearrange("p t n -> p n t"), scalar1=1.0, scalar2=0.0, op0=ALU.mult, op1=ALU.add)
 
         def w1_quantise(q):
             cols = slice(256 * q, 256 * q + 256)
@@ -146,27 +148,25 @@ def tile_graph_gan_pa_kernel(tc, x, fe_w0, fe_b0, fe_w1_bytes, fe_w1_scale, fe_b
         pair_sums = {}
         e1_mx = {}
         e1_tiles = [keep.tile([P, 5 * PAIRS], BF16, name="e1_tile%d" % j, align_bytes=64) for j in range(2)]
-        half = ROWS // 2
 
-        def pair_operands(k, i0, i1, v):
+        def pair_add(engine, v, k, i0, i1, z):
             graph = k // 2
             n0 = 32 * graph + ROWS * (k % 2)
             shape = [P, i1 - i0, 32, 4]
             u_rows = u_sb[:, n0 + i0 : n0 + i1, :].unsqueeze(2).to_broadcast(shape)
-            return u_rows, v[:, 32 * graph : 32 * graph + 32, :].unsqueeze(1).to_broadcast(shape)
+            v_rows = v[:, 32 * graph : 32 * graph + 32, :].unsqueeze(1).to_broadcast(shape)
+            engine.tensor_tensor(out=z.rearrange("p (i j t) -> p i j t", j=32, t=4), in0=u_rows, in1=v_rows, op=ALU.add)
 
         def e1_add(k, i0, i1):
-            z = work.tile([P, i1 - i0, 32, 4], F32, name="pair_sums")
-            in0, in1 = pair_operands(k, i0, i1, v_psum)
-            nc.vector.tensor_tensor(out=z[:], in0=in0, in1=in1, op=ALU.add)
-            pair_sums[k, i0] = z[:].rearrange("p i j t -> p (i j t)")
+            z = work.tile([P, 128 * (i1 - i0)], F32, name="pair_sums")
+            pair_add(nc.vector, v_psum, k, i0, i1, z[:])
+            pair_sums[k, i0] = z[:]
 
         def e1_add_gpsimd(k, i0, i1):
             home = e1_tiles[(k - 1) % 2]
             end = home.shape[1] // 2
             z = home[:].bitcast(F32)[:, end - 128 * (i1 - i0) : end]
-            in0, in1 = pair_operands(k, i0, i1, v_sb)
-            nc.gpsimd.tensor_tensor(out=z.rearrange("p (i j t) -> p i j t", j=32, t=4), in0=in0, in1=in1, op=ALU.add)
+            pair_add(nc.gpsimd, v_sb, k, i0, i1, z)
             pair_sums[k, i0] = z
 
         def e1_lrelu(k, i0, i1):
@@ -196,12 +196,11 @@ def tile_graph_gan_pa_kernel(tc, x, fe_w0, fe_b0, fe_w1_bytes, fe_w1_scale, fe_b
             dst = rows[PAIRS * k + 128 * s0 : PAIRS * k + 128 * s1, n0:n1]
             nc.sync.dma_start(out=dst.rearrange("(s p) c -> p s c", p=P), in_=out_rows(k)[:, s0:s1, n0:n1])
 
-        def tile_products(group, c0, c1):
-            k, s0, s1 = group[0], group[3], group[4]
+        def tile_products(k, c0, c1, s0, s1):
             acc = psum.tile([P, c1 - c0, 128 * (s1 - s0)], F32, name="tile_psum", tag="product")
             for c in range(c0, c1):
                 product(acc[:, c - c0, :], w1_mx, slice(128 * c, 128 * c + 128), e1_mx[k], slice(128 * s0, 128 * s1))
-                tile_psum[group, c] = acc[:, c - c0, :]
+                tile_psum[k, c, s0] = acc[:, c - c0, :]
 
         def part_products(part):
             k, s0, s1, n0, n1 = part
@@ -210,29 +209,36 @@ def tile_graph_gan_pa_kernel(tc, x, fe_w0, fe_b0, fe_w1_bytes, fe_w1_scale, fe_b
                 product(acc[:, s - s0, :], e1_mx[k], slice(128 * s, 128 * s + 128), w1_mx, slice(n0, n1))
             part_psum[part] = acc
 
-        def affine(group, c0, c1):
-            w = 128 * (group[4] - group[3])
+        def affine(group, c0, c1, s0, s1):
+            k, first_tile, end_tile, first_strip, end_strip = group
             if group not in a_sb:
-                a_sb[group] = work.tile([P, (group[2] - group[1]) * w], F32, name="a_sb", bufs=3)
-                r_sb[group] = work.tile([P, (group[2] - group[1]) * w], F32, name="r_sb", bufs=3)
+                shape = [P, end_tile - first_tile, 128 * (end_strip - first_strip)]
+                a_sb[group] = work.tile(shape, F32, name="a_sb", bufs=3)
+                r_sb[group] = work.tile(shape, F32, name="r_sb", bufs=3)
+            cols = slice(128 * (s0 - first_strip), 128 * (s1 - first_strip))
             for c in range(c0, c1):
-                i = c - group[1]
-                nc.scalar.activation(out=a_sb[group][:, w * i : w * i + w], in_=tile_psum[group, c], func=ACT.Identity, bias=b1_fifth[:, c : c + 1], scale=ALPHA)
+                nc.scalar.activation(out=a_sb[group][:, c - first_tile, cols], in_=tile_psum[k, c, s0], func=ACT.Identity, bias=b1_fifth[:, c : c + 1], scale=ALPHA)
+
+        def flat(tile, start, end):
+            return tile[:].rearrange("p c n -> p (c n)")[:, start:end]
 
         def relu_vector(group, start, end):
-            nc.vector.tensor_scalar(out=r_sb[group][:, start:end], in0=a_sb[group][:, start:end], scalar1=4.0, scalar2=0.0, op0=ALU.mult, op1=ALU.max)
+            nc.vector.tensor_scalar(out=flat(r_sb[group], start, end), in0=flat(a_sb[group], start, end), scalar1=4.0, scalar2=0.0, op0=ALU.mult, op1=ALU.max)
 
         def relu_scalar(group, start, end):
-            nc.scalar.activation(out=r_sb[group][:, start:end], in_=a_sb[group][:, start:end], func=ACT.Relu, scale=4.0)
+            nc.scalar.activation(out=flat(r_sb[group], start, end), in_=flat(a_sb[group], start, end), func=ACT.Relu, scale=4.0)
+
+        def relu_scalar_strips(group, c0, c1, s0, s1):
+            tiles, cols = slice(c0 - group[1], c1 - group[1]), slice(128 * s0, 128 * s1)
+            nc.scalar.activation(out=r_sb[group][:, tiles, cols], in_=a_sb[group][:, tiles, cols], func=ACT.Relu, scale=4.0)
 
         def turn(group, c0, c1, s0, s1, tag="turned"):
-            w = 128 * (group[4] - group[3])
             acc = psum.tile([P, s1 - s0, c1 - c0, P], F32, name="turned", tag=tag, bufs=3 if tag == "turned" else 1)
             for s in range(s0, s1):
+                cols = slice(128 * (s - group[3]), 128 * (s - group[3]) + 128)
                 for c in range(c0, c1):
-                    n0 = w * (c - group[1]) + 128 * (s - group[3])
                     for m, src in enumerate((a_sb[group], r_sb[group])):
-                        nc.tensor.matmul(acc[:, s - s0, c - c0, :], lhsT=src[:, n0 : n0 + 128], rhs=ident[:], is_transpose=True, start=(m == 0), stop=(m == 1))
+                        nc.tensor.matmul(acc[:, s - s0, c - c0, :], lhsT=src[:, c - group[1], cols], rhs=ident[:], is_transpose=True, start=(m == 0), stop=(m == 1))
             turned[group[0], c0, s0] = (acc, c1, s1)
 
         def leave(k, c0, s0):
@@ -252,99 +258,122 @@ def tile_graph_gan_pa_kernel(tc, x, fe_w0, fe_b0, fe_w1_bytes, fe_w1_scale, fe_b
             nc.vector.scalar_tensor_tensor(out=out_rows(k)[:, s0:s1, n0:n1], in0=z, scalar=ALPHA, in1=z, op0=ALU.mult, op1=ALU.max)
 
         def first(k):
-            return (k, 0, 3, 0, 4)
+            return (k, 3, 6, 0, 4)
 
         def second(k):
             return (k, 6, 8, 0, 4)
 
         def own_rows(k):
-            return {1: 8, CHUNKS - 1: half}.get(k, OWN_ROWS)
+            return {1: OWN_ROWS_CHUNK_1, CHUNKS - 1: HALF}.get(k, OWN_ROWS)
 
         def parts(k):
-            return [(k, 0, 2, 512, 768), (k, 2, 4, 512, 768), (k, 0, 4, 384, 512)]
+            return [(k, 0, 2, 0, 256), (k, 2, 4, 0, 256), (k, 0, 4, 256, 384)]
 
+        opening = (0, 2, 6, 0, 4)
+        x_part, y_part = parts(0)[0:2]
+        w1_widen(1)
+        w1_lay_gpsimd(1)
+        e1_add(0, 0, HALF)
         w1_widen(2)
         w1_lay_gpsimd(2)
-        e1_add(0, 0, half)
+        e1_add(0, HALF, ROWS)
         w1_widen(0)
-        e1_add(0, half, ROWS)
-        w1_widen(1)
-        w1_lay_scalar(0)
-        e1_lrelu(0, 0, half)
-        w1_quantise(2)
-        e1_quantise(0, 0, half)
-        part_products(parts(0)[0])
-        w1_lay_scalar(1)
-        e1_lrelu(0, half, ROWS)
+        w1_widen(3)
+        w1_lay(0)
+        e1_lrelu(0, 0, HALF)
+        w1_quantise(1)
+        e1_quantise(0, 0, HALF)
+        tile_products(0, 2, 4, 0, 2)
         nc.scalar.copy(out=v_sb[:], in_=v_psum)
         nc.scalar.activation(out=b1_fifth[:], in_=b1_turned[:, 0:8], func=ACT.Copy, scale=ALPHA)
+        w1_lay(3)
+        w1_quantise(2)
+        tile_products(0, 4, 6, 0, 2)
+        e1_lrelu(0, HALF, ROWS)
         w1_quantise(0)
-        w1_widen(3)
-        w1_lay_scalar(3)
+        e1_quantise(0, HALF, ROWS)
+        e1_add_gpsimd(1, own_rows(1), ROWS)
+        affine(opening, 2, 6, 0, 2)
+        tile_products(0, 2, 4, 2, 4)
+        tile_products(0, 4, 6, 2, 4)
+        part_products(x_part)
+        part_products(y_part)
+        relu_scalar_strips(opening, 2, 4, 0, 2)
+        relu_scalar_strips(opening, 4, 6, 0, 2)
+        affine(opening, 2, 6, 2, 4)
+        turn(opening, 2, 4, 0, 2)
+        turn(opening, 4, 6, 0, 2)
+        e1_add(1, 0, own_rows(1))
+        part_add(x_part)
+        part_add(y_part)
+        w1_quantise(3)
+        relu_scalar_strips(opening, 2, 4, 2, 4)
+        relu_scalar_strips(opening, 4, 6, 2, 4)
+        tile_products(0, 6, 7, 0, 4)
+        turn(opening, 2, 4, 2, 4)
+        tile_products(0, 7, 8, 0, 4)
+        leave(0, 2, 0)
+        leave(0, 4, 0)
+        store(0, 0, 2, 256, 768)
+        turn(opening, 4, 6, 2, 4)
+        part_lrelu(x_part)
+        e1_lrelu(1, 0, own_rows(1))
+        e1_lrelu(1, own_rows(1), ROWS)
 
-        for k in range(CHUNKS - 1):
+        for k in range(1, CHUNKS - 1):
             x_part, y_part, z_part = parts(k)
             own = own_rows(k + 1)
-            if k > 0:
-                affine(second(k - 1), 6, 8)
-                e1_quantise(k, half, ROWS)
-                e1_quantise(k, 0, half)
-                e1_add_gpsimd(k + 1, own, ROWS)
+            split = 1536 - SCALAR_RELU
+            affine(second(k - 1), 6, 8, 0, 4)
+            for i0 in (HALF, 0) if own_rows(k) <= HALF else (0, HALF):
+                e1_quantise(k, i0, i0 + HALF)
+            e1_add_gpsimd(k + 1, own, ROWS)
+            if k > 1:
                 part_lrelu(parts(k - 1)[2])
-                turn(first(k - 1), 0, 1, 0, 4)
-                turn(first(k - 1), 1, 3, 0, 2)
-                turn(first(k - 1), 1, 3, 2, 4)
-                part_products(x_part)
-                part_products(y_part)
-                part_products(z_part)
-                tile_products(first(k), 0, 1)
+                turn(first(k - 1), 3, 4, 0, 4)
+                turn(first(k - 1), 4, 6, 0, 2)
+                turn(first(k - 1), 4, 6, 2, 4)
             else:
-                e1_quantise(k, half, ROWS)
-                e1_add_gpsimd(k + 1, own, ROWS)
-                w1_quantise(1)
-                part_products(y_part)
-                tile_products(first(k), 0, 1)
-                part_products(z_part)
+                part_lrelu(parts(0)[1])
+                store(0, 0, 4, 0, 256)
+            part_products(x_part)
+            part_products(y_part)
+            part_products(z_part)
+            tile_products(k, 3, 4, 0, 4)
             e1_add(k + 1, 0, own)
-            if k > 0:
-                leave(k - 1, 0, 0)
+            if k > 1:
+                leave(k - 1, 3, 0)
                 relu_scalar(second(k - 1), 0, 1024)
-                leave(k - 1, 1, 0)
-                store(k - 1, 0, 2, 0, 512)
-                leave(k - 1, 1, 2)
-                store(k - 1, 2, 4, 0, 512)
-            affine(first(k), 0, 1)
+                leave(k - 1, 4, 0)
+                store(k - 1, 0, 2, 256, 768)
+            else:
+                leave(0, 2, 2)
+                relu_scalar(second(0), 0, 1024)
+            leave(k - 1, 4, 2)
+            store(k - 1, 2, 4, 256, 768)
+            affine(first(k), 3, 4, 0, 4)
             part_add(x_part)
-            tile_products(first(k), 1, 2)
+            tile_products(k, 4, 5, 0, 4)
             part_add(y_part)
-            tile_products(first(k), 2, 3)
+            tile_products(k, 5, 6, 0, 4)
             part_add(z_part)
-            affine(first(k), 1, 3)
+            affine(first(k), 4, 6, 0, 4)
             part_lrelu(x_part)
             part_lrelu(y_part)
-            store(k, 0, 4, 512, 768)
-            if k > 0:
-                turn(second(k - 1), 6, 8, 0, 2)
-                turn(second(k - 1), 6, 8, 2, 4)
-            else:
-                w1_quantise(3)
-            tile_products(second(k), 6, 7)
-            tile_products(second(k), 7, 8)
-            split = 1536 - SCALAR_RELU
-            if k > 0:
-                relu_vector(first(k), 0, split)
+            store(k, 0, 4, 0, 256)
+            turn(second(k - 1), 6, 8, 0, 2)
+            turn(second(k - 1), 6, 8, 2, 4)
+            tile_products(k, 6, 7, 0, 4)
+            tile_products(k, 7, 8, 0, 4)
+            relu_vector(first(k), 0, split)
             if k < CHUNKS - 2:
                 e1_lrelu(k + 1, own, ROWS)
             else:
-                e1_lrelu(k + 1, 0, half)
-            if k > 0:
-                leave(k - 1, 6, 0)
-                relu_scalar(first(k), split, 1536)
-                leave(k - 1, 6, 2)
-                store(k - 1, 0, 4, 768, 1024)
-            else:
-                relu_scalar(first(k), 0, 768)
-                relu_scalar(first(k), 768, 1536)
+                e1_lrelu(k + 1, 0, HALF)
+            leave(k - 1, 6, 0)
+            relu_scalar(first(k), split, 1536)
+            leave(k - 1, 6, 2)
+            store(k - 1, 0, 4, 768, 1024)
             if k < CHUNKS - 2:
                 e1_lrelu(k + 1, 0, own)
 
@@ -352,36 +381,36 @@ def tile_graph_gan_pa_kernel(tc, x, fe_w0, fe_b0, fe_w1_bytes, fe_w1_scale, fe_b
         early, late = (k, 0, 4, 0, 2), (k, 0, 2, 2, 4)
         ends = [(k, 0, 1, 512, 1024), (k, 1, 2, 512, 1024), (k, 2, 4, 256, 512), (k, 2, 3, 512, 1024), (k, 3, 4, 512, 1024)]
         part_lrelu(parts(k - 1)[2])
-        e1_quantise(k, 0, half)
-        turn(first(k - 1), 0, 1, 0, 4)
-        affine(second(k - 1), 6, 8)
-        turn(first(k - 1), 1, 3, 0, 2)
-        turn(first(k - 1), 1, 3, 2, 4, "v")
-        tile_products(early, 0, 2)
-        tile_products(early, 2, 4)
+        e1_quantise(k, 0, HALF)
+        turn(first(k - 1), 3, 4, 0, 4)
+        affine(second(k - 1), 6, 8, 0, 4)
+        turn(first(k - 1), 4, 6, 0, 2)
+        turn(first(k - 1), 4, 6, 2, 4, "v")
+        tile_products(k, 0, 2, 0, 2)
+        tile_products(k, 2, 4, 0, 2)
         part_products(ends[0])
         part_products(ends[1])
-        e1_lrelu(k, half, ROWS)
-        leave(k - 1, 0, 0)
-        leave(k - 1, 1, 0)
-        store(k - 1, 0, 2, 0, 512)
-        leave(k - 1, 1, 2)
-        store(k - 1, 2, 4, 0, 512)
+        e1_lrelu(k, HALF, ROWS)
+        leave(k - 1, 3, 0)
+        leave(k - 1, 4, 0)
+        store(k - 1, 0, 2, 256, 768)
+        leave(k - 1, 4, 2)
+        store(k - 1, 2, 4, 256, 768)
         relu_vector(second(k - 1), 0, 1024)
-        e1_quantise(k, half, ROWS)
+        e1_quantise(k, HALF, ROWS)
         part_add(ends[0])
         part_add(ends[1])
-        affine(early, 0, 4)
+        affine(early, 0, 4, 0, 2)
         turn(second(k - 1), 6, 8, 0, 2)
         turn(second(k - 1), 6, 8, 2, 4)
-        tile_products(late, 0, 2)
+        tile_products(k, 0, 2, 2, 4)
         part_products(ends[2])
         part_lrelu(ends[0])
         store(k, 0, 1, 512, 1024)
         part_products(ends[3])
         part_products(ends[4])
         leave(k - 1, 6, 0)
-        affine(late, 0, 2)
+        affine(late, 0, 2, 2, 4)
         relu_vector(early, 0, 1024)
         leave(k - 1, 6, 2)
         store(k - 1, 0, 4, 768, 1024)

@@ -21,7 +21,7 @@ ROWS = 16
 HALF = ROWS // 2
 OWN_ROWS = 7
 OWN_ROWS_CHUNK_1 = 10
-SCALAR_RELU = 768
+SCALAR_RELU = 832
 OUT_BUFFERS = 5
 
 
@@ -232,6 +232,10 @@ def tile_graph_gan_pa_kernel(tc, x, fe_w0, fe_b0, fe_w1_bytes, fe_w1_scale, fe_b
             tiles, cols = slice(c0 - group[1], c1 - group[1]), slice(128 * s0, 128 * s1)
             nc.scalar.activation(out=r_sb[group][:, tiles, cols], in_=a_sb[group][:, tiles, cols], func=ACT.Relu, scale=4.0)
 
+        def relu_vector_strips(group, s0, s1):
+            cols = slice(128 * s0, 128 * s1)
+            nc.vector.tensor_scalar(out=r_sb[group][:, :, cols], in0=a_sb[group][:, :, cols], scalar1=4.0, scalar2=0.0, op0=ALU.mult, op1=ALU.max)
+
         def turn(group, c0, c1, s0, s1, tag="turned"):
             acc = psum.tile([P, s1 - s0, c1 - c0, P], F32, name="turned", tag=tag, bufs=3 if tag == "turned" else 1)
             for s in range(s0, s1):
@@ -294,10 +298,10 @@ def tile_graph_gan_pa_kernel(tc, x, fe_w0, fe_b0, fe_w1_bytes, fe_w1_scale, fe_b
         e1_quantise(0, HALF, ROWS)
         e1_add_gpsimd(1, own_rows(1), ROWS)
         affine(opening, 2, 6, 0, 2)
-        tile_products(0, 2, 4, 2, 4)
-        tile_products(0, 4, 6, 2, 4)
         part_products(x_part)
+        tile_products(0, 2, 4, 2, 4)
         part_products(y_part)
+        tile_products(0, 4, 6, 2, 4)
         relu_scalar_strips(opening, 2, 4, 0, 2)
         relu_scalar_strips(opening, 4, 6, 0, 2)
         affine(opening, 2, 6, 2, 4)
@@ -330,7 +334,6 @@ def tile_graph_gan_pa_kernel(tc, x, fe_w0, fe_b0, fe_w1_bytes, fe_w1_scale, fe_b
             e1_add_gpsimd(k + 1, own, ROWS)
             if k > 1:
                 part_lrelu(parts(k - 1)[2])
-                turn(first(k - 1), 3, 4, 0, 4)
                 turn(first(k - 1), 4, 6, 0, 2)
                 turn(first(k - 1), 4, 6, 2, 4)
             else:
@@ -343,14 +346,13 @@ def tile_graph_gan_pa_kernel(tc, x, fe_w0, fe_b0, fe_w1_bytes, fe_w1_scale, fe_b
             e1_add(k + 1, 0, own)
             if k > 1:
                 leave(k - 1, 3, 0)
-                relu_scalar(second(k - 1), 0, 1024)
                 leave(k - 1, 4, 0)
                 store(k - 1, 0, 2, 256, 768)
             else:
                 leave(0, 2, 2)
-                relu_scalar(second(0), 0, 1024)
             leave(k - 1, 4, 2)
             store(k - 1, 2, 4, 256, 768)
+            relu_scalar(second(k - 1), 0, 1024)
             affine(first(k), 3, 4, 0, 4)
             part_add(x_part)
             tile_products(k, 4, 5, 0, 4)
@@ -359,69 +361,86 @@ def tile_graph_gan_pa_kernel(tc, x, fe_w0, fe_b0, fe_w1_bytes, fe_w1_scale, fe_b
             part_add(z_part)
             affine(first(k), 4, 6, 0, 4)
             part_lrelu(x_part)
-            part_lrelu(y_part)
-            store(k, 0, 4, 0, 256)
+            if k < CHUNKS - 2:
+                part_lrelu(y_part)
+                store(k, 0, 4, 0, 256)
+            else:
+                store(k, 0, 2, 0, 256)
             turn(second(k - 1), 6, 8, 0, 2)
             turn(second(k - 1), 6, 8, 2, 4)
             tile_products(k, 6, 7, 0, 4)
-            tile_products(k, 7, 8, 0, 4)
-            relu_vector(first(k), 0, split)
             if k < CHUNKS - 2:
+                relu_vector(first(k), 0, split)
+                turn(first(k), 3, 4, 0, 4)
+                tile_products(k, 7, 8, 0, 4)
                 e1_lrelu(k + 1, own, ROWS)
-            else:
-                e1_lrelu(k + 1, 0, HALF)
-            leave(k - 1, 6, 0)
-            relu_scalar(first(k), split, 1536)
-            leave(k - 1, 6, 2)
-            store(k - 1, 0, 4, 768, 1024)
-            if k < CHUNKS - 2:
+                leave(k - 1, 6, 0)
+                relu_scalar(first(k), split, 1536)
+                leave(k - 1, 6, 2)
+                store(k - 1, 0, 4, 768, 1024)
                 e1_lrelu(k + 1, 0, own)
+            else:
+                tile_products(k, 7, 8, 0, 4)
+                e1_lrelu(k + 1, 0, HALF)
+                relu_vector_strips(first(k), 0, 2)
+                turn(first(k), 3, 6, 0, 1)
+                leave(k - 1, 6, 0)
+                store(k - 1, 0, 2, 768, 1024)
+                relu_scalar_strips(first(k), 3, 6, 2, 4)
+                part_lrelu(y_part)
+                store(k, 2, 4, 0, 256)
+                leave(k - 1, 6, 2)
+                store(k - 1, 2, 4, 768, 1024)
 
         k = CHUNKS - 1
         early, late = (k, 0, 4, 0, 2), (k, 0, 2, 2, 4)
         ends = [(k, 0, 1, 512, 1024), (k, 1, 2, 512, 1024), (k, 2, 4, 256, 512), (k, 2, 3, 512, 1024), (k, 3, 4, 512, 1024)]
-        part_lrelu(parts(k - 1)[2])
         e1_quantise(k, 0, HALF)
-        turn(first(k - 1), 3, 4, 0, 4)
-        affine(second(k - 1), 6, 8, 0, 4)
-        turn(first(k - 1), 4, 6, 0, 2)
-        turn(first(k - 1), 4, 6, 2, 4, "v")
-        tile_products(k, 0, 2, 0, 2)
-        tile_products(k, 2, 4, 0, 2)
+        part_lrelu(parts(k - 1)[2])
+        turn(first(k - 1), 3, 6, 1, 2, "v")
+        turn(first(k - 1), 3, 6, 2, 3)
         part_products(ends[0])
         part_products(ends[1])
-        e1_lrelu(k, HALF, ROWS)
+        turn(first(k - 1), 3, 6, 3, 4)
         leave(k - 1, 3, 0)
-        leave(k - 1, 4, 0)
-        store(k - 1, 0, 2, 256, 768)
-        leave(k - 1, 4, 2)
-        store(k - 1, 2, 4, 256, 768)
-        relu_vector(second(k - 1), 0, 1024)
-        e1_quantise(k, HALF, ROWS)
+        store(k - 1, 0, 1, 256, 768)
+        affine(second(k - 1), 6, 8, 0, 4)
+        leave(k - 1, 3, 1)
+        store(k - 1, 1, 2, 256, 768)
+        tile_products(k, 0, 2, 0, 2)
+        tile_products(k, 2, 4, 0, 2)
+        e1_lrelu(k, HALF, ROWS)
+        leave(k - 1, 3, 2)
+        store(k - 1, 2, 3, 256, 768)
+        leave(k - 1, 3, 3)
+        store(k - 1, 3, 4, 256, 768)
         part_add(ends[0])
+        relu_vector(second(k - 1), 0, 1024)
         part_add(ends[1])
+        part_lrelu(ends[0])
+        store(k, 0, 1, 512, 1024)
+        e1_quantise(k, HALF, ROWS)
+        part_lrelu(ends[1])
+        store(k, 1, 2, 512, 1024)
         affine(early, 0, 4, 0, 2)
         turn(second(k - 1), 6, 8, 0, 2)
         turn(second(k - 1), 6, 8, 2, 4)
         tile_products(k, 0, 2, 2, 4)
         part_products(ends[2])
-        part_lrelu(ends[0])
-        store(k, 0, 1, 512, 1024)
         part_products(ends[3])
         part_products(ends[4])
         leave(k - 1, 6, 0)
-        affine(late, 0, 2, 2, 4)
+        store(k - 1, 0, 2, 768, 1024)
         relu_vector(early, 0, 1024)
         leave(k - 1, 6, 2)
-        store(k - 1, 0, 4, 768, 1024)
-        part_lrelu(ends[1])
-        store(k, 1, 2, 512, 1024)
-        relu_scalar(late, 0, 512)
+        store(k - 1, 2, 4, 768, 1024)
+        affine(late, 0, 2, 2, 4)
         turn(early, 0, 4, 0, 1)
         turn(early, 0, 4, 1, 2, "v")
-        turn(late, 0, 2, 2, 4)
         part_add(ends[2])
         part_add(ends[3])
+        relu_vector(late, 0, 512)
+        turn(late, 0, 2, 2, 4)
         part_lrelu(ends[2])
         leave(k, 0, 0)
         store(k, 0, 1, 0, 512)

from contextlib import ExitStack

import concourse.mybir as mybir
from concourse.masks import make_identity

F32 = mybir.dt.float32
BF16 = mybir.dt.bfloat16
U32 = mybir.dt.uint32
U8 = mybir.dt.uint8
FP8 = mybir.dt.float8_e4m3fn
FP8X4 = mybir.dt.float8_e4m3fn_x4
ALU = mybir.AluOpType
ACT = mybir.ActivationFunctionType

P = 128
FLOPS = 2 * 128 * 512 * 512 * 2 + 2 * 4096 * 512 * 1024
ALPHA = 0.2
CHUNKS = 8
PAIRS = 512
ROWS = 16
HALF = ROWS // 2
OWN_ROWS = 7
OWN_ROWS_CHUNK_1 = 10
SCALAR_RELU = 832
OUT_BUFFERS = 5


def tile_graph_gan_pa_kernel(tc, x, fe_w0, fe_b0, fe_w1_bytes, fe_w1_scale, fe_b1, out):
    nc = tc.nc
    rows = out.rearrange("b i j c -> (b i j) c")

    with ExitStack() as ctx:
        keep = ctx.enter_context(tc.tile_pool(name="keep", bufs=1))
        work = ctx.enter_context(tc.tile_pool(name="work", bufs=2))
        psum = ctx.enter_context(tc.psum_pool(name="psum", bufs=4))
        ctx.enter_context(tc.manual_schedule())

        x_sb = keep.tile([P, 512], BF16, name="x_sb", align_bytes=64)
        w0_raw = [keep.tile([P, 4, 512], BF16, name="w0_raw%d" % h, align_bytes=64) for h in range(2)]
        w1_bytes = [keep.tile([P, 2048], U8, name="w1_bytes%d" % g, align_bytes=64) for g in range(2)]
        w1_scale = keep.tile([P, 4], F32, name="w1_scale")
        b0_sb = keep.tile([P, 4], BF16, name="b0_sb")
        b1_rows = keep.tile([P, P], BF16, name="b1_rows")
        b1_spread = keep.tile([P, 1024], BF16, name="b1_spread")
        w0_rows = fe_w0.rearrange("(h p j) w -> h p j w", h=2, j=4)
        w1_rows = fe_w1_bytes.rearrange("(p t) n -> p (t n)", t=4)
        nc.sync.dma_start(out=x_sb[:], in_=x.rearrange("b n d -> (b n) d"))
        for h in range(2):
            nc.sync.dma_start(out=w0_raw[h][:], in_=w0_rows[h])
        nc.sync.dma_start(out=w1_scale[:], in_=fe_w1_scale.rearrange("(p t) o -> p (t o)", t=4))
        nc.sync.dma_start(out=b0_sb[:], in_=fe_b0.rearrange("(p t) -> p t", t=4))
        for g in range(2):
            nc.sync.dma_start(out=w1_bytes[g][:], in_=w1_rows[:, 2048 * g : 2048 * g + 2048])

        ident = keep.tile([P, P], F32, name="ident")
        ident_bf = keep.tile([P, P], BF16, name="ident_bf")
        make_identity(nc, ident[:])
        nc.vector.memset(b1_rows[:], 0.0)
        nc.sync.dma_start(out=b1_rows[0:8, :], in_=fe_b1.rearrange("(c m) -> c m", m=P))
        nc.sync.dma_start(out=b1_spread[:], in_=fe_b1.partition_broadcast(P))
        nc.scalar.activation(out=ident_bf[:], in_=ident[:], func=ACT.Copy)

        def quantise(codes, scales, values):
            nc.vector.quantize_mx(out=codes.bitcast(FP8X4), scales=scales, in_=values)

        def product(acc, lhs, lhs_cols, rhs, rhs_cols):
            nc.tensor.matmul_mx(
                out=acc,
                lhsT=lhs[0][:, lhs_cols].bitcast(FP8X4),
                lhsT_scale=lhs[1][:, lhs_cols],
                rhs=rhs[0][:, rhs_cols].bitcast(FP8X4),
                rhs_scale=rhs[1][:, rhs_cols],
                start=True,
                stop=True,
            )

        def mx_operand(pool, name, width, bufs):
            codes = pool.tile([P, width], U32, name=name + "_codes", bufs=bufs, align_bytes=64)
            scales = pool.tile([P, width], U8, name=name + "_scales", bufs=bufs, align_bytes=64)
            return codes, scales

        x_words = x_sb[:].bitcast(F32)
        x_turned = psum.tile([P, 2, P], F32, name="x_turned", tag="turned", bufs=3)
        for u in range(2):
            nc.tensor.transpose(x_turned[:, u, :], x_words[:, u:256:2], ident[:])
        x_laid = keep.tile([P, 4 * P], BF16, name="x_laid", align_bytes=64)
        x_mx = mx_operand(keep, "x", P, 1)
        w0_laid = [keep.tile([P, 2048], BF16, name="w0_laid%d" % h, align_bytes=64) for h in range(2)]
        w0_mx = [mx_operand(keep, "w0_%d" % h, 512, 1) for h in range(2)]

        def w0_lay(h, t0, t1, copy):
            dst = w0_laid[h][:].rearrange("p (t c i j) -> p c t i j", t=4, i=2, j=4)
            src = w0_raw[h][:].rearrange("p j (c i t) -> p c t i j", i=2, t=4)
            copy(out=dst[:, :, t0:t1], in_=src[:, :, t0:t1])

        def w0_quantise(h, g):
            cols = slice(256 * g, 256 * g + 256)
            quantise(w0_mx[h][0][:, cols], w0_mx[h][1][:, cols], w0_laid[h][:, 1024 * g : 1024 * g + 1024])

        def first_layer(h, acc, g):
            for t in range(2 * g, 2 * g + 2):
                product(acc[:, t, :], w0_mx[h], slice(128 * t, 128 * t + 128), x_mx, slice(0, P))

        u_acc = psum.tile([P, 4, P], F32, name="first_u", tag="turned", bufs=3)
        v_acc = psum.tile([P, 4, P], F32, name="first_v", tag="v", bufs=1)
        nc.vector.tensor_copy(out=x_laid[:].bitcast(F32).rearrange("p (n u) -> p n u", u=2), in_=x_turned[:].rearrange("p u n -> p n u"))
        w0_lay(0, 2, 4, nc.scalar.copy)
        w0_lay(1, 3, 4, nc.scalar.copy)
        w0_lay(0, 0, 2, nc.vector.tensor_copy)
        quantise(x_mx[0][:], x_mx[1][:], x_laid[:])
        w0_quantise(0, 0)
        w0_lay(1, 0, 2, nc.vector.tensor_copy)
        w0_quantise(0, 1)
        w0_lay(1, 2, 3, nc.vector.tensor_copy)
        for g in range(2):
            first_layer(0, u_acc, g)
        for g in range(2):
            w0_quantise(1, g)
            first_layer(1, v_acc, g)
        u_psum = u_acc[:].rearrange("p t n -> p n t")
        v_psum = v_acc[:].rearrange("p t n -> p n t")
        u_sb = keep.tile([P, P, 4], F32, name="u_sb")
        v_sb = keep.tile([P, P, 4], F32, name="v_sb")
        nc.vector.tensor_tensor(out=u_sb[:], in0=u_psum, in1=b0_sb[:].unsqueeze(1).to_broadcast([P, P, 4]), op=ALU.add)
        b1_turned = psum.tile([P, P], BF16, name="b1_turned", tag="turned", bufs=3)
        nc.tensor.transpose(b1_turned[:], b1_rows[:], ident_bf[:])
        b1_fifth = keep.tile([P, 8], F32, name="b1_fifth")

        w1_planes = [keep.tile([P, 4, 256], BF16, name="w1_planes%d" % q, align_bytes=64) for q in range(4)]
        w1_homes = [w0_laid[0][:, 0:1024], w0_laid[1][:, 1024:2048], w0_laid[1][:, 0:1024], w0_laid[0][:, 1024:2048]]
        w1_mx = mx_operand(keep, "w1", 1024, 1)

        def w1_widen(q, t0=0, t1=4):
            for t in range(t0, t1):
                n0 = 1024 * (t % 2) + 256 * q
                nc.scalar.activation(out=w1_planes[q][:, t, :], in_=w1_bytes[t // 2][:, n0 : n0 + 256].bitcast(FP8), func=ACT.Copy, scale=w1_scale[:, t : t + 1])

        def w1_lay(q):
            nc.scalar.copy(out=w1_homes[q].rearrange("p (c i t) -> p c t i", i=4, t=4), in_=w1_planes[q][:].rearrange("p t (c i) -> p c t i", i=4))

        def w1_lay_gpsimd(q):
            nc.gpsimd.tensor_scalar(out=w1_homes[q].rearrange("p (n t) -> p n t", t=4), in0=w1_planes[q][:].rearrange("p t n -> p n t"), scalar1=1.0, scalar2=0.0, op0=ALU.mult, op1=ALU.add)

        def w1_quantise(q):
            cols = slice(256 * q, 256 * q + 256)
            quantise(w1_mx[0][:, cols], w1_mx[1][:, cols], w1_homes[q])

        pair_sums = {}
        e1_mx = {}
        e1_tiles = [keep.tile([P, 5 * PAIRS], BF16, name="e1_tile%d" % j, align_bytes=64) for j in range(2)]

        def pair_add(engine, v, k, i0, i1, z):
            graph = k // 2
            n0 = 32 * graph + ROWS * (k % 2)
            shape = [P, i1 - i0, 32, 4]
            u_rows = u_sb[:, n0 + i0 : n0 + i1, :].unsqueeze(2).to_broadcast(shape)
            v_rows = v[:, 32 * graph : 32 * graph + 32, :].unsqueeze(1).to_broadcast(shape)
            engine.tensor_tensor(out=z.rearrange("p (i j t) -> p i j t", j=32, t=4), in0=u_rows, in1=v_rows, op=ALU.add)

        def e1_add(k, i0, i1):
            z = work.tile([P, 128 * (i1 - i0)], F32, name="pair_sums")
            pair_add(nc.vector, v_psum, k, i0, i1, z[:])
            pair_sums[k, i0] = z[:]

        def e1_add_gpsimd(k, i0, i1):
            home = e1_tiles[(k - 1) % 2]
            end = home.shape[1] // 2
            z = home[:].bitcast(F32)[:, end - 128 * (i1 - i0) : end]
            pair_add(nc.gpsimd, v_sb, k, i0, i1, z)
            pair_sums[k, i0] = z

        def e1_lrelu(k, i0, i1):
            z = pair_sums[k, i0]
            nc.vector.scalar_tensor_tensor(out=e1_tiles[k % 2][:, 128 * i0 : 128 * i1], in0=z, scalar=ALPHA, in1=z, op0=ALU.mult, op1=ALU.max)

        def e1_quantise(k, i0, i1):
            if k not in e1_mx:
                e1_mx[k] = mx_operand(work, "e1", PAIRS, 2)
            cols = slice(32 * i0, 32 * i1)
            quantise(e1_mx[k][0][:, cols], e1_mx[k][1][:, cols], e1_tiles[k % 2][:, 128 * i0 : 128 * i1])

        tile_psum = {}
        part_psum = {}
        a_sb = {}
        r_sb = {}
        turned = {}
        part_sums = {}
        out_sb = {}

        def out_rows(k):
            if k not in out_sb:
                out_sb[k] = work.tile([P, 4, 1024], F32, name="out_sb", bufs=OUT_BUFFERS)
            return out_sb[k]

        def store(k, s0, s1, n0, n1):
            dst = rows[PAIRS * k + 128 * s0 : PAIRS * k + 128 * s1, n0:n1]
            nc.sync.dma_start(out=dst.rearrange("(s p) c -> p s c", p=P), in_=out_rows(k)[:, s0:s1, n0:n1])

        def tile_products(k, c0, c1, s0, s1):
            acc = psum.tile([P, c1 - c0, 128 * (s1 - s0)], F32, name="tile_psum", tag="product")
            for c in range(c0, c1):
                product(acc[:, c - c0, :], w1_mx, slice(128 * c, 128 * c + 128), e1_mx[k], slice(128 * s0, 128 * s1))
                tile_psum[k, c, s0] = acc[:, c - c0, :]

        def part_products(part):
            k, s0, s1, n0, n1 = part
            acc = psum.tile([P, s1 - s0, n1 - n0], F32, name="part_psum", tag="product")
            for s in range(s0, s1):
                product(acc[:, s - s0, :], e1_mx[k], slice(128 * s, 128 * s + 128), w1_mx, slice(n0, n1))
            part_psum[part] = acc

        def affine(group, c0, c1, s0, s1):
            k, first_tile, end_tile, first_strip, end_strip = group
            if group not in a_sb:
                shape = [P, end_tile - first_tile, 128 * (end_strip - first_strip)]
                a_sb[group] = work.tile(shape, F32, name="a_sb", bufs=3)
                r_sb[group] = work.tile(shape, F32, name="r_sb", bufs=3)
            cols = slice(128 * (s0 - first_strip), 128 * (s1 - first_strip))
            for c in range(c0, c1):
                nc.scalar.activation(out=a_sb[group][:, c - first_tile, cols], in_=tile_psum[k, c, s0], func=ACT.Identity, bias=b1_fifth[:, c : c + 1], scale=ALPHA)

        def flat(tile, start, end):
            return tile[:].rearrange("p c n -> p (c n)")[:, start:end]

        def relu_vector(group, start, end):
            nc.vector.tensor_scalar(out=flat(r_sb[group], start, end), in0=flat(a_sb[group], start, end), scalar1=4.0, scalar2=0.0, op0=ALU.mult, op1=ALU.max)

        def relu_scalar(group, start, end):
            nc.scalar.activation(out=flat(r_sb[group], start, end), in_=flat(a_sb[group], start, end), func=ACT.Relu, scale=4.0)

        def relu_scalar_strips(group, c0, c1, s0, s1):
            tiles, cols = slice(c0 - group[1], c1 - group[1]), slice(128 * s0, 128 * s1)
            nc.scalar.activation(out=r_sb[group][:, tiles, cols], in_=a_sb[group][:, tiles, cols], func=ACT.Relu, scale=4.0)

        def relu_vector_strips(group, s0, s1):
            cols = slice(128 * s0, 128 * s1)
            nc.vector.tensor_scalar(out=r_sb[group][:, :, cols], in0=a_sb[group][:, :, cols], scalar1=4.0, scalar2=0.0, op0=ALU.mult, op1=ALU.max)

        def turn(group, c0, c1, s0, s1, tag="turned"):
            acc = psum.tile([P, s1 - s0, c1 - c0, P], F32, name="turned", tag=tag, bufs=3 if tag == "turned" else 1)
            for s in range(s0, s1):
                cols = slice(128 * (s - group[3]), 128 * (s - group[3]) + 128)
                for c in range(c0, c1):
                    for m, src in enumerate((a_sb[group], r_sb[group])):
                        nc.tensor.matmul(acc[:, s - s0, c - c0, :], lhsT=src[:, c - group[1], cols], rhs=ident[:], is_transpose=True, start=(m == 0), stop=(m == 1))
            turned[group[0], c0, s0] = (acc, c1, s1)

        def leave(k, c0, s0):
            acc, c1, s1 = turned[k, c0, s0]
            nc.scalar.copy(out=out_rows(k)[:, s0:s1, 128 * c0 : 128 * c1], in_=acc[:].rearrange("p s c m -> p s (c m)"))

        def part_add(part):
            k, s0, s1, n0, n1 = part
            shape = [P, s1 - s0, n1 - n0]
            z = work.tile(shape, F32, name="part_sums", bufs=4)
            nc.vector.tensor_tensor(out=z[:], in0=part_psum[part][:], in1=b1_spread[:, n0:n1].unsqueeze(1).to_broadcast(shape), op=ALU.add)
            part_sums[part] = z

        def part_lrelu(part):
            k, s0, s1, n0, n1 = part
            z = part_sums[part][:]
            nc.vector.scalar_tensor_tensor(out=out_rows(k)[:, s0:s1, n0:n1], in0=z, scalar=ALPHA, in1=z, op0=ALU.mult, op1=ALU.max)

        def first(k):
            return (k, 3, 6, 0, 4)

        def second(k):
            return (k, 6, 8, 0, 4)

        def own_rows(k):
            return {1: OWN_ROWS_CHUNK_1, CHUNKS - 1: HALF}.get(k, OWN_ROWS)

        def parts(k):
            return [(k, 0, 2, 0, 256), (k, 2, 4, 0, 256), (k, 0, 4, 256, 384)]

        opening = (0, 2, 6, 0, 4)
        x_part, y_part = parts(0)[0:2]
        w1_widen(1)
        w1_lay_gpsimd(1)
        e1_add(0, 0, HALF)
        w1_widen(2)
        w1_lay_gpsimd(2)
        e1_add(0, HALF, ROWS)
        w1_widen(0)
        w1_widen(3)
        w1_lay(0)
        e1_lrelu(0, 0, HALF)
        w1_quantise(1)
        e1_quantise(0, 0, HALF)
        tile_products(0, 2, 4, 0, 2)
        nc.scalar.copy(out=v_sb[:], in_=v_psum)
        nc.scalar.activation(out=b1_fifth[:], in_=b1_turned[:, 0:8], func=ACT.Copy, scale=ALPHA)
        w1_lay(3)
        w1_quantise(2)
        tile_products(0, 4, 6, 0, 2)
        e1_lrelu(0, HALF, ROWS)
        w1_quantise(0)
        e1_quantise(0, HALF, ROWS)
        e1_add_gpsimd(1, own_rows(1), ROWS)
        affine(opening, 2, 6, 0, 2)
        part_products(x_part)
        tile_products(0, 2, 4, 2, 4)
        part_products(y_part)
        tile_products(0, 4, 6, 2, 4)
        relu_scalar_strips(opening, 2, 4, 0, 2)
        relu_scalar_strips(opening, 4, 6, 0, 2)
        affine(opening, 2, 6, 2, 4)
        turn(opening, 2, 4, 0, 2)
        turn(opening, 4, 6, 0, 2)
        e1_add(1, 0, own_rows(1))
        part_add(x_part)
        part_add(y_part)
        w1_quantise(3)
        relu_scalar_strips(opening, 2, 4, 2, 4)
        relu_scalar_strips(opening, 4, 6, 2, 4)
        tile_products(0, 6, 7, 0, 4)
        turn(opening, 2, 4, 2, 4)
        tile_products(0, 7, 8, 0, 4)
        leave(0, 2, 0)
        leave(0, 4, 0)
        store(0, 0, 2, 256, 768)
        turn(opening, 4, 6, 2, 4)
        part_lrelu(x_part)
        e1_lrelu(1, 0, own_rows(1))
        e1_lrelu(1, own_rows(1), ROWS)

        for k in range(1, CHUNKS - 1):
            x_part, y_part, z_part = parts(k)
            own = own_rows(k + 1)
            split = 1536 - SCALAR_RELU
            affine(second(k - 1), 6, 8, 0, 4)
            for i0 in (HALF, 0) if own_rows(k) <= HALF else (0, HALF):
                e1_quantise(k, i0, i0 + HALF)
            e1_add_gpsimd(k + 1, own, ROWS)
            if k > 1:
                part_lrelu(parts(k - 1)[2])
                turn(first(k - 1), 4, 6, 0, 2)
                turn(first(k - 1), 4, 6, 2, 4)
            else:
                part_lrelu(parts(0)[1])
                store(0, 0, 4, 0, 256)
            part_products(x_part)
            part_products(y_part)
            part_products(z_part)
            tile_products(k, 3, 4, 0, 4)
            e1_add(k + 1, 0, own)
            if k > 1:
                leave(k - 1, 3, 0)
                leave(k - 1, 4, 0)
                store(k - 1, 0, 2, 256, 768)
            else:
                leave(0, 2, 2)
            leave(k - 1, 4, 2)
            store(k - 1, 2, 4, 256, 768)
            relu_scalar(second(k - 1), 0, 1024)
            affine(first(k), 3, 4, 0, 4)
            part_add(x_part)
            tile_products(k, 4, 5, 0, 4)
            part_add(y_part)
            tile_products(k, 5, 6, 0, 4)
            part_add(z_part)
            affine(first(k), 4, 6, 0, 4)
            part_lrelu(x_part)
            if k < CHUNKS - 2:
                part_lrelu(y_part)
                store(k, 0, 4, 0, 256)
            else:
                store(k, 0, 2, 0, 256)
            turn(second(k - 1), 6, 8, 0, 2)
            turn(second(k - 1), 6, 8, 2, 4)
            tile_products(k, 6, 7, 0, 4)
            if k < CHUNKS - 2:
                relu_vector(first(k), 0, split)
                turn(first(k), 3, 4, 0, 4)
                tile_products(k, 7, 8, 0, 4)
                e1_lrelu(k + 1, own, ROWS)
                leave(k - 1, 6, 0)
                relu_scalar(first(k), split, 1536)
                leave(k - 1, 6, 2)
                store(k - 1, 0, 4, 768, 1024)
                e1_lrelu(k + 1, 0, own)
            else:
                tile_products(k, 7, 8, 0, 4)
                e1_lrelu(k + 1, 0, HALF)
                relu_vector_strips(first(k), 0, 2)
                turn(first(k), 3, 6, 0, 1)
                leave(k - 1, 6, 0)
                store(k - 1, 0, 2, 768, 1024)
                relu_scalar_strips(first(k), 3, 6, 2, 4)
                part_lrelu(y_part)
                store(k, 2, 4, 0, 256)
                leave(k - 1, 6, 2)
                store(k - 1, 2, 4, 768, 1024)

        k = CHUNKS - 1
        early, late = (k, 0, 4, 0, 2), (k, 0, 2, 2, 4)
        ends = [(k, 0, 1, 512, 1024), (k, 1, 2, 512, 1024), (k, 2, 4, 256, 512), (k, 2, 3, 512, 1024), (k, 3, 4, 512, 1024)]
        e1_quantise(k, 0, HALF)
        part_lrelu(parts(k - 1)[2])
        turn(first(k - 1), 3, 6, 1, 2, "v")
        turn(first(k - 1), 3, 6, 2, 3)
        part_products(ends[0])
        part_products(ends[1])
        turn(first(k - 1), 3, 6, 3, 4)
        leave(k - 1, 3, 0)
        store(k - 1, 0, 1, 256, 768)
        affine(second(k - 1), 6, 8, 0, 4)
        leave(k - 1, 3, 1)
        store(k - 1, 1, 2, 256, 768)
        tile_products(k, 0, 2, 0, 2)
        tile_products(k, 2, 4, 0, 2)
        e1_lrelu(k, HALF, ROWS)
        leave(k - 1, 3, 2)
        store(k - 1, 2, 3, 256, 768)
        leave(k - 1, 3, 3)
        store(k - 1, 3, 4, 256, 768)
        part_add(ends[0])
        relu_vector(second(k - 1), 0, 1024)
        part_add(ends[1])
        part_lrelu(ends[0])
        store(k, 0, 1, 512, 1024)
        e1_quantise(k, HALF, ROWS)
        part_lrelu(ends[1])
        store(k, 1, 2, 512, 1024)
        affine(early, 0, 4, 0, 2)
        turn(second(k - 1), 6, 8, 0, 2)
        turn(second(k - 1), 6, 8, 2, 4)
        tile_products(k, 0, 2, 2, 4)
        part_products(ends[2])
        part_products(ends[3])
        part_products(ends[4])
        leave(k - 1, 6, 0)
        store(k - 1, 0, 2, 768, 1024)
        relu_vector(early, 0, 1024)
        leave(k - 1, 6, 2)
        store(k - 1, 2, 4, 768, 1024)
        affine(late, 0, 2, 2, 4)
        turn(early, 0, 4, 0, 1)
        turn(early, 0, 4, 1, 2, "v")
        part_add(ends[2])
        part_add(ends[3])
        relu_vector(late, 0, 512)
        turn(late, 0, 2, 2, 4)
        part_lrelu(ends[2])
        leave(k, 0, 0)
        store(k, 0, 1, 0, 512)
        part_add(ends[4])
        leave(k, 0, 1)
        store(k, 1, 2, 0, 512)
        part_lrelu(ends[3])
        leave(k, 0, 2)
        store(k, 2, 3, 0, 1024)
        part_lrelu(ends[4])
        store(k, 3, 4, 0, 1024)
